import numpy as np
import ml_dtypes


def mxq(x, axis, fmt="e4m3"):
    dtype, down = {"e4m3": (ml_dtypes.float8_e4m3fn, 7), "e5m2": (ml_dtypes.float8_e5m2, 14)}[fmt]
    v = np.moveaxis(np.asarray(x, np.float32).astype(ml_dtypes.bfloat16).astype(np.float64), axis, -1)
    blocks = v.reshape(v.shape[:-1] + (-1, 32))
    amax = np.abs(blocks).max(-1, keepdims=True)
    byte = np.maximum(np.where(amax > 0, np.frexp(amax)[1] - 1 + 127, 0) - down, 1)
    scale = np.exp2(byte - 127.0)
    codes = (blocks / scale).astype(np.float32).astype(dtype).astype(np.float64)
    return np.moveaxis((codes * scale).reshape(v.shape), -1, axis)


WIDE = False


def mx_kscale(k):
    if not WIDE:
        return np.ones(k)
    levels = np.array([10, -10, 5, -5, 0])
    a = np.random.permutation(np.resize(levels, k // 512 * 4)).reshape(k // 512, 4)
    idx = np.arange(k)
    return np.exp2(a[idx // 512, idx % 128 // 32])


BF16 = ml_dtypes.bfloat16


def bf(x):
    return np.asarray(x, np.float32).astype(BF16)


def f64(x):
    return np.asarray(x).astype(np.float64)


E2M1 = np.array([0.0, 0.5, 1.0, 1.5, 2.0, 3.0, 4.0, 6.0, -0.0, -0.5, -1.0, -1.5, -2.0, -3.0, -4.0, -6.0])


def pack_weight(w, fmt):
    k, n = w.shape
    w = f64(bf(w)).reshape(k // 32, 32, n)
    amax = np.abs(w).max(1)
    if fmt == "e4m3":
        byte = np.frexp(amax)[1] - 1 + 127 - 7
    else:
        mant, ex = np.frexp(amax / 6.0)
        byte = np.where(mant > 0.5, ex, ex - 1) + 127
    byte = np.clip(np.where(amax > 0, byte, 1), 1, 254)
    scaled = (w * np.exp2(127.0 - byte)[:, None, :]).reshape(k, n).astype(np.float32)
    by_word = np.ascontiguousarray(scaled.reshape(k // 512, 128, 4, n).transpose(0, 1, 3, 2))
    if fmt == "e4m3":
        words = by_word.astype(ml_dtypes.float8_e4m3fn).view(np.uint8)
    else:
        c = by_word.astype(ml_dtypes.float4_e2m1fn).view(np.uint8) & 0xF
        words = c[..., 0::2] | (c[..., 1::2] << 4)
    return np.ascontiguousarray(words), np.ascontiguousarray(byte.astype(np.uint8).reshape(k // 512, 16, n))


def unpack_weight(words, scales, fmt):
    g, p, n, _ = words.shape
    if fmt == "e4m3":
        vals = np.ascontiguousarray(words).view(ml_dtypes.float8_e4m3fn).astype(np.float64)
    else:
        nib = np.empty((g, p, n, 4), np.uint8)
        nib[..., 0::2] = words & 0xF
        nib[..., 1::2] = words >> 4
        vals = E2M1[nib]
    vals = vals * np.repeat(np.exp2(scales.astype(np.float64) - 127.0), 8, axis=1)[..., None]
    return vals.transpose(0, 1, 3, 2).reshape(g * 512, n)

def pack4(w):
    words, scales = pack_weight(w, "e2m1")
    return words.reshape(words.shape[0], 128, -1), scales


def unpack4(words, scales):
    return unpack_weight(words.reshape(words.shape[0], 128, -1, 2), scales, "e2m1")


B, I, H = 512, 1024, 1024
FORGET_GATE_BIAS = -1.0
EPS = 1e-5


def sigmoid(v):
    return 1.0 / (1.0 + np.exp(-v))


def layer_norm_1d(x, weight, bias):
    mean = np.mean(x, axis=1, keepdims=True)
    std = np.std(x, axis=1, keepdims=True, ddof=1)
    return (x - mean) / (std + EPS) * weight + bias


def setup_inputs():
    s, t = mx_kscale(I), mx_kscale(H)
    inputs = bf(np.random.standard_normal((B, I)) * s)
    hx = bf(np.random.standard_normal((B, H)) * t)
    cx = bf(np.random.standard_normal((B, H)))
    w_i2h = np.random.standard_normal((4 * H, I)) / np.sqrt(I) / s
    w_i2h_words, w_i2h_scales = pack4(np.ascontiguousarray(w_i2h.T))
    b_i2h = bf(np.random.standard_normal(4 * H) * 0.3)
    w_h2h = np.random.standard_normal((4 * H, H)) / np.sqrt(H) / t
    w_h2h_words, w_h2h_scales = pack4(np.ascontiguousarray(w_h2h.T))
    b_h2h = bf(np.random.standard_normal(4 * H) * 0.3)
    return {
        "inputs": inputs,
        "hx": hx,
        "cx": cx,
        "w_i2h_words": w_i2h_words,
        "w_i2h_scales": w_i2h_scales,
        "b_i2h": b_i2h,
        "w_h2h_words": w_h2h_words,
        "w_h2h_scales": w_h2h_scales,
        "b_h2h": b_h2h,
        "ln_i2h_w": bf(1.0 + 0.2 * np.random.standard_normal((1, 4 * H))),
        "ln_i2h_b": bf(0.2 * np.random.standard_normal((1, 4 * H))),
        "ln_h2h_w": bf(1.0 + 0.2 * np.random.standard_normal((1, 4 * H))),
        "ln_h2h_b": bf(0.2 * np.random.standard_normal((1, 4 * H))),
        "ln_h2o_w": bf(1.0 + 0.2 * np.random.standard_normal((1, H))),
        "ln_h2o_b": bf(0.2 * np.random.standard_normal((1, H))),
    }


def reference(inputs, hx, cx, w_i2h_words, w_i2h_scales, b_i2h, w_h2h_words, w_h2h_scales, b_h2h,
              ln_i2h_w, ln_i2h_b, ln_h2h_w, ln_h2h_b, ln_h2o_w, ln_h2o_b):
    i2h = (mxq(f64(inputs), 1, "e4m3") @ unpack4(w_i2h_words, w_i2h_scales)) + f64(b_i2h)
    h2h = (mxq(f64(hx), 1, "e4m3") @ unpack4(w_h2h_words, w_h2h_scales)) + f64(b_h2h)
    x = layer_norm_1d(i2h, f64(ln_i2h_w), f64(ln_i2h_b)) + layer_norm_1d(h2h, f64(ln_h2h_w), f64(ln_h2h_b))
    g_i, g_f, g_o, g_c = np.split(x, 4, axis=1)
    in_gate = sigmoid(g_i)
    forget_gate = sigmoid(g_f + FORGET_GATE_BIAS)
    out_gate = sigmoid(g_o)
    in_transform = np.tanh(g_c)
    cx_new = forget_gate * f64(cx) + in_gate * in_transform
    hx_new = out_gate * np.tanh(layer_norm_1d(cx_new, f64(ln_h2o_w), f64(ln_h2o_b)))
    return hx_new, cx_new

@@ -1,0 +1,263 @@
+from contextlib import ExitStack
+import math
+
+import concourse.mybir as mybir
+from concourse.masks import make_identity
+
+F32 = mybir.dt.float32
+BF16 = mybir.dt.bfloat16
+I32 = mybir.dt.int32
+U32 = mybir.dt.uint32
+U8 = mybir.dt.uint8
+FP8X4 = mybir.dt.float8_e4m3fn_x4
+FP4X4 = mybir.dt.float4_e2m1fn_x4
+ALU = mybir.AluOpType
+ACT = mybir.ActivationFunctionType
+AXIS = mybir.AxisListType
+
+P = 128
+BATCH = 512
+K = 1024
+HIDDEN = 1024
+GATES = 4 * HIDDEN
+K_PASS = 4 * P
+PASSES = K // K_PASS
+BATCH_TILES = BATCH // P
+BANK = 512
+CHUNKS = GATES // BANK
+FORGET_GATE_BIAS = -1.0
+EPS = 1e-5
+
+FLOPS = 2 * 2 * BATCH * K * GATES
+
+
+def tile_layernormlstmcell_kernel(
+    tc,
+    inputs,
+    hx,
+    cx,
+    w_i2h_words,
+    w_i2h_scales,
+    b_i2h,
+    w_h2h_words,
+    w_h2h_scales,
+    b_h2h,
+    ln_i2h_w,
+    ln_i2h_b,
+    ln_h2h_w,
+    ln_h2h_b,
+    ln_h2o_w,
+    ln_h2o_b,
+    out_0,
+    out_1,
+):
+    nc = tc.nc
+    acts = (inputs, hx)
+    w_words = (w_i2h_words, w_h2h_words)
+    w_scales = (w_i2h_scales, w_h2h_scales)
+    biases = (b_i2h, b_h2h)
+    gains = (ln_i2h_w, ln_h2h_w)
+    shifts = (ln_i2h_b, ln_h2h_b)
+
+    with ExitStack() as ctx:
+        keep = ctx.enter_context(tc.tile_pool(name="keep", bufs=1))
+        stage = ctx.enter_context(tc.tile_pool(name="stage", bufs=2))
+        rows = ctx.enter_context(tc.tile_pool(name="rows", bufs=2))
+        stats = ctx.enter_context(tc.tile_pool(name="stats", bufs=4))
+        psum = ctx.enter_context(tc.psum_pool(name="psum", bufs=8))
+
+        identity = keep.tile([P, P], F32, name="identity")
+        make_identity(nc, identity[:])
+        half = keep.tile([P, 1], F32, name="half")
+        nc.gpsimd.memset(half[:], 0.5)
+
+        planes = []
+        words = []
+        for j in range(2):
+            plane = keep.tile([P, PASSES, GATES], U8, name="plane%d" % j, align_bytes=64)
+            nc.vector.memset(plane[:].bitcast(I32), 0)
+            planes.append(plane)
+            words.append(keep.tile([P, PASSES, 2 * GATES], U8, name="words%d" % j, align_bytes=64))
+        for j in range(2):
+            scale_rows = w_scales[j].bitcast(I32).rearrange("g (q r) n -> r q g n", r=4)
+            for r in range(4):
+                nc.sync.dma_start(out=planes[j][r:P:32, :, :].bitcast(I32), in_=scale_rows[r])
+
+        def load_activation(j, bt):
+            x_sb = stage.tile([P, K], BF16, tag="x_sb", bufs=4)
+            nc.sync.dma_start(out=x_sb[:], in_=acts[j][bt * P : (bt + 1) * P, :])
+            return x_sb
+
+        def load_words(j):
+            step = 2 * GATES // 4
+            for c in range(4):
+                cols = slice(c * step, (c + 1) * step)
+                nc.sync.dma_start(
+                    out=words[j][:, :, cols].bitcast(I32),
+                    in_=w_words[j][:, :, cols].bitcast(I32).rearrange("g p n -> p g n"),
+                )
+
+        x_tiles = {}
+        for j in range(2):
+            x_tiles[(j, 0)] = load_activation(j, 0)
+        for j in range(2):
+            load_words(j)
+
+        def load_repeated(vector, width, name):
+            repeated = keep.tile([P, width], BF16, name=name)
+            nc.scalar.dma_start(out=repeated[:], in_=vector.partition_broadcast(P))
+            return repeated
+
+        bias_rep = [load_repeated(biases[j], GATES, "bias_rep%d" % j) for j in range(2)]
+        gain_rep = [
+            load_repeated(gains[j].rearrange("o n -> (o n)"), GATES, "gain_rep%d" % j) for j in range(2)
+        ]
+        shift_rep = [
+            load_repeated(shifts[j].rearrange("o n -> (o n)"), GATES, "shift_rep%d" % j) for j in range(2)
+        ]
+        gain_out = load_repeated(ln_h2o_w.rearrange("o n -> (o n)"), HIDDEN, "gain_out")
+        shift_out = load_repeated(ln_h2o_b.rearrange("o n -> (o n)"), HIDDEN, "shift_out")
+        shift_sum = keep.tile([P, GATES], F32, name="shift_sum")
+        nc.gpsimd.tensor_tensor(out=shift_sum[:], in0=shift_rep[0][:], in1=shift_rep[1][:], op=ALU.add)
+
+        x_codes = {}
+        x_scales = {}
+
+        def quantise_activation(j, bt):
+            x_words = x_tiles[(j, bt)][:].bitcast(F32)
+            flipped = psum.tile([P, PASSES * 2, P], F32, tag="bank")
+            for g in range(PASSES):
+                for u in range(2):
+                    nc.tensor.transpose(
+                        flipped[:, 2 * g + u, :],
+                        x_words[:, 256 * g + u : 256 * (g + 1) : 2],
+                        identity[:],
+                    )
+            grouped = stage.tile([P, PASSES * P * 4], BF16, tag="grouped", align_bytes=64)
+            nc.scalar.copy(
+                out=grouped[:].bitcast(F32).rearrange("p (g b u) -> p g b u", g=PASSES, u=2),
+                in_=flipped[:].rearrange("p (g u) b -> p g b u", u=2),
+            )
+            codes = keep.tile([P, PASSES * P], U32, name="codes%d_%d" % (j, bt), align_bytes=64)
+            scales = keep.tile([P, PASSES * P], U8, name="scales%d_%d" % (j, bt), align_bytes=64)
+            nc.vector.quantize_mx(out=codes[:].bitcast(FP8X4), scales=scales[:], in_=grouped[:])
+            x_codes[(j, bt)] = codes
+            x_scales[(j, bt)] = scales
+
+        for bt in range(BATCH_TILES):
+            for j in range(2):
+                if bt > 0:
+                    x_tiles[(j, bt)] = load_activation(j, bt)
+                quantise_activation(j, bt)
+
+        squares = keep.tile([P, GATES], BF16, name="squares")
+
+        def row_statistics(sum_parts, values, width):
+            scale = 1.0 / math.sqrt(width - 1)
+            total = stats.tile([P, 1], F32, tag="total")
+            nc.vector.reduce_sum(out=total[:], in_=sum_parts, axis=AXIS.X)
+            neg_mean = stats.tile([P, 1], F32, tag="neg_mean")
+            nc.vector.tensor_scalar_mul(out=neg_mean[:], in0=total[:], scalar1=-1.0 / width)
+            neg_mean_scaled = stats.tile([P, 1], F32, tag="neg_mean_scaled")
+            nc.vector.tensor_scalar_mul(out=neg_mean_scaled[:], in0=total[:], scalar1=-scale / width)
+            variance = stats.tile([P, 1], F32, tag="variance")
+            nc.scalar.activation(
+                out=squares[:, :width],
+                in_=values,
+                func=ACT.Square,
+                bias=neg_mean_scaled[:],
+                scale=scale,
+                accum_out=variance[:],
+            )
+            std = stats.tile([P, 1], F32, tag="std")
+            nc.gpsimd.tensor_tensor(out=std[:], in0=variance[:], in1=half[:], op=ALU.pow)
+            std_eps = stats.tile([P, 1], F32, tag="std_eps")
+            nc.vector.tensor_scalar_add(out=std_eps[:], in0=std[:], scalar1=EPS)
+            inv_std = stats.tile([P, 1], F32, tag="inv_std")
+            nc.vector.reciprocal(out=inv_std[:], in_=std_eps[:])
+            return neg_mean, inv_std
+
+        for bt in range(BATCH_TILES):
+            batch_rows = slice(bt * P, (bt + 1) * P)
+            cx_sb = stage.tile([P, HIDDEN], BF16, tag="cx_sb")
+            nc.sync.dma_start(out=cx_sb[:], in_=cx[batch_rows, :])
+            pre = []
+            neg_mean = []
+            inv_std = []
+            for j in range(2):
+                pre_j = rows.tile([P, GATES], F32, tag="pre%d" % j)
+                sum_parts = stats.tile([P, CHUNKS], F32, tag="sum_parts")
+                for c in range(CHUNKS):
+                    acc = psum.tile([P, BANK], F32, tag="bank")
+                    for g in range(PASSES):
+                        nc.tensor.matmul_mx(
+                            out=acc[:],
+                            lhsT=x_codes[(j, bt)][:, g * P : (g + 1) * P].bitcast(FP8X4),
+                            lhsT_scale=x_scales[(j, bt)][:, g * P : (g + 1) * P],
+                            rhs=words[j][:, g, 2 * BANK * c : 2 * BANK * (c + 1)].bitcast(FP4X4),
+                            rhs_scale=planes[j][:, g, BANK * c : BANK * (c + 1)],
+                            start=(g == 0),
+                            stop=(g == PASSES - 1),
+                        )
+                    cols = slice(c * BANK, (c + 1) * BANK)
+                    nc.vector.scalar_tensor_tensor(
+                        out=pre_j[:, cols],
+                        in0=acc[:],
+                        scalar=1.0,
+                        in1=bias_rep[j][:, cols],
+                        op0=ALU.mult,
+                        op1=ALU.add,
+                        accum_out=sum_parts[:, c : c + 1],
+                    )
+                stat = row_statistics(sum_parts[:], pre_j[:], GATES)
+                pre.append(pre_j)
+                neg_mean.append(stat[0])
+                inv_std.append(stat[1])
+
+            for j in range(2):
+                nc.vector.scalar_tensor_tensor(
+                    out=pre[j][:], in0=pre[j][:], scalar=neg_mean[j][:], in1=gain_rep[j][:],
+                    op0=ALU.add, op1=ALU.mult,
+                )
+            nc.vector.scalar_tensor_tensor(
+                out=pre[0][:], in0=pre[0][:], scalar=inv_std[0][:], in1=shift_sum[:],
+                op0=ALU.mult, op1=ALU.add,
+            )
+            x = pre[1]
+            nc.vector.scalar_tensor_tensor(
+                out=x[:], in0=pre[1][:], scalar=inv_std[1][:], in1=pre[0][:],
+                op0=ALU.mult, op1=ALU.add,
+            )
+
+            in_gate = x[:, 0 * HIDDEN : 1 * HIDDEN]
+            forget_gate = x[:, 1 * HIDDEN : 2 * HIDDEN]
+            out_gate = x[:, 2 * HIDDEN : 3 * HIDDEN]
+            in_transform = x[:, 3 * HIDDEN : 4 * HIDDEN]
+            nc.scalar.activation(out=in_gate, in_=in_gate, func=ACT.Sigmoid)
+            nc.scalar.activation(out=forget_gate, in_=forget_gate, func=ACT.Sigmoid, bias=FORGET_GATE_BIAS)
+            nc.scalar.activation(out=in_transform, in_=in_transform, func=ACT.Tanh)
+            nc.scalar.activation(out=out_gate, in_=out_gate, func=ACT.Sigmoid)
+
+            nc.vector.tensor_mul(out=forget_gate, in0=forget_gate, in1=cx_sb[:])
+            nc.vector.tensor_mul(out=in_gate, in0=in_gate, in1=in_transform)
+            cell = rows.tile([P, HIDDEN], F32, tag="cell")
+            cell_sum = stats.tile([P, 1], F32, tag="cell_sum")
+            nc.vector.scalar_tensor_tensor(
+                out=cell[:], in0=forget_gate, scalar=1.0, in1=in_gate,
+                op0=ALU.mult, op1=ALU.add, accum_out=cell_sum[:],
+            )
+            nc.sync.dma_start(out=out_1[batch_rows, :], in_=cell[:])
+
+            cell_neg_mean, cell_inv_std = row_statistics(cell_sum[:], cell[:], HIDDEN)
+            hidden = rows.tile([P, HIDDEN], F32, tag="hidden")
+            nc.vector.scalar_tensor_tensor(
+                out=hidden[:], in0=cell[:], scalar=cell_neg_mean[:], in1=gain_out[:],
+                op0=ALU.add, op1=ALU.mult,
+            )
+            nc.vector.scalar_tensor_tensor(
+                out=hidden[:], in0=hidden[:], scalar=cell_inv_std[:], in1=shift_out[:],
+                op0=ALU.mult, op1=ALU.add,
+            )
+            nc.scalar.activation(out=hidden[:], in_=hidden[:], func=ACT.Tanh)
+            nc.vector.tensor_mul(out=hidden[:], in0=hidden[:], in1=out_gate)
+            nc.sync.dma_start(out=out_0[batch_rows, :], in_=hidden[:])

@@ -25,6 +25,15 @@ PASSES = K // K_PASS
 BATCH_TILES = BATCH // P
 BANK = 512
 CHUNKS = GATES // BANK
+FEATURE_TILES = GATES // P
+HIDDEN_TILES = HIDDEN // P
+BLOCKS_PER_BANK = BANK // P
+IN_GATE = 0 * HIDDEN_TILES
+FORGET_GATE = 1 * HIDDEN_TILES
+OUT_GATE = 2 * HIDDEN_TILES
+IN_TRANSFORM = 3 * HIDDEN_TILES
+GROUP_TILES = 4
+GROUPS = BATCH_TILES // GROUP_TILES
 FORGET_GATE_BIAS = -1.0
 EPS = 1e-5
 
@@ -56,18 +65,17 @@ def tile_layernormlstmcell_kernel(
     w_words = (w_i2h_words, w_h2h_words)
     w_scales = (w_i2h_scales, w_h2h_scales)
     biases = (b_i2h, b_h2h)
-    gains = (ln_i2h_w, ln_h2h_w)
-    shifts = (ln_i2h_b, ln_h2h_b)
 
     with ExitStack() as ctx:
         keep = ctx.enter_context(tc.tile_pool(name="keep", bufs=1))
         stage = ctx.enter_context(tc.tile_pool(name="stage", bufs=2))
-        rows = ctx.enter_context(tc.tile_pool(name="rows", bufs=2))
         stats = ctx.enter_context(tc.tile_pool(name="stats", bufs=4))
         psum = ctx.enter_context(tc.psum_pool(name="psum", bufs=8))
 
         identity = keep.tile([P, P], F32, name="identity")
         make_identity(nc, identity[:])
+        identity_bf16 = keep.tile([P, P], BF16, name="identity_bf16")
+        make_identity(nc, identity_bf16[:])
         half = keep.tile([P, 1], F32, name="half")
         nc.gpsimd.memset(half[:], 0.5)
 
@@ -84,7 +92,7 @@ def tile_layernormlstmcell_kernel(
                 nc.sync.dma_start(out=planes[j][r:P:32, :, :].bitcast(I32), in_=scale_rows[r])
 
         def load_activation(j, bt):
-            x_sb = stage.tile([P, K], BF16, tag="x_sb", bufs=4)
+            x_sb = stage.tile([P, K], BF16, tag="x_sb", bufs=3)
             nc.sync.dma_start(out=x_sb[:], in_=acts[j][bt * P : (bt + 1) * P, :])
             return x_sb
 
@@ -97,11 +105,15 @@ def tile_layernormlstmcell_kernel(
                     in_=w_words[j][:, :, cols].bitcast(I32).rearrange("g p n -> p g n"),
                 )
 
+        product_order = [
+            (j, grp * GROUP_TILES + t) for grp in range(GROUPS) for j in range(2) for t in range(GROUP_TILES)
+        ]
         x_tiles = {}
-        for j in range(2):
-            x_tiles[(j, 0)] = load_activation(j, 0)
-        for j in range(2):
-            load_words(j)
+        x_tiles[product_order[0]] = load_activation(*product_order[0])
+        load_words(0)
+        x_tiles[product_order[1]] = load_activation(*product_order[1])
+        x_tiles[product_order[2]] = load_activation(*product_order[2])
+        load_words(1)
 
         def load_repeated(vector, width, name):
             repeated = keep.tile([P, width], BF16, name=name)
@@ -109,22 +121,29 @@ def tile_layernormlstmcell_kernel(
             return repeated
 
         bias_rep = [load_repeated(biases[j], GATES, "bias_rep%d" % j) for j in range(2)]
-        gain_rep = [
-            load_repeated(gains[j].rearrange("o n -> (o n)"), GATES, "gain_rep%d" % j) for j in range(2)
-        ]
-        shift_rep = [
-            load_repeated(shifts[j].rearrange("o n -> (o n)"), GATES, "shift_rep%d" % j) for j in range(2)
-        ]
+        vector_rows = keep.tile([P, P], BF16, name="vector_rows")
+        for i, vector in enumerate((ln_i2h_w, ln_h2h_w, ln_i2h_b, ln_h2h_b)):
+            nc.scalar.dma_start(
+                out=vector_rows[i * FEATURE_TILES : (i + 1) * FEATURE_TILES, :],
+                in_=vector.rearrange("o (f p) -> (o f) p", p=P),
+            )
         gain_out = load_repeated(ln_h2o_w.rearrange("o n -> (o n)"), HIDDEN, "gain_out")
         shift_out = load_repeated(ln_h2o_b.rearrange("o n -> (o n)"), HIDDEN, "shift_out")
-        shift_sum = keep.tile([P, GATES], F32, name="shift_sum")
-        nc.gpsimd.tensor_tensor(out=shift_sum[:], in0=shift_rep[0][:], in1=shift_rep[1][:], op=ALU.add)
 
-        x_codes = {}
-        x_scales = {}
+        vector_cols = psum.tile([P, P], BF16, tag="bank")
+        nc.tensor.transpose(vector_cols[:], vector_rows[:], identity_bf16[:])
+        per_feature = keep.tile([P, 4, FEATURE_TILES], F32, name="per_feature")
+        nc.vector.tensor_copy(out=per_feature[:].rearrange("p i f -> p (i f)"), in_=vector_cols[:])
+        gain_col = (per_feature[:, 0, :], per_feature[:, 1, :])
+        shift_col = keep.tile([P, FEATURE_TILES], F32, name="shift_col")
+        nc.vector.tensor_add(out=shift_col[:], in0=per_feature[:, 2, :], in1=per_feature[:, 3, :])
+        forget_tiles = slice(FORGET_GATE, FORGET_GATE + HIDDEN_TILES)
+        nc.vector.tensor_scalar_add(
+            out=shift_col[:, forget_tiles], in0=shift_col[:, forget_tiles], scalar1=FORGET_GATE_BIAS
+        )
 
-        def quantise_activation(j, bt):
-            x_words = x_tiles[(j, bt)][:].bitcast(F32)
+        def quantise_activation(x_sb):
+            x_words = x_sb[:].bitcast(F32)
             flipped = psum.tile([P, PASSES * 2, P], F32, tag="bank")
             for g in range(PASSES):
                 for u in range(2):
@@ -138,126 +157,160 @@ def tile_layernormlstmcell_kernel(
                 out=grouped[:].bitcast(F32).rearrange("p (g b u) -> p g b u", g=PASSES, u=2),
                 in_=flipped[:].rearrange("p (g u) b -> p g b u", u=2),
             )
-            codes = keep.tile([P, PASSES * P], U32, name="codes%d_%d" % (j, bt), align_bytes=64)
-            scales = keep.tile([P, PASSES * P], U8, name="scales%d_%d" % (j, bt), align_bytes=64)
+            codes = stage.tile([P, PASSES * P], U32, tag="codes", bufs=4, align_bytes=64)
+            scales = stage.tile([P, PASSES * P], U8, tag="scales", bufs=4, align_bytes=64)
             nc.vector.quantize_mx(out=codes[:].bitcast(FP8X4), scales=scales[:], in_=grouped[:])
-            x_codes[(j, bt)] = codes
-            x_scales[(j, bt)] = scales
-
-        for bt in range(BATCH_TILES):
-            for j in range(2):
-                if bt > 0:
-                    x_tiles[(j, bt)] = load_activation(j, bt)
-                quantise_activation(j, bt)
+            return codes, scales
 
         squares = keep.tile([P, GATES], BF16, name="squares")
 
         def row_statistics(sum_parts, values, width):
-            scale = 1.0 / math.sqrt(width - 1)
             total = stats.tile([P, 1], F32, tag="total")
             nc.vector.reduce_sum(out=total[:], in_=sum_parts, axis=AXIS.X)
             neg_mean = stats.tile([P, 1], F32, tag="neg_mean")
             nc.vector.tensor_scalar_mul(out=neg_mean[:], in0=total[:], scalar1=-1.0 / width)
-            neg_mean_scaled = stats.tile([P, 1], F32, tag="neg_mean_scaled")
-            nc.vector.tensor_scalar_mul(out=neg_mean_scaled[:], in0=total[:], scalar1=-scale / width)
-            variance = stats.tile([P, 1], F32, tag="variance")
+            square_sum = stats.tile([P, 1], F32, tag="square_sum")
             nc.scalar.activation(
                 out=squares[:, :width],
                 in_=values,
                 func=ACT.Square,
-                bias=neg_mean_scaled[:],
-                scale=scale,
-                accum_out=variance[:],
+                bias=neg_mean[:],
+                accum_out=square_sum[:],
             )
-            std = stats.tile([P, 1], F32, tag="std")
-            nc.gpsimd.tensor_tensor(out=std[:], in0=variance[:], in1=half[:], op=ALU.pow)
+            root = stats.tile([P, 1], F32, tag="root")
+            nc.gpsimd.tensor_tensor(out=root[:], in0=square_sum[:], in1=half[:], op=ALU.pow)
             std_eps = stats.tile([P, 1], F32, tag="std_eps")
-            nc.vector.tensor_scalar_add(out=std_eps[:], in0=std[:], scalar1=EPS)
+            nc.vector.tensor_scalar(
+                out=std_eps[:], in0=root[:], scalar1=1.0 / math.sqrt(width - 1), scalar2=EPS,
+                op0=ALU.mult, op1=ALU.add,
+            )
             inv_std = stats.tile([P, 1], F32, tag="inv_std")
             nc.vector.reciprocal(out=inv_std[:], in_=std_eps[:])
             return neg_mean, inv_std
 
-        for bt in range(BATCH_TILES):
-            batch_rows = slice(bt * P, (bt + 1) * P)
-            cx_sb = stage.tile([P, HIDDEN], BF16, tag="cx_sb")
-            nc.sync.dma_start(out=cx_sb[:], in_=cx[batch_rows, :])
-            pre = []
-            neg_mean = []
-            inv_std = []
-            for j in range(2):
-                pre_j = rows.tile([P, GATES], F32, tag="pre%d" % j)
-                sum_parts = stats.tile([P, CHUNKS], F32, tag="sum_parts")
-                for c in range(CHUNKS):
-                    acc = psum.tile([P, BANK], F32, tag="bank")
-                    for g in range(PASSES):
-                        nc.tensor.matmul_mx(
-                            out=acc[:],
-                            lhsT=x_codes[(j, bt)][:, g * P : (g + 1) * P].bitcast(FP8X4),
-                            lhsT_scale=x_scales[(j, bt)][:, g * P : (g + 1) * P],
-                            rhs=words[j][:, g, 2 * BANK * c : 2 * BANK * (c + 1)].bitcast(FP4X4),
-                            rhs_scale=planes[j][:, g, BANK * c : BANK * (c + 1)],
-                            start=(g == 0),
-                            stop=(g == PASSES - 1),
-                        )
-                    cols = slice(c * BANK, (c + 1) * BANK)
+        pre = [
+            [keep.tile([P, GROUP_TILES, GATES], F32, name="pre%d_%d" % (j, grp)) for grp in range(GROUPS)]
+            for j in range(2)
+        ]
+
+        def normalised_product(j, bt):
+            if (j, bt) not in x_tiles:
+                x_tiles[(j, bt)] = load_activation(j, bt)
+            codes, scales = quantise_activation(x_tiles[(j, bt)])
+            v = pre[j][bt // GROUP_TILES][:, bt % GROUP_TILES, :]
+            sum_parts = stats.tile([P, CHUNKS], F32, tag="sum_parts")
+            for c in range(CHUNKS):
+                acc = psum.tile([P, BANK], F32, tag="bank")
+                for g in range(PASSES):
+                    nc.tensor.matmul_mx(
+                        out=acc[:],
+                        lhsT=codes[:, g * P : (g + 1) * P].bitcast(FP8X4),
+                        lhsT_scale=scales[:, g * P : (g + 1) * P],
+                        rhs=words[j][:, g, 2 * BANK * c : 2 * BANK * (c + 1)].bitcast(FP4X4),
+                        rhs_scale=planes[j][:, g, BANK * c : BANK * (c + 1)],
+                        start=(g == 0),
+                        stop=(g == PASSES - 1),
+                    )
+                cols = slice(c * BANK, (c + 1) * BANK)
+                nc.vector.scalar_tensor_tensor(
+                    out=v[:, cols],
+                    in0=acc[:],
+                    scalar=1.0,
+                    in1=bias_rep[j][:, cols],
+                    op0=ALU.mult,
+                    op1=ALU.add,
+                    accum_out=sum_parts[:, c : c + 1],
+                )
+            neg_mean, inv_std = row_statistics(sum_parts[:], v, GATES)
+            nc.gpsimd.tensor_scalar(
+                out=v, in0=v, scalar1=neg_mean[:], scalar2=inv_std[:], op0=ALU.add, op1=ALU.mult
+            )
+
+        def to_features(j, grp, f):
+            flipped = psum.tile([P, GROUP_TILES, P], F32, tag="bank")
+            for t in range(GROUP_TILES):
+                nc.tensor.transpose(flipped[:, t, :], pre[j][grp][:, t, f * P : (f + 1) * P], identity[:])
+            return flipped
+
+        def gate(grp, f, func):
+            block = slice(f * P, (f + 1) * P)
+            first = pre[0][grp][:, :, block]
+            nc.scalar.activation(
+                out=first,
+                in_=to_features(0, grp, f)[:],
+                func=ACT.Identity,
+                scale=gain_col[0][:, f : f + 1],
+                bias=shift_col[:, f : f + 1],
+            )
+            result = pre[1][grp][:, :, block]
+            nc.vector.scalar_tensor_tensor(
+                out=result,
+                in0=to_features(1, grp, f)[:],
+                scalar=gain_col[1][:, f : f + 1],
+                in1=first,
+                op0=ALU.mult,
+                op1=ALU.add,
+            )
+            nc.scalar.activation(out=result, in_=result, func=func)
+            return result
+
+        def to_rows(grp, t, first_tile, bank):
+            back = psum.tile([P, BANK], F32, tag="bank")
+            for q in range(BLOCKS_PER_BANK):
+                f = first_tile + bank * BLOCKS_PER_BANK + q
+                nc.tensor.transpose(
+                    back[:, q * P : (q + 1) * P], pre[1][grp][:, t, f * P : (f + 1) * P], identity[:]
+                )
+            return back
+
+        for j, bt in product_order:
+            normalised_product(j, bt)
+
+        for grp in range(GROUPS):
+            for h in range(HIDDEN_TILES):
+                in_gate = gate(grp, IN_GATE + h, ACT.Sigmoid)
+                in_transform = gate(grp, IN_TRANSFORM + h, ACT.Tanh)
+                nc.gpsimd.tensor_tensor(out=in_gate, in0=in_gate, in1=in_transform, op=ALU.mult)
+                gate(grp, FORGET_GATE + h, ACT.Sigmoid)
+            for h in range(HIDDEN_TILES):
+                gate(grp, OUT_GATE + h, ACT.Sigmoid)
+
+            for t in range(GROUP_TILES):
+                bt = grp * GROUP_TILES + t
+                batch_rows = slice(bt * P, (bt + 1) * P)
+                cx_sb = stage.tile([P, HIDDEN], BF16, tag="cx_sb")
+                nc.sync.dma_start(out=cx_sb[:], in_=cx[batch_rows, :])
+                cell = pre[0][grp][:, t, 0:HIDDEN]
+                hidden = pre[0][grp][:, t, HIDDEN : 2 * HIDDEN]
+
+                cell_sums = stats.tile([P, HIDDEN // BANK], F32, tag="cell_sums")
+                for bank in range(HIDDEN // BANK):
+                    cols = slice(bank * BANK, (bank + 1) * BANK)
+                    nc.vector.tensor_mul(
+                        out=cell[:, cols], in0=to_rows(grp, t, FORGET_GATE, bank)[:], in1=cx_sb[:, cols]
+                    )
                     nc.vector.scalar_tensor_tensor(
-                        out=pre_j[:, cols],
-                        in0=acc[:],
+                        out=cell[:, cols],
+                        in0=to_rows(grp, t, IN_GATE, bank)[:],
                         scalar=1.0,
-                        in1=bias_rep[j][:, cols],
+                        in1=cell[:, cols],
                         op0=ALU.mult,
                         op1=ALU.add,
-                        accum_out=sum_parts[:, c : c + 1],
+                        accum_out=cell_sums[:, bank : bank + 1],
                     )
-                stat = row_statistics(sum_parts[:], pre_j[:], GATES)
-                pre.append(pre_j)
-                neg_mean.append(stat[0])
-                inv_std.append(stat[1])
+                nc.sync.dma_start(out=out_1[batch_rows, :], in_=cell)
 
-            for j in range(2):
+                neg_mean, inv_std = row_statistics(cell_sums[:], cell, HIDDEN)
                 nc.vector.scalar_tensor_tensor(
-                    out=pre[j][:], in0=pre[j][:], scalar=neg_mean[j][:], in1=gain_rep[j][:],
-                    op0=ALU.add, op1=ALU.mult,
+                    out=hidden, in0=cell, scalar=neg_mean[:], in1=gain_out[:], op0=ALU.add, op1=ALU.mult
                 )
-            nc.vector.scalar_tensor_tensor(
-                out=pre[0][:], in0=pre[0][:], scalar=inv_std[0][:], in1=shift_sum[:],
-                op0=ALU.mult, op1=ALU.add,
-            )
-            x = pre[1]
-            nc.vector.scalar_tensor_tensor(
-                out=x[:], in0=pre[1][:], scalar=inv_std[1][:], in1=pre[0][:],
-                op0=ALU.mult, op1=ALU.add,
-            )
-
-            in_gate = x[:, 0 * HIDDEN : 1 * HIDDEN]
-            forget_gate = x[:, 1 * HIDDEN : 2 * HIDDEN]
-            out_gate = x[:, 2 * HIDDEN : 3 * HIDDEN]
-            in_transform = x[:, 3 * HIDDEN : 4 * HIDDEN]
-            nc.scalar.activation(out=in_gate, in_=in_gate, func=ACT.Sigmoid)
-            nc.scalar.activation(out=forget_gate, in_=forget_gate, func=ACT.Sigmoid, bias=FORGET_GATE_BIAS)
-            nc.scalar.activation(out=in_transform, in_=in_transform, func=ACT.Tanh)
-            nc.scalar.activation(out=out_gate, in_=out_gate, func=ACT.Sigmoid)
-
-            nc.vector.tensor_mul(out=forget_gate, in0=forget_gate, in1=cx_sb[:])
-            nc.vector.tensor_mul(out=in_gate, in0=in_gate, in1=in_transform)
-            cell = rows.tile([P, HIDDEN], F32, tag="cell")
-            cell_sum = stats.tile([P, 1], F32, tag="cell_sum")
-            nc.vector.scalar_tensor_tensor(
-                out=cell[:], in0=forget_gate, scalar=1.0, in1=in_gate,
-                op0=ALU.mult, op1=ALU.add, accum_out=cell_sum[:],
-            )
-            nc.sync.dma_start(out=out_1[batch_rows, :], in_=cell[:])
-
-            cell_neg_mean, cell_inv_std = row_statistics(cell_sum[:], cell[:], HIDDEN)
-            hidden = rows.tile([P, HIDDEN], F32, tag="hidden")
-            nc.vector.scalar_tensor_tensor(
-                out=hidden[:], in0=cell[:], scalar=cell_neg_mean[:], in1=gain_out[:],
-                op0=ALU.add, op1=ALU.mult,
-            )
-            nc.vector.scalar_tensor_tensor(
-                out=hidden[:], in0=hidden[:], scalar=cell_inv_std[:], in1=shift_out[:],
-                op0=ALU.mult, op1=ALU.add,
-            )
-            nc.scalar.activation(out=hidden[:], in_=hidden[:], func=ACT.Tanh)
-            nc.vector.tensor_mul(out=hidden[:], in0=hidden[:], in1=out_gate)
-            nc.sync.dma_start(out=out_0[batch_rows, :], in_=hidden[:])
+                nc.vector.scalar_tensor_tensor(
+                    out=hidden, in0=hidden, scalar=inv_std[:], in1=shift_out[:], op0=ALU.mult, op1=ALU.add
+                )
+                nc.scalar.activation(out=hidden, in_=hidden, func=ACT.Tanh)
+                for bank in range(HIDDEN // BANK):
+                    cols = slice(bank * BANK, (bank + 1) * BANK)
+                    nc.vector.tensor_mul(
+                        out=hidden[:, cols], in0=to_rows(grp, t, OUT_GATE, bank)[:], in1=hidden[:, cols]
+                    )
+                nc.sync.dma_start(out=out_0[batch_rows, :], in_=hidden)

@@ -222,8 +222,15 @@ def tile_layernormlstmcell_kernel(
                     accum_out=sum_parts[:, c : c + 1],
                 )
             neg_mean, inv_std = row_statistics(sum_parts[:], v, GATES)
-            nc.gpsimd.tensor_scalar(
-                out=v, in0=v, scalar1=neg_mean[:], scalar2=inv_std[:], op0=ALU.add, op1=ALU.mult
+            left = v[:, : GATES // 2]
+            nc.vector.tensor_scalar(
+                out=left, in0=left, scalar1=neg_mean[:], scalar2=inv_std[:], op0=ALU.add, op1=ALU.mult
+            )
+            neg_mean_over_std = stats.tile([P, 1], F32, tag="neg_mean_over_std")
+            nc.vector.tensor_mul(out=neg_mean_over_std[:], in0=neg_mean[:], in1=inv_std[:])
+            right = v[:, GATES // 2 :]
+            nc.scalar.activation(
+                out=right, in_=right, func=ACT.Identity, scale=inv_std[:], bias=neg_mean_over_std[:]
             )
 
         def to_features(j, grp, f):
@@ -270,7 +277,7 @@ def tile_layernormlstmcell_kernel(
             for h in range(HIDDEN_TILES):
                 in_gate = gate(grp, IN_GATE + h, ACT.Sigmoid)
                 in_transform = gate(grp, IN_TRANSFORM + h, ACT.Tanh)
-                nc.gpsimd.tensor_tensor(out=in_gate, in0=in_gate, in1=in_transform, op=ALU.mult)
+                nc.vector.tensor_mul(out=in_gate, in0=in_gate, in1=in_transform)
                 gate(grp, FORGET_GATE + h, ACT.Sigmoid)
             for h in range(HIDDEN_TILES):
                 gate(grp, OUT_GATE + h, ACT.Sigmoid)

@@ -86,17 +86,16 @@ def tile_layernormlstmcell_kernel(
             nc.vector.memset(plane[:].bitcast(I32), 0)
             planes.append(plane)
             words.append(keep.tile([P, PASSES, 2 * GATES], U8, name="words%d" % j, align_bytes=64))
-        for j in range(2):
-            scale_rows = w_scales[j].bitcast(I32).rearrange("g (q r) n -> r q g n", r=4)
-            for r in range(4):
-                nc.sync.dma_start(out=planes[j][r:P:32, :, :].bitcast(I32), in_=scale_rows[r])
 
         def load_activation(j, bt):
             x_sb = stage.tile([P, K], BF16, tag="x_sb", bufs=3)
             nc.sync.dma_start(out=x_sb[:], in_=acts[j][bt * P : (bt + 1) * P, :])
             return x_sb
 
-        def load_words(j):
+        def load_weight(j):
+            scale_rows = w_scales[j].bitcast(I32).rearrange("g (q r) n -> r q g n", r=4)
+            for r in range(4):
+                nc.sync.dma_start(out=planes[j][r:P:32, :, :].bitcast(I32), in_=scale_rows[r])
             step = 2 * GATES // 4
             for c in range(4):
                 cols = slice(c * step, (c + 1) * step)
@@ -110,37 +109,25 @@ def tile_layernormlstmcell_kernel(
         ]
         x_tiles = {}
         x_tiles[product_order[0]] = load_activation(*product_order[0])
-        load_words(0)
+        load_weight(0)
         x_tiles[product_order[1]] = load_activation(*product_order[1])
         x_tiles[product_order[2]] = load_activation(*product_order[2])
-        load_words(1)
+        load_weight(1)
 
         def load_repeated(vector, width, name):
             repeated = keep.tile([P, width], BF16, name=name)
             nc.scalar.dma_start(out=repeated[:], in_=vector.partition_broadcast(P))
             return repeated
 
-        bias_rep = [load_repeated(biases[j], GATES, "bias_rep%d" % j) for j in range(2)]
         vector_rows = keep.tile([P, P], BF16, name="vector_rows")
         for i, vector in enumerate((ln_i2h_w, ln_h2h_w, ln_i2h_b, ln_h2h_b)):
             nc.scalar.dma_start(
                 out=vector_rows[i * FEATURE_TILES : (i + 1) * FEATURE_TILES, :],
                 in_=vector.rearrange("o (f p) -> (o f) p", p=P),
             )
+        bias_rep = [load_repeated(biases[j], GATES, "bias_rep%d" % j) for j in range(2)]
         gain_out = load_repeated(ln_h2o_w.rearrange("o n -> (o n)"), HIDDEN, "gain_out")
         shift_out = load_repeated(ln_h2o_b.rearrange("o n -> (o n)"), HIDDEN, "shift_out")
-
-        vector_cols = psum.tile([P, P], BF16, tag="bank")
-        nc.tensor.transpose(vector_cols[:], vector_rows[:], identity_bf16[:])
-        per_feature = keep.tile([P, 4, FEATURE_TILES], F32, name="per_feature")
-        nc.vector.tensor_copy(out=per_feature[:].rearrange("p i f -> p (i f)"), in_=vector_cols[:])
-        gain_col = (per_feature[:, 0, :], per_feature[:, 1, :])
-        shift_col = keep.tile([P, FEATURE_TILES], F32, name="shift_col")
-        nc.vector.tensor_add(out=shift_col[:], in0=per_feature[:, 2, :], in1=per_feature[:, 3, :])
-        forget_tiles = slice(FORGET_GATE, FORGET_GATE + HIDDEN_TILES)
-        nc.vector.tensor_scalar_add(
-            out=shift_col[:, forget_tiles], in0=shift_col[:, forget_tiles], scalar1=FORGET_GATE_BIAS
-        )
 
         def quantise_activation(x_sb):
             x_words = x_sb[:].bitcast(F32)
@@ -270,54 +257,82 @@ def tile_layernormlstmcell_kernel(
                 )
             return back
 
+        def cell_gates(grp, h):
+            in_gate = gate(grp, IN_GATE + h, ACT.Sigmoid)
+            in_transform = gate(grp, IN_TRANSFORM + h, ACT.Tanh)
+            nc.vector.tensor_mul(out=in_gate, in0=in_gate, in1=in_transform)
+            gate(grp, FORGET_GATE + h, ACT.Sigmoid)
+
+        def cell_of(grp, t):
+            return pre[0][grp][:, t, 0:HIDDEN]
+
+        def hidden_of(grp, t):
+            return pre[0][grp][:, t, HIDDEN : 2 * HIDDEN]
+
+        def batch_rows(grp, t):
+            bt = grp * GROUP_TILES + t
+            return slice(bt * P, (bt + 1) * P)
+
+        def new_cell(grp, t, bank, cell_sums):
+            cols = slice(bank * BANK, (bank + 1) * BANK)
+            cx_sb = stage.tile([P, BANK], BF16, tag="cx_sb", bufs=4)
+            nc.sync.dma_start(out=cx_sb[:], in_=cx[batch_rows(grp, t), cols])
+            cell = cell_of(grp, t)[:, cols]
+            nc.vector.tensor_mul(out=cell, in0=to_rows(grp, t, FORGET_GATE, bank)[:], in1=cx_sb[:])
+            nc.vector.scalar_tensor_tensor(
+                out=cell,
+                in0=to_rows(grp, t, IN_GATE, bank)[:],
+                scalar=1.0,
+                in1=cell,
+                op0=ALU.mult,
+                op1=ALU.add,
+                accum_out=cell_sums[:, bank : bank + 1],
+            )
+
+        def new_hidden(grp, t, neg_mean, inv_std):
+            hidden = hidden_of(grp, t)
+            nc.vector.scalar_tensor_tensor(
+                out=hidden, in0=cell_of(grp, t), scalar=neg_mean[:], in1=gain_out[:], op0=ALU.add, op1=ALU.mult
+            )
+            nc.vector.scalar_tensor_tensor(
+                out=hidden, in0=hidden, scalar=inv_std[:], in1=shift_out[:], op0=ALU.mult, op1=ALU.add
+            )
+            nc.scalar.activation(out=hidden, in_=hidden, func=ACT.Tanh)
+            for bank in range(HIDDEN // BANK):
+                cols = slice(bank * BANK, (bank + 1) * BANK)
+                nc.vector.tensor_mul(
+                    out=hidden[:, cols], in0=to_rows(grp, t, OUT_GATE, bank)[:], in1=hidden[:, cols]
+                )
+            nc.sync.dma_start(out=out_0[batch_rows(grp, t), :], in_=hidden)
+
         for j, bt in product_order:
             normalised_product(j, bt)
 
+        vector_cols = psum.tile([P, P], BF16, tag="bank")
+        nc.tensor.transpose(vector_cols[:], vector_rows[:], identity_bf16[:])
+        per_feature = keep.tile([P, 4, FEATURE_TILES], F32, name="per_feature")
+        nc.vector.tensor_copy(out=per_feature[:].rearrange("p i f -> p (i f)"), in_=vector_cols[:])
+        gain_col = (per_feature[:, 0, :], per_feature[:, 1, :])
+        shift_col = keep.tile([P, FEATURE_TILES], F32, name="shift_col")
+        nc.vector.tensor_add(out=shift_col[:], in0=per_feature[:, 2, :], in1=per_feature[:, 3, :])
+        forget_tiles = slice(FORGET_GATE, FORGET_GATE + HIDDEN_TILES)
+        nc.vector.tensor_scalar_add(
+            out=shift_col[:, forget_tiles], in0=shift_col[:, forget_tiles], scalar1=FORGET_GATE_BIAS
+        )
+
         for grp in range(GROUPS):
-            for h in range(HIDDEN_TILES):
-                in_gate = gate(grp, IN_GATE + h, ACT.Sigmoid)
-                in_transform = gate(grp, IN_TRANSFORM + h, ACT.Tanh)
-                nc.vector.tensor_mul(out=in_gate, in0=in_gate, in1=in_transform)
-                gate(grp, FORGET_GATE + h, ACT.Sigmoid)
+            tiles = range(GROUP_TILES)
+            cell_sums = [stats.tile([P, HIDDEN // BANK], F32, name="cell_sums%d" % t, tag="cell_sums") for t in tiles]
+            for bank in range(HIDDEN // BANK):
+                for h in range(bank * BLOCKS_PER_BANK, (bank + 1) * BLOCKS_PER_BANK):
+                    cell_gates(grp, h)
+                for t in tiles:
+                    new_cell(grp, t, bank, cell_sums[t])
+            cell_stats = []
+            for t in tiles:
+                nc.sync.dma_start(out=out_1[batch_rows(grp, t), :], in_=cell_of(grp, t))
+                cell_stats.append(row_statistics(cell_sums[t][:], cell_of(grp, t), HIDDEN))
             for h in range(HIDDEN_TILES):
                 gate(grp, OUT_GATE + h, ACT.Sigmoid)
-
-            for t in range(GROUP_TILES):
-                bt = grp * GROUP_TILES + t
-                batch_rows = slice(bt * P, (bt + 1) * P)
-                cx_sb = stage.tile([P, HIDDEN], BF16, tag="cx_sb")
-                nc.sync.dma_start(out=cx_sb[:], in_=cx[batch_rows, :])
-                cell = pre[0][grp][:, t, 0:HIDDEN]
-                hidden = pre[0][grp][:, t, HIDDEN : 2 * HIDDEN]
-
-                cell_sums = stats.tile([P, HIDDEN // BANK], F32, tag="cell_sums")
-                for bank in range(HIDDEN // BANK):
-                    cols = slice(bank * BANK, (bank + 1) * BANK)
-                    nc.vector.tensor_mul(
-                        out=cell[:, cols], in0=to_rows(grp, t, FORGET_GATE, bank)[:], in1=cx_sb[:, cols]
-                    )
-                    nc.vector.scalar_tensor_tensor(
-                        out=cell[:, cols],
-                        in0=to_rows(grp, t, IN_GATE, bank)[:],
-                        scalar=1.0,
-                        in1=cell[:, cols],
-                        op0=ALU.mult,
-                        op1=ALU.add,
-                        accum_out=cell_sums[:, bank : bank + 1],
-                    )
-                nc.sync.dma_start(out=out_1[batch_rows, :], in_=cell)
-
-                neg_mean, inv_std = row_statistics(cell_sums[:], cell, HIDDEN)
-                nc.vector.scalar_tensor_tensor(
-                    out=hidden, in0=cell, scalar=neg_mean[:], in1=gain_out[:], op0=ALU.add, op1=ALU.mult
-                )
-                nc.vector.scalar_tensor_tensor(
-                    out=hidden, in0=hidden, scalar=inv_std[:], in1=shift_out[:], op0=ALU.mult, op1=ALU.add
-                )
-                nc.scalar.activation(out=hidden, in_=hidden, func=ACT.Tanh)
-                for bank in range(HIDDEN // BANK):
-                    cols = slice(bank * BANK, (bank + 1) * BANK)
-                    nc.vector.tensor_mul(
-                        out=hidden[:, cols], in0=to_rows(grp, t, OUT_GATE, bank)[:], in1=hidden[:, cols]
-                    )
-                nc.sync.dma_start(out=out_0[batch_rows, :], in_=hidden)
+            for t in tiles:
+                new_hidden(grp, t, *cell_stats[t])

@@ -25,15 +25,18 @@ PASSES = K // K_PASS
 BATCH_TILES = BATCH // P
 BANK = 512
 CHUNKS = GATES // BANK
+QUARTERS = 4
+QUARTER = GATES // QUARTERS
+CHUNKS_PER_QUARTER = CHUNKS // QUARTERS
 FEATURE_TILES = GATES // P
 HIDDEN_TILES = HIDDEN // P
+HIDDEN_BANKS = HIDDEN // BANK
 BLOCKS_PER_BANK = BANK // P
 IN_GATE = 0 * HIDDEN_TILES
 FORGET_GATE = 1 * HIDDEN_TILES
 OUT_GATE = 2 * HIDDEN_TILES
 IN_TRANSFORM = 3 * HIDDEN_TILES
-GROUP_TILES = 4
-GROUPS = BATCH_TILES // GROUP_TILES
+VECTOR_SHARE = 5 * GATES // 8
 FORGET_GATE_BIAS = -1.0
 EPS = 1e-5
 
@@ -65,6 +68,7 @@ def tile_layernormlstmcell_kernel(
     w_words = (w_i2h_words, w_h2h_words)
     w_scales = (w_i2h_scales, w_h2h_scales)
     biases = (b_i2h, b_h2h)
+    product_order = [(j, bt) for j in range(2) for bt in range(BATCH_TILES)]
 
     with ExitStack() as ctx:
         keep = ctx.enter_context(tc.tile_pool(name="keep", bufs=1))
@@ -79,91 +83,24 @@ def tile_layernormlstmcell_kernel(
         half = keep.tile([P, 1], F32, name="half")
         nc.gpsimd.memset(half[:], 0.5)
 
-        planes = []
-        words = []
-        for j in range(2):
-            plane = keep.tile([P, PASSES, GATES], U8, name="plane%d" % j, align_bytes=64)
-            nc.vector.memset(plane[:].bitcast(I32), 0)
-            planes.append(plane)
-            words.append(keep.tile([P, PASSES, 2 * GATES], U8, name="words%d" % j, align_bytes=64))
-
-        def load_activation(j, bt):
-            x_sb = stage.tile([P, K], BF16, tag="x_sb", bufs=3)
-            nc.sync.dma_start(out=x_sb[:], in_=acts[j][bt * P : (bt + 1) * P, :])
-            return x_sb
-
-        def load_weight(j):
-            scale_rows = w_scales[j].bitcast(I32).rearrange("g (q r) n -> r q g n", r=4)
-            for r in range(4):
-                nc.sync.dma_start(out=planes[j][r:P:32, :, :].bitcast(I32), in_=scale_rows[r])
-            step = 2 * GATES // 4
-            for c in range(4):
-                cols = slice(c * step, (c + 1) * step)
-                nc.sync.dma_start(
-                    out=words[j][:, :, cols].bitcast(I32),
-                    in_=w_words[j][:, :, cols].bitcast(I32).rearrange("g p n -> p g n"),
-                )
-
-        product_order = [
-            (j, grp * GROUP_TILES + t) for grp in range(GROUPS) for j in range(2) for t in range(GROUP_TILES)
-        ]
-        x_tiles = {}
-        x_tiles[product_order[0]] = load_activation(*product_order[0])
-        load_weight(0)
-        x_tiles[product_order[1]] = load_activation(*product_order[1])
-        x_tiles[product_order[2]] = load_activation(*product_order[2])
-        load_weight(1)
-
-        def load_repeated(vector, width, name):
-            repeated = keep.tile([P, width], BF16, name=name)
-            nc.scalar.dma_start(out=repeated[:], in_=vector.partition_broadcast(P))
-            return repeated
-
+        pre = [[keep.tile([P, GATES], F32, name="pre%d_%d" % (j, bt)) for bt in range(BATCH_TILES)] for j in range(2)]
         vector_rows = keep.tile([P, P], BF16, name="vector_rows")
-        for i, vector in enumerate((ln_i2h_w, ln_h2h_w, ln_i2h_b, ln_h2h_b)):
-            nc.scalar.dma_start(
-                out=vector_rows[i * FEATURE_TILES : (i + 1) * FEATURE_TILES, :],
-                in_=vector.rearrange("o (f p) -> (o f) p", p=P),
-            )
-        bias_rep = [load_repeated(biases[j], GATES, "bias_rep%d" % j) for j in range(2)]
-        gain_out = load_repeated(ln_h2o_w.rearrange("o n -> (o n)"), HIDDEN, "gain_out")
-        shift_out = load_repeated(ln_h2o_b.rearrange("o n -> (o n)"), HIDDEN, "shift_out")
+        gain_out = keep.tile([P, HIDDEN], BF16, name="gain_out")
+        shift_out = keep.tile([P, HIDDEN], BF16, name="shift_out")
 
-        def quantise_activation(x_sb):
-            x_words = x_sb[:].bitcast(F32)
-            flipped = psum.tile([P, PASSES * 2, P], F32, tag="bank")
-            for g in range(PASSES):
-                for u in range(2):
-                    nc.tensor.transpose(
-                        flipped[:, 2 * g + u, :],
-                        x_words[:, 256 * g + u : 256 * (g + 1) : 2],
-                        identity[:],
-                    )
-            grouped = stage.tile([P, PASSES * P * 4], BF16, tag="grouped", align_bytes=64)
-            nc.scalar.copy(
-                out=grouped[:].bitcast(F32).rearrange("p (g b u) -> p g b u", g=PASSES, u=2),
-                in_=flipped[:].rearrange("p (g u) b -> p g b u", u=2),
-            )
-            codes = stage.tile([P, PASSES * P], U32, tag="codes", bufs=4, align_bytes=64)
-            scales = stage.tile([P, PASSES * P], U8, tag="scales", bufs=4, align_bytes=64)
-            nc.vector.quantize_mx(out=codes[:].bitcast(FP8X4), scales=scales[:], in_=grouped[:])
-            return codes, scales
-
-        squares = keep.tile([P, GATES], BF16, name="squares")
-
-        def row_statistics(sum_parts, values, width):
+        def centred_squares(sum_parts, values, squares):
+            width = values.shape[1]
             total = stats.tile([P, 1], F32, tag="total")
             nc.vector.reduce_sum(out=total[:], in_=sum_parts, axis=AXIS.X)
             neg_mean = stats.tile([P, 1], F32, tag="neg_mean")
             nc.vector.tensor_scalar_mul(out=neg_mean[:], in0=total[:], scalar1=-1.0 / width)
             square_sum = stats.tile([P, 1], F32, tag="square_sum")
             nc.scalar.activation(
-                out=squares[:, :width],
-                in_=values,
-                func=ACT.Square,
-                bias=neg_mean[:],
-                accum_out=square_sum[:],
+                out=squares, in_=values, func=ACT.Square, bias=neg_mean[:], accum_out=square_sum[:]
             )
+            return neg_mean, square_sum
+
+        def inverse_deviation(square_sum, width):
             root = stats.tile([P, 1], F32, tag="root")
             nc.gpsimd.tensor_tensor(out=root[:], in0=square_sum[:], in1=half[:], op=ALU.pow)
             std_eps = stats.tile([P, 1], F32, tag="std_eps")
@@ -173,166 +110,243 @@ def tile_layernormlstmcell_kernel(
             )
             inv_std = stats.tile([P, 1], F32, tag="inv_std")
             nc.vector.reciprocal(out=inv_std[:], in_=std_eps[:])
-            return neg_mean, inv_std
+            return inv_std
 
-        pre = [
-            [keep.tile([P, GROUP_TILES, GATES], F32, name="pre%d_%d" % (j, grp)) for grp in range(GROUPS)]
-            for j in range(2)
-        ]
+        with tc.tile_pool(name="weights", bufs=1) as weights:
+            planes = []
+            for j in range(2):
+                plane = weights.tile([P, PASSES, GATES], U8, name="plane%d" % j, align_bytes=64)
+                nc.vector.memset(plane[:].bitcast(I32), 0)
+                planes.append(plane)
+            words = [
+                [weights.tile([P, PASSES, 2 * QUARTER], U8, name="words%d_%d" % (j, c), align_bytes=64) for c in range(QUARTERS)]
+                for j in range(2)
+            ]
+            bias_rep = [
+                [weights.tile([P, QUARTER], BF16, name="bias_rep%d_%d" % (j, c)) for c in range(QUARTERS)]
+                for j in range(2)
+            ]
+            squares = weights.tile([P, GATES], BF16, name="squares")
 
-        def normalised_product(j, bt):
-            if (j, bt) not in x_tiles:
-                x_tiles[(j, bt)] = load_activation(j, bt)
-            codes, scales = quantise_activation(x_tiles[(j, bt)])
-            v = pre[j][bt // GROUP_TILES][:, bt % GROUP_TILES, :]
-            sum_parts = stats.tile([P, CHUNKS], F32, tag="sum_parts")
-            for c in range(CHUNKS):
-                acc = psum.tile([P, BANK], F32, tag="bank")
-                for g in range(PASSES):
-                    nc.tensor.matmul_mx(
-                        out=acc[:],
-                        lhsT=codes[:, g * P : (g + 1) * P].bitcast(FP8X4),
-                        lhsT_scale=scales[:, g * P : (g + 1) * P],
-                        rhs=words[j][:, g, 2 * BANK * c : 2 * BANK * (c + 1)].bitcast(FP4X4),
-                        rhs_scale=planes[j][:, g, BANK * c : BANK * (c + 1)],
-                        start=(g == 0),
-                        stop=(g == PASSES - 1),
+            def load_activation(j, bt):
+                x_sb = stage.tile([P, K], BF16, tag="x_sb", bufs=3)
+                nc.sync.dma_start(out=x_sb[:], in_=acts[j][bt * P : (bt + 1) * P, :])
+                return x_sb
+
+            def load_weight(j):
+                scale_rows = w_scales[j].bitcast(I32).rearrange("g (q r) n -> r q g n", r=4)
+                for r in range(4):
+                    nc.sync.dma_start(out=planes[j][r:P:32, :, :].bitcast(I32), in_=scale_rows[r])
+                for c in range(QUARTERS):
+                    nc.sync.dma_start(
+                        out=words[j][c][:].bitcast(I32),
+                        in_=w_words[j][:, :, 2 * c * QUARTER : 2 * (c + 1) * QUARTER].bitcast(I32).rearrange("g p n -> p g n"),
                     )
-                cols = slice(c * BANK, (c + 1) * BANK)
+                    nc.sync.dma_start(
+                        out=bias_rep[j][c][:], in_=biases[j][c * QUARTER : (c + 1) * QUARTER].partition_broadcast(P)
+                    )
+
+            x_tiles = {}
+            with tc.manual_schedule():
+                x_tiles[product_order[0]] = load_activation(*product_order[0])
+                x_tiles[product_order[1]] = load_activation(*product_order[1])
+                load_weight(0)
+                x_tiles[product_order[2]] = load_activation(*product_order[2])
+                load_weight(1)
+                for i, vector in enumerate((ln_i2h_w, ln_h2h_w, ln_i2h_b, ln_h2h_b)):
+                    nc.sync.dma_start(
+                        out=vector_rows[i * FEATURE_TILES : (i + 1) * FEATURE_TILES, :],
+                        in_=vector.rearrange("o (f p) -> (o f) p", p=P),
+                    )
+                nc.sync.dma_start(out=gain_out[:], in_=ln_h2o_w.rearrange("o n -> (o n)").partition_broadcast(P))
+                nc.sync.dma_start(out=shift_out[:], in_=ln_h2o_b.rearrange("o n -> (o n)").partition_broadcast(P))
+
+            def regroup_activation(j, bt):
+                if (j, bt) not in x_tiles:
+                    x_tiles[(j, bt)] = load_activation(j, bt)
+                x_words = x_tiles[(j, bt)][:].bitcast(F32)
+                flipped = psum.tile([P, PASSES * 2, P], F32, tag="bank")
+                for g in range(PASSES):
+                    for u in range(2):
+                        nc.tensor.transpose(
+                            flipped[:, 2 * g + u, :],
+                            x_words[:, 256 * g + u : 256 * (g + 1) : 2],
+                            identity[:],
+                        )
+                grouped = stage.tile([P, PASSES * P * 4], BF16, tag="grouped", align_bytes=64)
+                nc.scalar.copy(
+                    out=grouped[:].bitcast(F32).rearrange("p (g b u) -> p g b u", g=PASSES, u=2),
+                    in_=flipped[:].rearrange("p (g u) b -> p g b u", u=2),
+                )
+                return grouped
+
+            def quantise_activation(grouped):
+                codes = stage.tile([P, PASSES * P], U32, tag="codes", align_bytes=64)
+                scales = stage.tile([P, PASSES * P], U8, tag="scales", align_bytes=64)
+                nc.vector.quantize_mx(out=codes[:].bitcast(FP8X4), scales=scales[:], in_=grouped[:])
+                return codes, scales
+
+            def biased_product(j, bt, codes, scales):
+                v = pre[j][bt]
+                sum_parts = stats.tile([P, CHUNKS], F32, tag="sum_parts")
+                for c in range(CHUNKS):
+                    quarter = c // CHUNKS_PER_QUARTER
+                    part = c % CHUNKS_PER_QUARTER
+                    acc = psum.tile([P, BANK], F32, tag="bank")
+                    for g in range(PASSES):
+                        nc.tensor.matmul_mx(
+                            out=acc[:],
+                            lhsT=codes[:, g * P : (g + 1) * P].bitcast(FP8X4),
+                            lhsT_scale=scales[:, g * P : (g + 1) * P],
+                            rhs=words[j][quarter][:, g, 2 * BANK * part : 2 * BANK * (part + 1)].bitcast(FP4X4),
+                            rhs_scale=planes[j][:, g, BANK * c : BANK * (c + 1)],
+                            start=(g == 0),
+                            stop=(g == PASSES - 1),
+                        )
+                    nc.vector.scalar_tensor_tensor(
+                        out=v[:, c * BANK : (c + 1) * BANK],
+                        in0=acc[:],
+                        scalar=1.0,
+                        in1=bias_rep[j][quarter][:, part * BANK : (part + 1) * BANK],
+                        op0=ALU.mult,
+                        op1=ALU.add,
+                        accum_out=sum_parts[:, c : c + 1],
+                    )
+                return v, sum_parts
+
+            def normalise(v, neg_mean, square_sum):
+                inv_std = inverse_deviation(square_sum, GATES)
+                left = v[:, :VECTOR_SHARE]
+                nc.vector.tensor_scalar(
+                    out=left, in0=left, scalar1=neg_mean[:], scalar2=inv_std[:], op0=ALU.add, op1=ALU.mult
+                )
+                neg_mean_over_std = stats.tile([P, 1], F32, tag="neg_mean_over_std")
+                nc.vector.tensor_mul(out=neg_mean_over_std[:], in0=neg_mean[:], in1=inv_std[:])
+                right = v[:, VECTOR_SHARE:]
+                nc.scalar.activation(
+                    out=right, in_=right, func=ACT.Identity, scale=inv_std[:], bias=neg_mean_over_std[:]
+                )
+
+            count = len(product_order)
+            with tc.manual_schedule():
+                grouped = {0: regroup_activation(*product_order[0]), 1: regroup_activation(*product_order[1])}
+                operands = {0: quantise_activation(grouped[0])}
+                unfinished = None
+                for i, (j, bt) in enumerate(product_order):
+                    v, sum_parts = biased_product(j, bt, *operands[i])
+                    neg_mean, square_sum = centred_squares(sum_parts[:], v[:], squares[:])
+                    if i + 1 < count:
+                        operands[i + 1] = quantise_activation(grouped[i + 1])
+                    if unfinished is not None:
+                        normalise(*unfinished)
+                    unfinished = (v, neg_mean, square_sum)
+                    if i + 2 < count:
+                        grouped[i + 2] = regroup_activation(*product_order[i + 2])
+                normalise(*unfinished)
+
+        with tc.tile_pool(name="gates", bufs=1) as gate_pool:
+            vector_cols = psum.tile([P, P], BF16, tag="bank")
+            nc.tensor.transpose(vector_cols[:], vector_rows[:], identity_bf16[:])
+            per_feature = gate_pool.tile([P, 4, FEATURE_TILES], F32, name="per_feature")
+            nc.vector.tensor_copy(out=per_feature[:].rearrange("p i f -> p (i f)"), in_=vector_cols[:])
+            gain_col = (per_feature[:, 0, :], per_feature[:, 1, :])
+            shift_col = gate_pool.tile([P, FEATURE_TILES], F32, name="shift_col")
+            nc.vector.tensor_add(out=shift_col[:], in0=per_feature[:, 2, :], in1=per_feature[:, 3, :])
+            forget_tiles = slice(FORGET_GATE, FORGET_GATE + HIDDEN_TILES)
+            nc.vector.tensor_scalar_add(
+                out=shift_col[:, forget_tiles], in0=shift_col[:, forget_tiles], scalar1=FORGET_GATE_BIAS
+            )
+            cell_squares = gate_pool.tile([P, HIDDEN], BF16, name="cell_squares")
+
+            def to_features(j, f):
+                flipped = psum.tile([P, BATCH_TILES, P], F32, tag="bank")
+                for bt in range(BATCH_TILES):
+                    nc.tensor.transpose(flipped[:, bt, :], pre[j][bt][:, f * P : (f + 1) * P], identity[:])
+                return flipped
+
+            def gate(f, func, result):
+                first = gate_pool.tile([P, BATCH_TILES, P], F32, tag="first", bufs=3)
+                nc.scalar.activation(
+                    out=first[:],
+                    in_=to_features(0, f)[:],
+                    func=ACT.Identity,
+                    scale=gain_col[0][:, f : f + 1],
+                    bias=shift_col[:, f : f + 1],
+                )
                 nc.vector.scalar_tensor_tensor(
-                    out=v[:, cols],
-                    in0=acc[:],
-                    scalar=1.0,
-                    in1=bias_rep[j][:, cols],
+                    out=result[:],
+                    in0=to_features(1, f)[:],
+                    scalar=gain_col[1][:, f : f + 1],
+                    in1=first[:],
                     op0=ALU.mult,
                     op1=ALU.add,
-                    accum_out=sum_parts[:, c : c + 1],
                 )
-            neg_mean, inv_std = row_statistics(sum_parts[:], v, GATES)
-            left = v[:, : GATES // 2]
-            nc.vector.tensor_scalar(
-                out=left, in0=left, scalar1=neg_mean[:], scalar2=inv_std[:], op0=ALU.add, op1=ALU.mult
-            )
-            neg_mean_over_std = stats.tile([P, 1], F32, tag="neg_mean_over_std")
-            nc.vector.tensor_mul(out=neg_mean_over_std[:], in0=neg_mean[:], in1=inv_std[:])
-            right = v[:, GATES // 2 :]
-            nc.scalar.activation(
-                out=right, in_=right, func=ACT.Identity, scale=inv_std[:], bias=neg_mean_over_std[:]
-            )
+                nc.scalar.activation(out=result[:], in_=result[:], func=func)
 
-        def to_features(j, grp, f):
-            flipped = psum.tile([P, GROUP_TILES, P], F32, tag="bank")
-            for t in range(GROUP_TILES):
-                nc.tensor.transpose(flipped[:, t, :], pre[j][grp][:, t, f * P : (f + 1) * P], identity[:])
-            return flipped
+            def gate_tiles(name):
+                return [gate_pool.tile([P, BATCH_TILES, P], F32, name="%s%d" % (name, h)) for h in range(HIDDEN_TILES)]
 
-        def gate(grp, f, func):
-            block = slice(f * P, (f + 1) * P)
-            first = pre[0][grp][:, :, block]
-            nc.scalar.activation(
-                out=first,
-                in_=to_features(0, grp, f)[:],
-                func=ACT.Identity,
-                scale=gain_col[0][:, f : f + 1],
-                bias=shift_col[:, f : f + 1],
-            )
-            result = pre[1][grp][:, :, block]
-            nc.vector.scalar_tensor_tensor(
-                out=result,
-                in0=to_features(1, grp, f)[:],
-                scalar=gain_col[1][:, f : f + 1],
-                in1=first,
-                op0=ALU.mult,
-                op1=ALU.add,
-            )
-            nc.scalar.activation(out=result, in_=result, func=func)
-            return result
+            forget = gate_tiles("forget")
+            fresh = gate_tiles("fresh")
+            out_gate = gate_tiles("out_gate")
 
-        def to_rows(grp, t, first_tile, bank):
-            back = psum.tile([P, BANK], F32, tag="bank")
-            for q in range(BLOCKS_PER_BANK):
-                f = first_tile + bank * BLOCKS_PER_BANK + q
-                nc.tensor.transpose(
-                    back[:, q * P : (q + 1) * P], pre[1][grp][:, t, f * P : (f + 1) * P], identity[:]
-                )
-            return back
+            def to_rows(tiles, bt, bank):
+                back = psum.tile([P, BANK], F32, tag="bank")
+                for q in range(BLOCKS_PER_BANK):
+                    nc.tensor.transpose(
+                        back[:, q * P : (q + 1) * P], tiles[bank * BLOCKS_PER_BANK + q][:, bt, :], identity[:]
+                    )
+                return back
 
-        def cell_gates(grp, h):
-            in_gate = gate(grp, IN_GATE + h, ACT.Sigmoid)
-            in_transform = gate(grp, IN_TRANSFORM + h, ACT.Tanh)
-            nc.vector.tensor_mul(out=in_gate, in0=in_gate, in1=in_transform)
-            gate(grp, FORGET_GATE + h, ACT.Sigmoid)
+            cell = [pre[0][bt][:, 0:HIDDEN] for bt in range(BATCH_TILES)]
+            hidden = [pre[0][bt][:, HIDDEN : 2 * HIDDEN] for bt in range(BATCH_TILES)]
 
-        def cell_of(grp, t):
-            return pre[0][grp][:, t, 0:HIDDEN]
-
-        def hidden_of(grp, t):
-            return pre[0][grp][:, t, HIDDEN : 2 * HIDDEN]
-
-        def batch_rows(grp, t):
-            bt = grp * GROUP_TILES + t
-            return slice(bt * P, (bt + 1) * P)
-
-        def new_cell(grp, t, bank, cell_sums):
-            cols = slice(bank * BANK, (bank + 1) * BANK)
-            cx_sb = stage.tile([P, BANK], BF16, tag="cx_sb", bufs=4)
-            nc.sync.dma_start(out=cx_sb[:], in_=cx[batch_rows(grp, t), cols])
-            cell = cell_of(grp, t)[:, cols]
-            nc.vector.tensor_mul(out=cell, in0=to_rows(grp, t, FORGET_GATE, bank)[:], in1=cx_sb[:])
-            nc.vector.scalar_tensor_tensor(
-                out=cell,
-                in0=to_rows(grp, t, IN_GATE, bank)[:],
-                scalar=1.0,
-                in1=cell,
-                op0=ALU.mult,
-                op1=ALU.add,
-                accum_out=cell_sums[:, bank : bank + 1],
-            )
-
-        def new_hidden(grp, t, neg_mean, inv_std):
-            hidden = hidden_of(grp, t)
-            nc.vector.scalar_tensor_tensor(
-                out=hidden, in0=cell_of(grp, t), scalar=neg_mean[:], in1=gain_out[:], op0=ALU.add, op1=ALU.mult
-            )
-            nc.vector.scalar_tensor_tensor(
-                out=hidden, in0=hidden, scalar=inv_std[:], in1=shift_out[:], op0=ALU.mult, op1=ALU.add
-            )
-            nc.scalar.activation(out=hidden, in_=hidden, func=ACT.Tanh)
-            for bank in range(HIDDEN // BANK):
+            def new_cell(bt, bank, cell_sums):
                 cols = slice(bank * BANK, (bank + 1) * BANK)
-                nc.vector.tensor_mul(
-                    out=hidden[:, cols], in0=to_rows(grp, t, OUT_GATE, bank)[:], in1=hidden[:, cols]
+                cx_sb = stage.tile([P, BANK], BF16, tag="cx_sb", bufs=4)
+                nc.sync.dma_start(out=cx_sb[:], in_=cx[bt * P : (bt + 1) * P, cols])
+                nc.vector.tensor_mul(out=cell[bt][:, cols], in0=to_rows(forget, bt, bank)[:], in1=cx_sb[:])
+                nc.vector.scalar_tensor_tensor(
+                    out=cell[bt][:, cols],
+                    in0=to_rows(fresh, bt, bank)[:],
+                    scalar=1.0,
+                    in1=cell[bt][:, cols],
+                    op0=ALU.mult,
+                    op1=ALU.add,
+                    accum_out=cell_sums[:, bank : bank + 1],
                 )
-            nc.sync.dma_start(out=out_0[batch_rows(grp, t), :], in_=hidden)
 
-        for j, bt in product_order:
-            normalised_product(j, bt)
+            def new_hidden(bt, neg_mean, inv_std):
+                nc.vector.scalar_tensor_tensor(
+                    out=hidden[bt], in0=cell[bt], scalar=neg_mean[:], in1=gain_out[:], op0=ALU.add, op1=ALU.mult
+                )
+                nc.vector.scalar_tensor_tensor(
+                    out=hidden[bt], in0=hidden[bt], scalar=inv_std[:], in1=shift_out[:], op0=ALU.mult, op1=ALU.add
+                )
+                nc.scalar.activation(out=hidden[bt], in_=hidden[bt], func=ACT.Tanh)
+                for bank in range(HIDDEN_BANKS):
+                    cols = slice(bank * BANK, (bank + 1) * BANK)
+                    nc.vector.tensor_mul(
+                        out=hidden[bt][:, cols], in0=to_rows(out_gate, bt, bank)[:], in1=hidden[bt][:, cols]
+                    )
+                nc.sync.dma_start(out=out_0[bt * P : (bt + 1) * P, :], in_=hidden[bt])
 
-        vector_cols = psum.tile([P, P], BF16, tag="bank")
-        nc.tensor.transpose(vector_cols[:], vector_rows[:], identity_bf16[:])
-        per_feature = keep.tile([P, 4, FEATURE_TILES], F32, name="per_feature")
-        nc.vector.tensor_copy(out=per_feature[:].rearrange("p i f -> p (i f)"), in_=vector_cols[:])
-        gain_col = (per_feature[:, 0, :], per_feature[:, 1, :])
-        shift_col = keep.tile([P, FEATURE_TILES], F32, name="shift_col")
-        nc.vector.tensor_add(out=shift_col[:], in0=per_feature[:, 2, :], in1=per_feature[:, 3, :])
-        forget_tiles = slice(FORGET_GATE, FORGET_GATE + HIDDEN_TILES)
-        nc.vector.tensor_scalar_add(
-            out=shift_col[:, forget_tiles], in0=shift_col[:, forget_tiles], scalar1=FORGET_GATE_BIAS
-        )
-
-        for grp in range(GROUPS):
-            tiles = range(GROUP_TILES)
-            cell_sums = [stats.tile([P, HIDDEN // BANK], F32, name="cell_sums%d" % t, tag="cell_sums") for t in tiles]
-            for bank in range(HIDDEN // BANK):
+            batch_tiles = range(BATCH_TILES)
+            cell_sums = [stats.tile([P, HIDDEN_BANKS], F32, name="cell_sums%d" % bt, tag="cell_sums") for bt in batch_tiles]
+            for bank in range(HIDDEN_BANKS):
                 for h in range(bank * BLOCKS_PER_BANK, (bank + 1) * BLOCKS_PER_BANK):
-                    cell_gates(grp, h)
-                for t in tiles:
-                    new_cell(grp, t, bank, cell_sums[t])
+                    gate(IN_GATE + h, ACT.Sigmoid, fresh[h])
+                    in_transform = gate_pool.tile([P, BATCH_TILES, P], F32, tag="in_transform", bufs=2)
+                    gate(IN_TRANSFORM + h, ACT.Tanh, in_transform)
+                    nc.vector.tensor_mul(out=fresh[h][:], in0=fresh[h][:], in1=in_transform[:])
+                    gate(FORGET_GATE + h, ACT.Sigmoid, forget[h])
+                for bt in batch_tiles:
+                    new_cell(bt, bank, cell_sums[bt])
             cell_stats = []
-            for t in tiles:
-                nc.sync.dma_start(out=out_1[batch_rows(grp, t), :], in_=cell_of(grp, t))
-                cell_stats.append(row_statistics(cell_sums[t][:], cell_of(grp, t), HIDDEN))
+            for bt in batch_tiles:
+                nc.sync.dma_start(out=out_1[bt * P : (bt + 1) * P, :], in_=cell[bt])
+                cell_stats.append(centred_squares(cell_sums[bt][:], cell[bt], cell_squares[:]))
             for h in range(HIDDEN_TILES):
-                gate(grp, OUT_GATE + h, ACT.Sigmoid)
-            for t in tiles:
-                new_hidden(grp, t, *cell_stats[t])
+                gate(OUT_GATE + h, ACT.Sigmoid, out_gate[h])
+            for bt in batch_tiles:
+                new_hidden(bt, cell_stats[bt][0], inverse_deviation(cell_stats[bt][1], HIDDEN))

@@ -36,7 +36,6 @@ IN_GATE = 0 * HIDDEN_TILES
 FORGET_GATE = 1 * HIDDEN_TILES
 OUT_GATE = 2 * HIDDEN_TILES
 IN_TRANSFORM = 3 * HIDDEN_TILES
-VECTOR_SHARE = 5 * GATES // 8
 FORGET_GATE_BIAS = -1.0
 EPS = 1e-5
 
@@ -82,6 +81,8 @@ def tile_layernormlstmcell_kernel(
         make_identity(nc, identity_bf16[:])
         half = keep.tile([P, 1], F32, name="half")
         nc.gpsimd.memset(half[:], 0.5)
+        minus_one = keep.tile([P, 1], F32, name="minus_one")
+        nc.gpsimd.memset(minus_one[:], -1.0)
 
         pre = [[keep.tile([P, GATES], F32, name="pre%d_%d" % (j, bt)) for bt in range(BATCH_TILES)] for j in range(2)]
         vector_rows = keep.tile([P, P], BF16, name="vector_rows")
@@ -214,35 +215,68 @@ def tile_layernormlstmcell_kernel(
                     )
                 return v, sum_parts
 
-            def normalise(v, neg_mean, square_sum):
-                inv_std = inverse_deviation(square_sum, GATES)
-                left = v[:, :VECTOR_SHARE]
-                nc.vector.tensor_scalar(
-                    out=left, in0=left, scalar1=neg_mean[:], scalar2=inv_std[:], op0=ALU.add, op1=ALU.mult
-                )
-                neg_mean_over_std = stats.tile([P, 1], F32, tag="neg_mean_over_std")
-                nc.vector.tensor_mul(out=neg_mean_over_std[:], in0=neg_mean[:], in1=inv_std[:])
-                right = v[:, VECTOR_SHARE:]
+            def product_squares(sum_parts, v):
+                scaled_parts = stats.tile([P, CHUNKS], F32, tag="scaled_parts")
+                neg_mean = stats.tile([P, 1], F32, tag="neg_mean")
                 nc.scalar.activation(
-                    out=right, in_=right, func=ACT.Identity, scale=inv_std[:], bias=neg_mean_over_std[:]
+                    out=scaled_parts[:], in_=sum_parts[:], func=ACT.Identity, scale=-1.0 / GATES, accum_out=neg_mean[:]
+                )
+                square_sum = stats.tile([P, 1], F32, tag="square_sum")
+                nc.scalar.activation(
+                    out=squares[:], in_=v[:], func=ACT.Square, bias=neg_mean[:], accum_out=square_sum[:]
+                )
+                return neg_mean, square_sum
+
+            def deviation(neg_mean, square_sum):
+                root = stats.tile([P, 1], F32, tag="root")
+                nc.gpsimd.tensor_tensor(out=root[:], in0=square_sum[:], in1=half[:], op=ALU.pow)
+                std_eps = stats.tile([P, 1], F32, tag="std_eps")
+                nc.gpsimd.tensor_scalar(
+                    out=std_eps[:], in0=root[:], scalar1=1.0 / math.sqrt(GATES - 1), scalar2=EPS,
+                    op0=ALU.mult, op1=ALU.add,
+                )
+                inv_std = stats.tile([P, 1], F32, tag="inv_std")
+                nc.gpsimd.tensor_tensor(out=inv_std[:], in0=std_eps[:], in1=minus_one[:], op=ALU.pow)
+                neg_mean_over_std = stats.tile([P, 1], F32, tag="neg_mean_over_std")
+                nc.gpsimd.tensor_tensor(out=neg_mean_over_std[:], in0=neg_mean[:], in1=inv_std[:], op=ALU.mult)
+                return inv_std, neg_mean_over_std
+
+            def gate_columns(v, first_tile):
+                return v[:, first_tile * P : first_tile * P + HIDDEN]
+
+            def normalise_on(engine, v, first_tile, inv_std, neg_mean_over_std):
+                piece = gate_columns(v, first_tile)
+                engine.tensor_scalar(
+                    out=piece, in0=piece, scalar1=inv_std[:], scalar2=neg_mean_over_std[:],
+                    op0=ALU.mult, op1=ALU.add,
+                )
+
+            def normalise_on_scalar(v, first_tile, inv_std, neg_mean_over_std):
+                piece = gate_columns(v, first_tile)
+                nc.scalar.activation(
+                    out=piece, in_=piece, func=ACT.Identity, scale=inv_std[:], bias=neg_mean_over_std[:]
                 )
 
             count = len(product_order)
             with tc.manual_schedule():
                 grouped = {0: regroup_activation(*product_order[0]), 1: regroup_activation(*product_order[1])}
                 operands = {0: quantise_activation(grouped[0])}
-                unfinished = None
+                scalar_part = None
                 for i, (j, bt) in enumerate(product_order):
                     v, sum_parts = biased_product(j, bt, *operands[i])
-                    neg_mean, square_sum = centred_squares(sum_parts[:], v[:], squares[:])
+                    neg_mean, square_sum = product_squares(sum_parts, v)
                     if i + 1 < count:
                         operands[i + 1] = quantise_activation(grouped[i + 1])
-                    if unfinished is not None:
-                        normalise(*unfinished)
-                    unfinished = (v, neg_mean, square_sum)
+                    if scalar_part is not None:
+                        normalise_on_scalar(*scalar_part)
+                    factors = deviation(neg_mean, square_sum)
+                    scalar_part = (v, IN_GATE) + factors
+                    engine = nc.gpsimd if i + 1 < count else nc.vector
+                    for first_tile in (IN_TRANSFORM, FORGET_GATE, OUT_GATE):
+                        normalise_on(engine, v, first_tile, *factors)
                     if i + 2 < count:
                         grouped[i + 2] = regroup_activation(*product_order[i + 2])
-                normalise(*unfinished)
+                normalise_on_scalar(*scalar_part)
 
         with tc.tile_pool(name="gates", bufs=1) as gate_pool:
             vector_cols = psum.tile([P, P], BF16, tag="bank")

@@ -36,8 +36,15 @@ IN_GATE = 0 * HIDDEN_TILES
 FORGET_GATE = 1 * HIDDEN_TILES
 OUT_GATE = 2 * HIDDEN_TILES
 IN_TRANSFORM = 3 * HIDDEN_TILES
+GATE_ORDER = (IN_GATE, IN_TRANSFORM, FORGET_GATE, OUT_GATE)
 FORGET_GATE_BIAS = -1.0
 EPS = 1e-5
+PAIR = 2
+LEAD = 8
+HELD_BACK = 3
+PAUSE = 3
+VECTOR_EVERY = 3
+PREPARE_AT = 3
 
 FLOPS = 2 * 2 * BATCH * K * GATES
 
@@ -67,51 +74,126 @@ def tile_layernormlstmcell_kernel(
     w_words = (w_i2h_words, w_h2h_words)
     w_scales = (w_i2h_scales, w_h2h_scales)
     biases = (b_i2h, b_h2h)
-    product_order = [(j, bt) for j in range(2) for bt in range(BATCH_TILES)]
+    batch_tiles = range(BATCH_TILES)
 
     with ExitStack() as ctx:
+        ctx.enter_context(tc.manual_schedule())
         keep = ctx.enter_context(tc.tile_pool(name="keep", bufs=1))
         stage = ctx.enter_context(tc.tile_pool(name="stage", bufs=2))
-        stats = ctx.enter_context(tc.tile_pool(name="stats", bufs=4))
-        psum = ctx.enter_context(tc.psum_pool(name="psum", bufs=8))
+        psum = ctx.enter_context(tc.psum_pool(name="psum", bufs=6))
 
         identity = keep.tile([P, P], F32, name="identity")
         make_identity(nc, identity[:])
         identity_bf16 = keep.tile([P, P], BF16, name="identity_bf16")
         make_identity(nc, identity_bf16[:])
-        half = keep.tile([P, 1], F32, name="half")
+        half = keep.tile([P, BATCH_TILES], F32, name="half")
         nc.gpsimd.memset(half[:], 0.5)
-        minus_one = keep.tile([P, 1], F32, name="minus_one")
+        minus_one = keep.tile([P, BATCH_TILES], F32, name="minus_one")
         nc.gpsimd.memset(minus_one[:], -1.0)
 
-        pre = [[keep.tile([P, GATES], F32, name="pre%d_%d" % (j, bt)) for bt in range(BATCH_TILES)] for j in range(2)]
+        pre = [[keep.tile([P, GATES], F32, name="pre%d_%d" % (j, bt)) for bt in batch_tiles] for j in range(2)]
+        cx_sb = [keep.tile([P, HIDDEN], BF16, name="cx_sb%d" % bt) for bt in batch_tiles]
         vector_rows = keep.tile([P, P], BF16, name="vector_rows")
-        gain_out = keep.tile([P, HIDDEN], BF16, name="gain_out")
-        shift_out = keep.tile([P, HIDDEN], BF16, name="shift_out")
+        out_rows = keep.tile([P, P], BF16, name="out_rows")
+        nc.gpsimd.memset(out_rows[:], 0.0)
+        per_feature = keep.tile([P, 4, FEATURE_TILES], F32, name="per_feature")
+        shift_col = keep.tile([P, FEATURE_TILES], F32, name="shift_col")
+        out_feature = keep.tile([P, 2, HIDDEN_TILES], F32, name="out_feature")
 
-        def centred_squares(sum_parts, values, squares):
-            width = values.shape[1]
-            total = stats.tile([P, 1], F32, tag="total")
-            nc.vector.reduce_sum(out=total[:], in_=sum_parts, axis=AXIS.X)
-            neg_mean = stats.tile([P, 1], F32, tag="neg_mean")
-            nc.vector.tensor_scalar_mul(out=neg_mean[:], in0=total[:], scalar1=-1.0 / width)
-            square_sum = stats.tile([P, 1], F32, tag="square_sum")
+        def columns(name, width):
+            return keep.tile([P, width], F32, name=name)
+
+        def new_statistics(name, width, chunks, length):
+            return {
+                "width": width,
+                "chunks": chunks,
+                "length": length,
+                "spread": math.sqrt(length / chunks),
+                "sums": keep.tile([P, width, chunks], F32, name=name + "_sums"),
+                "square_sums": keep.tile([P, width, chunks], F32, name=name + "_square_sums"),
+                "neg_pivot": columns(name + "_neg_pivot", width),
+                "spread_neg_pivot": columns(name + "_spread_neg_pivot", width),
+                "neg_mean": columns(name + "_neg_mean", width),
+                "offset_term": columns(name + "_offset_term", width),
+                "neg_centred": columns(name + "_neg_centred", width),
+                "centred": columns(name + "_centred", width),
+                "root": columns(name + "_root", width),
+                "std_eps": columns(name + "_std_eps", width),
+                "inv_std": columns(name + "_inv_std", width),
+                "neg_mean_over_std": columns(name + "_neg_mean_over_std", width),
+            }
+
+        def column(st, key, i):
+            return st[key][:, i : i + 1]
+
+        def pivot(st, i):
+            chunk_length = st["length"] // st["chunks"]
+            first_sum = st["sums"][:, i, 0:1]
+            nc.scalar.activation(out=column(st, "neg_pivot", i), in_=first_sum, func=ACT.Identity, scale=-1.0 / chunk_length)
             nc.scalar.activation(
-                out=squares, in_=values, func=ACT.Square, bias=neg_mean[:], accum_out=square_sum[:]
+                out=column(st, "spread_neg_pivot", i), in_=first_sum, func=ACT.Identity, scale=-st["spread"] / chunk_length
             )
-            return neg_mean, square_sum
 
-        def inverse_deviation(square_sum, width):
-            root = stats.tile([P, 1], F32, tag="root")
-            nc.gpsimd.tensor_tensor(out=root[:], in0=square_sum[:], in1=half[:], op=ALU.pow)
-            std_eps = stats.tile([P, 1], F32, tag="std_eps")
-            nc.vector.tensor_scalar(
-                out=std_eps[:], in0=root[:], scalar1=1.0 / math.sqrt(width - 1), scalar2=EPS,
+        def squares_about_pivot(st, i, c, values):
+            unread = stage.tile([P, BANK], BF16, tag="unread_squares")
+            nc.scalar.activation(
+                out=unread[:], in_=values, func=ACT.Square, bias=column(st, "neg_pivot", i),
+                accum_out=st["square_sums"][:, i, c : c + 1],
+            )
+
+        def mean_of(st, i):
+            unread = stage.tile([P, CHUNKS], F32, tag="unread_columns")
+            nc.scalar.activation(
+                out=unread[:, 0 : st["chunks"]], in_=st["sums"][:, i, :], func=ACT.Identity, scale=-1.0 / st["length"],
+                accum_out=column(st, "neg_mean", i),
+            )
+            nc.scalar.activation(
+                out=column(st, "offset_term", i), in_=column(st, "neg_mean", i), func=ACT.Square,
+                scale=-st["spread"], bias=column(st, "spread_neg_pivot", i),
+            )
+
+        def centred_of(st, i):
+            unread = stage.tile([P, CHUNKS], F32, tag="unread_columns")
+            nc.scalar.activation(
+                out=unread[:, 0 : st["chunks"]], in_=st["square_sums"][:, i, :], func=ACT.Identity, scale=-1.0,
+                bias=column(st, "offset_term", i), accum_out=column(st, "neg_centred", i),
+            )
+
+        def deviation_of(st):
+            width = st["width"]
+            nc.gpsimd.tensor_scalar(
+                out=st["centred"][:], in0=st["neg_centred"][:], scalar1=-1.0, scalar2=0.0, op0=ALU.mult, op1=ALU.max
+            )
+            nc.gpsimd.tensor_tensor(out=st["root"][:], in0=st["centred"][:], in1=half[:, 0:width], op=ALU.pow)
+            nc.gpsimd.tensor_scalar(
+                out=st["std_eps"][:], in0=st["root"][:], scalar1=1.0 / math.sqrt(st["length"] - 1), scalar2=EPS,
                 op0=ALU.mult, op1=ALU.add,
             )
-            inv_std = stats.tile([P, 1], F32, tag="inv_std")
-            nc.vector.reciprocal(out=inv_std[:], in_=std_eps[:])
-            return inv_std
+            nc.gpsimd.tensor_tensor(out=st["inv_std"][:], in0=st["std_eps"][:], in1=minus_one[:, 0:width], op=ALU.pow)
+            nc.gpsimd.tensor_tensor(
+                out=st["neg_mean_over_std"][:], in0=st["neg_mean"][:], in1=st["inv_std"][:], op=ALU.mult
+            )
+
+        def normalise(engine, out, in_, st, i):
+            scale, shift = column(st, "inv_std", i), column(st, "neg_mean_over_std", i)
+            if engine == "scalar":
+                nc.scalar.activation(out=out, in_=in_, func=ACT.Identity, scale=scale, bias=shift)
+            elif engine == "vector":
+                nc.vector.tensor_scalar(out=out, in0=in_, scalar1=scale, scalar2=shift, op0=ALU.mult, op1=ALU.add)
+            else:
+                nc.gpsimd.tensor_scalar(out=out, in0=in_, scalar1=scale, scalar2=shift, op0=ALU.mult, op1=ALU.add)
+
+        def gate_columns(j, bt, first_tile):
+            return pre[j][bt][:, first_tile * P : first_tile * P + HIDDEN]
+
+        groups = [(j, first) for j in range(2) for first in range(0, BATCH_TILES, PAIR)]
+        statistics = {group: new_statistics("pre%d_%d" % group, PAIR, CHUNKS, GATES) for group in groups}
+
+        def normalise_group(engines, group, first_tile):
+            j, first = group
+            for i, engine in enumerate(engines):
+                piece = gate_columns(j, first + i, first_tile)
+                normalise(engine, piece, piece, statistics[group], i)
 
         with tc.tile_pool(name="weights", bufs=1) as weights:
             planes = []
@@ -127,46 +209,72 @@ def tile_layernormlstmcell_kernel(
                 [weights.tile([P, QUARTER], BF16, name="bias_rep%d_%d" % (j, c)) for c in range(QUARTERS)]
                 for j in range(2)
             ]
-            squares = weights.tile([P, GATES], BF16, name="squares")
+            codes = [
+                [weights.tile([P, PASSES * P], U32, name="codes%d_%d" % (j, bt), align_bytes=64) for bt in batch_tiles]
+                for j in range(2)
+            ]
+            code_scales = [
+                [weights.tile([P, PASSES * P], U8, name="code_scales%d_%d" % (j, bt), align_bytes=64) for bt in batch_tiles]
+                for j in range(2)
+            ]
+
+            x_tiles = {}
 
             def load_activation(j, bt):
-                x_sb = stage.tile([P, K], BF16, tag="x_sb", bufs=3)
+                x_sb = stage.tile([P, K], BF16, tag="x_sb", bufs=4)
                 nc.sync.dma_start(out=x_sb[:], in_=acts[j][bt * P : (bt + 1) * P, :])
-                return x_sb
+                x_tiles[(j, bt)] = x_sb
 
-            def load_weight(j):
+            def load_scales(j):
                 scale_rows = w_scales[j].bitcast(I32).rearrange("g (q r) n -> r q g n", r=4)
                 for r in range(4):
                     nc.sync.dma_start(out=planes[j][r:P:32, :, :].bitcast(I32), in_=scale_rows[r])
-                for c in range(QUARTERS):
+
+            def load_quarter(j, c):
+                nc.sync.dma_start(
+                    out=words[j][c][:].bitcast(I32),
+                    in_=w_words[j][:, :, 2 * c * QUARTER : 2 * (c + 1) * QUARTER].bitcast(I32).rearrange("g p n -> p g n"),
+                )
+                nc.sync.dma_start(
+                    out=bias_rep[j][c][:], in_=biases[j][c * QUARTER : (c + 1) * QUARTER].partition_broadcast(P)
+                )
+
+            def load_rows(rows, vectors, count):
+                for i, vector in enumerate(vectors):
                     nc.sync.dma_start(
-                        out=words[j][c][:].bitcast(I32),
-                        in_=w_words[j][:, :, 2 * c * QUARTER : 2 * (c + 1) * QUARTER].bitcast(I32).rearrange("g p n -> p g n"),
-                    )
-                    nc.sync.dma_start(
-                        out=bias_rep[j][c][:], in_=biases[j][c * QUARTER : (c + 1) * QUARTER].partition_broadcast(P)
+                        out=rows[i * count : (i + 1) * count, :], in_=vector.rearrange("o (f p) -> (o f) p", p=P)
                     )
 
-            x_tiles = {}
-            with tc.manual_schedule():
-                x_tiles[product_order[0]] = load_activation(*product_order[0])
-                x_tiles[product_order[1]] = load_activation(*product_order[1])
-                load_weight(0)
-                x_tiles[product_order[2]] = load_activation(*product_order[2])
-                load_weight(1)
-                for i, vector in enumerate((ln_i2h_w, ln_h2h_w, ln_i2h_b, ln_h2h_b)):
-                    nc.sync.dma_start(
-                        out=vector_rows[i * FEATURE_TILES : (i + 1) * FEATURE_TILES, :],
-                        in_=vector.rearrange("o (f p) -> (o f) p", p=P),
-                    )
-                nc.sync.dma_start(out=gain_out[:], in_=ln_h2o_w.rearrange("o n -> (o n)").partition_broadcast(P))
-                nc.sync.dma_start(out=shift_out[:], in_=ln_h2o_b.rearrange("o n -> (o n)").partition_broadcast(P))
+            load_activation(0, 0)
+            load_activation(0, 1)
+            load_scales(0)
+            load_quarter(0, 0)
+            load_quarter(0, 1)
+            load_activation(0, 2)
+            load_activation(0, 3)
+            load_quarter(0, 2)
+            load_quarter(0, 3)
+
+            def late_loads():
+                for bt in range(PAIR):
+                    load_activation(1, bt)
+                load_rows(vector_rows, (ln_i2h_w, ln_h2h_w, ln_i2h_b, ln_h2h_b), FEATURE_TILES)
+                load_rows(out_rows, (ln_h2o_w, ln_h2o_b), HIDDEN_TILES)
+                load_scales(1)
+                for c in range(QUARTERS):
+                    load_quarter(1, c)
+
+            def last_loads():
+                for bt in range(PAIR, BATCH_TILES):
+                    load_activation(1, bt)
+                for bt in batch_tiles:
+                    nc.sync.dma_start(out=cx_sb[bt][:], in_=cx[bt * P : (bt + 1) * P, :])
+
+            grouped_tiles = {}
 
             def regroup_activation(j, bt):
-                if (j, bt) not in x_tiles:
-                    x_tiles[(j, bt)] = load_activation(j, bt)
                 x_words = x_tiles[(j, bt)][:].bitcast(F32)
-                flipped = psum.tile([P, PASSES * 2, P], F32, tag="bank")
+                flipped = psum.tile([P, PASSES * 2, P], F32, tag="flip", bufs=2)
                 for g in range(PASSES):
                     for u in range(2):
                         nc.tensor.transpose(
@@ -179,143 +287,95 @@ def tile_layernormlstmcell_kernel(
                     out=grouped[:].bitcast(F32).rearrange("p (g b u) -> p g b u", g=PASSES, u=2),
                     in_=flipped[:].rearrange("p (g u) b -> p g b u", u=2),
                 )
-                return grouped
+                grouped_tiles[(j, bt)] = grouped
 
-            def quantise_activation(grouped):
-                codes = stage.tile([P, PASSES * P], U32, tag="codes", align_bytes=64)
-                scales = stage.tile([P, PASSES * P], U8, tag="scales", align_bytes=64)
-                nc.vector.quantize_mx(out=codes[:].bitcast(FP8X4), scales=scales[:], in_=grouped[:])
-                return codes, scales
+            def quantise_activation(j, bt):
+                nc.vector.quantize_mx(
+                    out=codes[j][bt][:].bitcast(FP8X4), scales=code_scales[j][bt][:], in_=grouped_tiles[(j, bt)][:]
+                )
 
-            def biased_product(j, bt, codes, scales):
-                v = pre[j][bt]
-                sum_parts = stats.tile([P, CHUNKS], F32, tag="sum_parts")
-                for c in range(CHUNKS):
-                    quarter = c // CHUNKS_PER_QUARTER
-                    part = c % CHUNKS_PER_QUARTER
-                    acc = psum.tile([P, BANK], F32, tag="bank")
-                    for g in range(PASSES):
-                        nc.tensor.matmul_mx(
-                            out=acc[:],
-                            lhsT=codes[:, g * P : (g + 1) * P].bitcast(FP8X4),
-                            lhsT_scale=scales[:, g * P : (g + 1) * P],
-                            rhs=words[j][quarter][:, g, 2 * BANK * part : 2 * BANK * (part + 1)].bitcast(FP4X4),
-                            rhs_scale=planes[j][:, g, BANK * c : BANK * (c + 1)],
-                            start=(g == 0),
-                            stop=(g == PASSES - 1),
-                        )
-                    nc.vector.scalar_tensor_tensor(
-                        out=v[:, c * BANK : (c + 1) * BANK],
-                        in0=acc[:],
-                        scalar=1.0,
-                        in1=bias_rep[j][quarter][:, part * BANK : (part + 1) * BANK],
-                        op0=ALU.mult,
-                        op1=ALU.add,
-                        accum_out=sum_parts[:, c : c + 1],
+            def chunk_columns(c):
+                return slice(c * BANK, (c + 1) * BANK)
+
+            def chunk_product(j, bt, c):
+                quarter = c // CHUNKS_PER_QUARTER
+                part = c % CHUNKS_PER_QUARTER
+                acc = psum.tile([P, BANK], F32, tag="acc")
+                for g in range(PASSES):
+                    nc.tensor.matmul_mx(
+                        out=acc[:],
+                        lhsT=codes[j][bt][:, g * P : (g + 1) * P].bitcast(FP8X4),
+                        lhsT_scale=code_scales[j][bt][:, g * P : (g + 1) * P],
+                        rhs=words[j][quarter][:, g, 2 * BANK * part : 2 * BANK * (part + 1)].bitcast(FP4X4),
+                        rhs_scale=planes[j][:, g, BANK * c : BANK * (c + 1)],
+                        start=(g == 0),
+                        stop=(g == PASSES - 1),
                     )
-                return v, sum_parts
-
-            def product_squares(sum_parts, v):
-                scaled_parts = stats.tile([P, CHUNKS], F32, tag="scaled_parts")
-                neg_mean = stats.tile([P, 1], F32, tag="neg_mean")
-                nc.scalar.activation(
-                    out=scaled_parts[:], in_=sum_parts[:], func=ACT.Identity, scale=-1.0 / GATES, accum_out=neg_mean[:]
-                )
-                square_sum = stats.tile([P, 1], F32, tag="square_sum")
-                nc.scalar.activation(
-                    out=squares[:], in_=v[:], func=ACT.Square, bias=neg_mean[:], accum_out=square_sum[:]
-                )
-                return neg_mean, square_sum
-
-            def deviation(neg_mean, square_sum):
-                root = stats.tile([P, 1], F32, tag="root")
-                nc.gpsimd.tensor_tensor(out=root[:], in0=square_sum[:], in1=half[:], op=ALU.pow)
-                std_eps = stats.tile([P, 1], F32, tag="std_eps")
-                nc.gpsimd.tensor_scalar(
-                    out=std_eps[:], in0=root[:], scalar1=1.0 / math.sqrt(GATES - 1), scalar2=EPS,
-                    op0=ALU.mult, op1=ALU.add,
-                )
-                inv_std = stats.tile([P, 1], F32, tag="inv_std")
-                nc.gpsimd.tensor_tensor(out=inv_std[:], in0=std_eps[:], in1=minus_one[:], op=ALU.pow)
-                neg_mean_over_std = stats.tile([P, 1], F32, tag="neg_mean_over_std")
-                nc.gpsimd.tensor_tensor(out=neg_mean_over_std[:], in0=neg_mean[:], in1=inv_std[:], op=ALU.mult)
-                return inv_std, neg_mean_over_std
-
-            def gate_columns(v, first_tile):
-                return v[:, first_tile * P : first_tile * P + HIDDEN]
-
-            def normalise_on(engine, v, first_tile, inv_std, neg_mean_over_std):
-                piece = gate_columns(v, first_tile)
-                engine.tensor_scalar(
-                    out=piece, in0=piece, scalar1=inv_std[:], scalar2=neg_mean_over_std[:],
-                    op0=ALU.mult, op1=ALU.add,
-                )
-
-            def normalise_on_scalar(v, first_tile, inv_std, neg_mean_over_std):
-                piece = gate_columns(v, first_tile)
-                nc.scalar.activation(
-                    out=piece, in_=piece, func=ACT.Identity, scale=inv_std[:], bias=neg_mean_over_std[:]
-                )
-
-            count = len(product_order)
-            with tc.manual_schedule():
-                grouped = {0: regroup_activation(*product_order[0]), 1: regroup_activation(*product_order[1])}
-                operands = {0: quantise_activation(grouped[0])}
-                scalar_part = None
-                for i, (j, bt) in enumerate(product_order):
-                    v, sum_parts = biased_product(j, bt, *operands[i])
-                    neg_mean, square_sum = product_squares(sum_parts, v)
-                    if i + 1 < count:
-                        operands[i + 1] = quantise_activation(grouped[i + 1])
-                    if scalar_part is not None:
-                        normalise_on_scalar(*scalar_part)
-                    factors = deviation(neg_mean, square_sum)
-                    scalar_part = (v, IN_GATE) + factors
-                    engine = nc.gpsimd if i + 1 < count else nc.vector
-                    for first_tile in (IN_TRANSFORM, FORGET_GATE, OUT_GATE):
-                        normalise_on(engine, v, first_tile, *factors)
-                    if i + 2 < count:
-                        grouped[i + 2] = regroup_activation(*product_order[i + 2])
-                normalise_on_scalar(*scalar_part)
-
-        with tc.tile_pool(name="gates", bufs=1) as gate_pool:
-            vector_cols = psum.tile([P, P], BF16, tag="bank")
-            nc.tensor.transpose(vector_cols[:], vector_rows[:], identity_bf16[:])
-            per_feature = gate_pool.tile([P, 4, FEATURE_TILES], F32, name="per_feature")
-            nc.vector.tensor_copy(out=per_feature[:].rearrange("p i f -> p (i f)"), in_=vector_cols[:])
-            gain_col = (per_feature[:, 0, :], per_feature[:, 1, :])
-            shift_col = gate_pool.tile([P, FEATURE_TILES], F32, name="shift_col")
-            nc.vector.tensor_add(out=shift_col[:], in0=per_feature[:, 2, :], in1=per_feature[:, 3, :])
-            forget_tiles = slice(FORGET_GATE, FORGET_GATE + HIDDEN_TILES)
-            nc.vector.tensor_scalar_add(
-                out=shift_col[:, forget_tiles], in0=shift_col[:, forget_tiles], scalar1=FORGET_GATE_BIAS
-            )
-            cell_squares = gate_pool.tile([P, HIDDEN], BF16, name="cell_squares")
-
-            def to_features(j, f):
-                flipped = psum.tile([P, BATCH_TILES, P], F32, tag="bank")
-                for bt in range(BATCH_TILES):
-                    nc.tensor.transpose(flipped[:, bt, :], pre[j][bt][:, f * P : (f + 1) * P], identity[:])
-                return flipped
-
-            def gate(f, func, result):
-                first = gate_pool.tile([P, BATCH_TILES, P], F32, tag="first", bufs=3)
-                nc.scalar.activation(
-                    out=first[:],
-                    in_=to_features(0, f)[:],
-                    func=ACT.Identity,
-                    scale=gain_col[0][:, f : f + 1],
-                    bias=shift_col[:, f : f + 1],
-                )
                 nc.vector.scalar_tensor_tensor(
-                    out=result[:],
-                    in0=to_features(1, f)[:],
-                    scalar=gain_col[1][:, f : f + 1],
-                    in1=first[:],
+                    out=pre[j][bt][:, chunk_columns(c)],
+                    in0=acc[:],
+                    scalar=1.0,
+                    in1=bias_rep[j][quarter][:, part * BANK : (part + 1) * BANK],
                     op0=ALU.mult,
                     op1=ALU.add,
+                    accum_out=statistics[(j, bt - bt % PAIR)]["sums"][:, bt % PAIR, c : c + 1],
                 )
-                nc.scalar.activation(out=result[:], in_=result[:], func=func)
+
+            def chunk_squares(j, bt, c):
+                squares_about_pivot(statistics[(j, bt - bt % PAIR)], bt % PAIR, c, pre[j][bt][:, chunk_columns(c)])
+
+            def feature_vectors():
+                vector_cols = psum.tile([P, P], BF16, tag="flip", bufs=2)
+                nc.tensor.transpose(vector_cols[:], vector_rows[:], identity_bf16[:])
+                nc.scalar.copy(out=per_feature[:].rearrange("p i f -> p (i f)"), in_=vector_cols[:])
+                nc.gpsimd.tensor_tensor(out=shift_col[:], in0=per_feature[:, 2, :], in1=per_feature[:, 3, :], op=ALU.add)
+                forget_tiles = slice(FORGET_GATE, FORGET_GATE + HIDDEN_TILES)
+                nc.gpsimd.tensor_scalar(
+                    out=shift_col[:, forget_tiles], in0=shift_col[:, forget_tiles], scalar1=1.0, scalar2=FORGET_GATE_BIAS,
+                    op0=ALU.mult, op1=ALU.add,
+                )
+                out_cols = psum.tile([P, P], BF16, tag="flip", bufs=2)
+                nc.tensor.transpose(out_cols[:], out_rows[:], identity_bf16[:])
+                nc.scalar.copy(out=out_feature[:].rearrange("p i f -> p (i f)"), in_=out_cols[:, 0 : 2 * HIDDEN_TILES])
+
+            for i in range(PAIR):
+                regroup_activation(0, i)
+                quantise_activation(0, i)
+            for number, group in enumerate(groups):
+                j, first = group
+                st = statistics[group]
+                for c in range(CHUNKS):
+                    for i in range(PAIR):
+                        chunk_product(j, first + i, c)
+                        if c > 0:
+                            chunk_squares(j, first + i, c)
+                    if c == 0:
+                        for i in range(PAIR):
+                            pivot(st, i)
+                            chunk_squares(j, first + i, 0)
+                    if number == 0 and c == 0:
+                        late_loads()
+                    if number == 0 and c == PREPARE_AT + PAIR:
+                        last_loads()
+                    if number + 1 < len(groups) and PREPARE_AT <= c < PREPARE_AT + PAIR:
+                        regroup_activation(groups[number + 1][0], groups[number + 1][1] + c - PREPARE_AT)
+                    if number + 1 < len(groups) and PREPARE_AT + 1 <= c < PREPARE_AT + 1 + PAIR:
+                        quantise_activation(groups[number + 1][0], groups[number + 1][1] + c - PREPARE_AT - 1)
+                    if number == 1 and c == CHUNKS - 1:
+                        feature_vectors()
+                    if c == CHUNKS - 1:
+                        for i in range(PAIR):
+                            mean_of(st, i)
+                            centred_of(st, i)
+                        if number + 1 < len(groups):
+                            deviation_of(st)
+                            wanted = GATE_ORDER if number + 2 < len(groups) else GATE_ORDER[:2]
+                            for first_tile in wanted:
+                                normalise_group(("gpsimd",) * PAIR, group, first_tile)
+
+
+        with tc.tile_pool(name="gates", bufs=1) as gate_pool:
+            gain_col = (per_feature[:, 0, :], per_feature[:, 1, :])
 
             def gate_tiles(name):
                 return [gate_pool.tile([P, BATCH_TILES, P], F32, name="%s%d" % (name, h)) for h in range(HIDDEN_TILES)]
@@ -324,63 +384,198 @@ def tile_layernormlstmcell_kernel(
             fresh = gate_tiles("fresh")
             out_gate = gate_tiles("out_gate")
 
-            def to_rows(tiles, bt, bank):
-                back = psum.tile([P, BANK], F32, tag="bank")
+            sequence = [(first_tile, h) for first_tile in GATE_ORDER for h in range(HIDDEN_TILES)]
+            count = len(sequence)
+            flipped = ({}, {})
+            first_part = {}
+            result = {}
+
+            def to_features(j, t):
+                f = sequence[t][0] + sequence[t][1]
+                bank = psum.tile([P, BATCH_TILES, P], F32, tag="acc")
+                for bt in batch_tiles:
+                    nc.tensor.transpose(bank[:, bt, :], pre[j][bt][:, f * P : (f + 1) * P], identity[:])
+                flipped[j][t] = bank
+
+            def first_product_part(t, on_vector):
+                f = sequence[t][0] + sequence[t][1]
+                part = gate_pool.tile([P, BATCH_TILES, P], F32, tag="first_part", bufs=LEAD + 1)
+                if on_vector:
+                    nc.vector.tensor_scalar(
+                        out=part[:], in0=flipped[0][t][:], scalar1=gain_col[0][:, f : f + 1],
+                        scalar2=shift_col[:, f : f + 1], op0=ALU.mult, op1=ALU.add,
+                    )
+                else:
+                    nc.scalar.activation(
+                        out=part[:], in_=flipped[0][t][:], func=ACT.Identity,
+                        scale=gain_col[0][:, f : f + 1], bias=shift_col[:, f : f + 1],
+                    )
+                first_part[t] = part
+
+            def argument(t):
+                first_tile, h = sequence[t]
+                f = first_tile + h
+                if first_tile == IN_GATE:
+                    result[t] = fresh[h]
+                elif first_tile == FORGET_GATE:
+                    result[t] = forget[h]
+                elif first_tile == OUT_GATE:
+                    result[t] = out_gate[h]
+                else:
+                    squashed = gate_pool.tile([P, BATCH_TILES, P], F32, tag="squashed", bufs=4)
+                    result[t] = squashed
+                nc.vector.scalar_tensor_tensor(
+                    out=result[t][:], in0=flipped[1][t][:], scalar=gain_col[1][:, f : f + 1], in1=first_part[t][:],
+                    op0=ALU.mult, op1=ALU.add,
+                )
+
+            def function(t):
+                first_tile, h = sequence[t]
+                func = ACT.Tanh if first_tile == IN_TRANSFORM else ACT.Sigmoid
+                nc.scalar.activation(out=result[t][:], in_=result[t][:], func=func)
+                if first_tile == IN_TRANSFORM:
+                    nc.gpsimd.tensor_tensor(out=fresh[h][:], in0=fresh[h][:], in1=result[t][:], op=ALU.mult)
+
+            cx_features = {}
+
+            def flip_cx(h):
+                bank = psum.tile([P, BATCH_TILES, P], BF16, tag="flip", bufs=2)
+                for bt in batch_tiles:
+                    nc.tensor.transpose(bank[:, bt, :], cx_sb[bt][:, h * P : (h + 1) * P], identity_bf16[:])
+                cx_features[h] = bank
+
+            def kept_part(h):
+                nc.vector.tensor_mul(out=forget[h][:], in0=forget[h][:], in1=cx_features[h][:])
+
+            cell = [pre[0][bt][:, 0:HIDDEN] for bt in batch_tiles]
+            cell_normal = [pre[0][bt][:, HIDDEN : 2 * HIDDEN] for bt in batch_tiles]
+            hidden = [pre[1][bt][:, 0:HIDDEN] for bt in batch_tiles]
+            cell_st = new_statistics("cell", BATCH_TILES, HIDDEN_BANKS, HIDDEN)
+            rows_bank = {}
+
+            def bank_columns(bank):
+                return slice(bank * BANK, (bank + 1) * BANK)
+
+            def cell_to_rows(bt, bank):
+                back = psum.tile([P, BANK], F32, tag="flip", bufs=2)
+                for q in range(BLOCKS_PER_BANK):
+                    h = bank * BLOCKS_PER_BANK + q
+                    for i, tiles in enumerate((forget, fresh)):
+                        nc.tensor.matmul(
+                            out=back[:, q * P : (q + 1) * P], lhsT=tiles[h][:, bt, :], rhs=identity[:],
+                            is_transpose=True, start=(i == 0), stop=(i == 1),
+                        )
+                rows_bank[(bt, bank)] = back
+
+            def cell_out(bt, bank):
+                cols = bank_columns(bank)
+                if bt % 2 == 0:
+                    nc.vector.tensor_scalar(
+                        out=cell[bt][:, cols], in0=rows_bank[(bt, bank)][:], scalar1=1.0, scalar2=0.0,
+                        op0=ALU.mult, op1=ALU.add, accum_out=cell_st["sums"][:, bt, bank : bank + 1],
+                    )
+                else:
+                    nc.scalar.activation(
+                        out=cell[bt][:, cols], in_=rows_bank[(bt, bank)][:], func=ACT.Identity,
+                        accum_out=cell_st["sums"][:, bt, bank : bank + 1],
+                    )
+                nc.sync.dma_start(out=out_1[bt * P : (bt + 1) * P, cols], in_=cell[bt][:, cols])
+
+            def cell_squares(bt, bank):
+                if bank == 0:
+                    pivot(cell_st, bt)
+                squares_about_pivot(cell_st, bt, bank, cell[bt][:, bank_columns(bank)])
+                if bank == HIDDEN_BANKS - 1:
+                    mean_of(cell_st, bt)
+                    centred_of(cell_st, bt)
+
+            last = groups[-1]
+            for t in range(LEAD):
+                to_features(0, t)
+                if t >= 1:
+                    first_product_part(t - 1, on_vector=(t % 2 == 1))
+            first_product_part(LEAD - 1, on_vector=False)
+            deviation_of(statistics[last])
+            normalise_group(("gpsimd", "scalar"), last, IN_GATE)
+            normalise_group(("gpsimd",) * PAIR, last, IN_TRANSFORM)
+            for group in groups[-2:]:
+                normalise_group(("gpsimd",) * PAIR, group, FORGET_GATE)
+
+            jobs = {}
+
+            def at(step, job, *args):
+                jobs.setdefault(step, []).append((job, args))
+
+            steps = list(range(count - HELD_BACK)) + [None] * PAUSE + list(range(count - HELD_BACK, count))
+            forget_step = sequence.index((FORGET_GATE, 0))
+            for group in groups[-2:]:
+                at(forget_step + 1, normalise_group, ("gpsimd",) * PAIR, group, OUT_GATE)
+            for h in range(HIDDEN_TILES):
+                at(forget_step + h, flip_cx, h)
+                at(forget_step + h + 2, kept_part, h)
+            for bank in range(HIDDEN_BANKS):
+                start = forget_step + (bank + 1) * BLOCKS_PER_BANK + 2
+                for bt in batch_tiles:
+                    at(start + bt, cell_to_rows, bt, bank)
+                    at(start + bt + 1, cell_out, bt, bank)
+                    at(start + bt + 2, cell_squares, bt, bank)
+            last_cell_step = start + BATCH_TILES + 1
+            at(last_cell_step, deviation_of, cell_st)
+
+            def tile_at(step):
+                return steps[step] if 0 <= step < len(steps) else None
+
+            to_features(1, 0)
+            made = LEAD
+            for step in range(max(len(steps), last_cell_step) + 1):
+                if tile_at(step + 1) is not None:
+                    to_features(1, tile_at(step + 1))
+                if tile_at(step) is not None:
+                    waiting = made - 1 if made - 1 not in first_part else None
+                    if made < count:
+                        to_features(0, made)
+                        made += 1
+                    argument(tile_at(step))
+                    if waiting is not None:
+                        first_product_part(waiting, on_vector=(waiting % VECTOR_EVERY == 0))
+                if tile_at(step - 1) is not None:
+                    function(tile_at(step - 1))
+                for job, args in jobs.get(step, ()):
+                    job(*args)
+
+            for bank in range(HIDDEN_BANKS):
+                cols = bank_columns(bank)
+                for bt, engine in zip(batch_tiles, ("vector", "vector", "vector", "scalar")):
+                    normalise(engine, cell_normal[bt][:, cols], cell[bt][:, cols], cell_st, bt)
+
+            def squash(h):
+                bank = psum.tile([P, BATCH_TILES, P], F32, tag="acc")
+                for bt in batch_tiles:
+                    nc.tensor.transpose(bank[:, bt, :], cell_normal[bt][:, h * P : (h + 1) * P], identity[:])
+                squashed = gate_pool.tile([P, BATCH_TILES, P], F32, tag="squashed", bufs=4)
+                nc.scalar.activation(
+                    out=squashed[:], in_=bank[:], func=ACT.Tanh,
+                    scale=out_feature[:, 0, h : h + 1], bias=out_feature[:, 1, h : h + 1],
+                )
+                nc.vector.tensor_mul(out=out_gate[h][:], in0=out_gate[h][:], in1=squashed[:])
+
+            def hidden_out(bt, bank):
+                back = psum.tile([P, BANK], F32, tag="flip", bufs=2)
                 for q in range(BLOCKS_PER_BANK):
                     nc.tensor.transpose(
-                        back[:, q * P : (q + 1) * P], tiles[bank * BLOCKS_PER_BANK + q][:, bt, :], identity[:]
+                        back[:, q * P : (q + 1) * P], out_gate[bank * BLOCKS_PER_BANK + q][:, bt, :], identity[:]
                     )
-                return back
+                cols = bank_columns(bank)
+                if bt % 2 == 0:
+                    nc.vector.tensor_copy(out=hidden[bt][:, cols], in_=back[:])
+                else:
+                    nc.scalar.copy(out=hidden[bt][:, cols], in_=back[:])
+                nc.sync.dma_start(out=out_0[bt * P : (bt + 1) * P, cols], in_=hidden[bt][:, cols])
 
-            cell = [pre[0][bt][:, 0:HIDDEN] for bt in range(BATCH_TILES)]
-            hidden = [pre[0][bt][:, HIDDEN : 2 * HIDDEN] for bt in range(BATCH_TILES)]
-
-            def new_cell(bt, bank, cell_sums):
-                cols = slice(bank * BANK, (bank + 1) * BANK)
-                cx_sb = stage.tile([P, BANK], BF16, tag="cx_sb", bufs=4)
-                nc.sync.dma_start(out=cx_sb[:], in_=cx[bt * P : (bt + 1) * P, cols])
-                nc.vector.tensor_mul(out=cell[bt][:, cols], in0=to_rows(forget, bt, bank)[:], in1=cx_sb[:])
-                nc.vector.scalar_tensor_tensor(
-                    out=cell[bt][:, cols],
-                    in0=to_rows(fresh, bt, bank)[:],
-                    scalar=1.0,
-                    in1=cell[bt][:, cols],
-                    op0=ALU.mult,
-                    op1=ALU.add,
-                    accum_out=cell_sums[:, bank : bank + 1],
-                )
-
-            def new_hidden(bt, neg_mean, inv_std):
-                nc.vector.scalar_tensor_tensor(
-                    out=hidden[bt], in0=cell[bt], scalar=neg_mean[:], in1=gain_out[:], op0=ALU.add, op1=ALU.mult
-                )
-                nc.vector.scalar_tensor_tensor(
-                    out=hidden[bt], in0=hidden[bt], scalar=inv_std[:], in1=shift_out[:], op0=ALU.mult, op1=ALU.add
-                )
-                nc.scalar.activation(out=hidden[bt], in_=hidden[bt], func=ACT.Tanh)
-                for bank in range(HIDDEN_BANKS):
-                    cols = slice(bank * BANK, (bank + 1) * BANK)
-                    nc.vector.tensor_mul(
-                        out=hidden[bt][:, cols], in0=to_rows(out_gate, bt, bank)[:], in1=hidden[bt][:, cols]
-                    )
-                nc.sync.dma_start(out=out_0[bt * P : (bt + 1) * P, :], in_=hidden[bt])
-
-            batch_tiles = range(BATCH_TILES)
-            cell_sums = [stats.tile([P, HIDDEN_BANKS], F32, name="cell_sums%d" % bt, tag="cell_sums") for bt in batch_tiles]
-            for bank in range(HIDDEN_BANKS):
-                for h in range(bank * BLOCKS_PER_BANK, (bank + 1) * BLOCKS_PER_BANK):
-                    gate(IN_GATE + h, ACT.Sigmoid, fresh[h])
-                    in_transform = gate_pool.tile([P, BATCH_TILES, P], F32, tag="in_transform", bufs=2)
-                    gate(IN_TRANSFORM + h, ACT.Tanh, in_transform)
-                    nc.vector.tensor_mul(out=fresh[h][:], in0=fresh[h][:], in1=in_transform[:])
-                    gate(FORGET_GATE + h, ACT.Sigmoid, forget[h])
-                for bt in batch_tiles:
-                    new_cell(bt, bank, cell_sums[bt])
-            cell_stats = []
+            for h in range(HIDDEN_TILES + 2):
+                if h < HIDDEN_TILES:
+                    squash(h)
+                if h >= BLOCKS_PER_BANK + 1 and h - BLOCKS_PER_BANK - 1 < BATCH_TILES:
+                    hidden_out(h - BLOCKS_PER_BANK - 1, 0)
             for bt in batch_tiles:
-                nc.sync.dma_start(out=out_1[bt * P : (bt + 1) * P, :], in_=cell[bt])
-                cell_stats.append(centred_squares(cell_sums[bt][:], cell[bt], cell_squares[:]))
-            for h in range(HIDDEN_TILES):
-                gate(OUT_GATE + h, ACT.Sigmoid, out_gate[h])
-            for bt in batch_tiles:
-                new_hidden(bt, cell_stats[bt][0], inverse_deviation(cell_stats[bt][1], HIDDEN))
+                hidden_out(bt, 1)

@@ -40,11 +40,14 @@ GATE_ORDER = (IN_GATE, IN_TRANSFORM, FORGET_GATE, OUT_GATE)
 FORGET_GATE_BIAS = -1.0
 EPS = 1e-5
 PAIR = 2
-LEAD = 8
+LEAD = 12
 HELD_BACK = 3
 PAUSE = 3
 VECTOR_EVERY = 3
-PREPARE_AT = 3
+PREPARE_AT = 2
+QUANTISE_AFTER = 3
+SQUARE_PIECES = ((0, 2), (2, 4), (4, 6), (6, 7), (7, 8))
+SQUARES_PIECE = 2 * BANK
 
 FLOPS = 2 * 2 * BATCH * K * GATES
 
@@ -103,16 +106,15 @@ def tile_layernormlstmcell_kernel(
         def columns(name, width):
             return keep.tile([P, width], F32, name=name)
 
-        def new_statistics(name, width, chunks, length):
+        def new_statistics(name, width, chunks, pieces, length):
             return {
                 "width": width,
                 "chunks": chunks,
+                "pieces": pieces,
                 "length": length,
-                "spread": math.sqrt(length / chunks),
                 "sums": keep.tile([P, width, chunks], F32, name=name + "_sums"),
-                "square_sums": keep.tile([P, width, chunks], F32, name=name + "_square_sums"),
+                "square_sums": keep.tile([P, width, pieces], F32, name=name + "_square_sums"),
                 "neg_pivot": columns(name + "_neg_pivot", width),
-                "spread_neg_pivot": columns(name + "_spread_neg_pivot", width),
                 "neg_mean": columns(name + "_neg_mean", width),
                 "offset_term": columns(name + "_offset_term", width),
                 "neg_centred": columns(name + "_neg_centred", width),
@@ -128,16 +130,14 @@ def tile_layernormlstmcell_kernel(
 
         def pivot(st, i):
             chunk_length = st["length"] // st["chunks"]
-            first_sum = st["sums"][:, i, 0:1]
-            nc.scalar.activation(out=column(st, "neg_pivot", i), in_=first_sum, func=ACT.Identity, scale=-1.0 / chunk_length)
             nc.scalar.activation(
-                out=column(st, "spread_neg_pivot", i), in_=first_sum, func=ACT.Identity, scale=-st["spread"] / chunk_length
+                out=column(st, "neg_pivot", i), in_=st["sums"][:, i, 0:1], func=ACT.Identity, scale=-1.0 / chunk_length
             )
 
         def squares_about_pivot(st, i, c, values):
-            unread = stage.tile([P, BANK], BF16, tag="unread_squares")
+            unread = stage.tile([P, SQUARES_PIECE], BF16, tag="unread_squares")
             nc.scalar.activation(
-                out=unread[:], in_=values, func=ACT.Square, bias=column(st, "neg_pivot", i),
+                out=unread[:, 0 : values.shape[1]], in_=values, func=ACT.Square, bias=column(st, "neg_pivot", i),
                 accum_out=st["square_sums"][:, i, c : c + 1],
             )
 
@@ -149,51 +149,60 @@ def tile_layernormlstmcell_kernel(
             )
             nc.scalar.activation(
                 out=column(st, "offset_term", i), in_=column(st, "neg_mean", i), func=ACT.Square,
-                scale=-st["spread"], bias=column(st, "spread_neg_pivot", i),
+                scale=-1.0, bias=column(st, "neg_pivot", i),
             )
 
         def centred_of(st, i):
             unread = stage.tile([P, CHUNKS], F32, tag="unread_columns")
             nc.scalar.activation(
-                out=unread[:, 0 : st["chunks"]], in_=st["square_sums"][:, i, :], func=ACT.Identity, scale=-1.0,
+                out=unread[:, 0 : st["pieces"]], in_=st["square_sums"][:, i, :], func=ACT.Identity,
+                scale=-1.0 * st["pieces"] / st["length"],
                 bias=column(st, "offset_term", i), accum_out=column(st, "neg_centred", i),
+            )
+            nc.scalar.activation(
+                out=column(st, "centred", i), in_=column(st, "neg_centred", i), func=ACT.Relu,
+                scale=-1.0 * st["length"] / st["pieces"],
             )
 
         def deviation_of(st):
             width = st["width"]
-            nc.gpsimd.tensor_scalar(
-                out=st["centred"][:], in0=st["neg_centred"][:], scalar1=-1.0, scalar2=0.0, op0=ALU.mult, op1=ALU.max
-            )
             nc.gpsimd.tensor_tensor(out=st["root"][:], in0=st["centred"][:], in1=half[:, 0:width], op=ALU.pow)
             nc.gpsimd.tensor_scalar(
                 out=st["std_eps"][:], in0=st["root"][:], scalar1=1.0 / math.sqrt(st["length"] - 1), scalar2=EPS,
                 op0=ALU.mult, op1=ALU.add,
             )
             nc.gpsimd.tensor_tensor(out=st["inv_std"][:], in0=st["std_eps"][:], in1=minus_one[:, 0:width], op=ALU.pow)
-            nc.gpsimd.tensor_tensor(
-                out=st["neg_mean_over_std"][:], in0=st["neg_mean"][:], in1=st["inv_std"][:], op=ALU.mult
-            )
 
         def normalise(engine, out, in_, st, i):
-            scale, shift = column(st, "inv_std", i), column(st, "neg_mean_over_std", i)
+            neg_mean, inv_std = column(st, "neg_mean", i), column(st, "inv_std", i)
             if engine == "scalar":
-                nc.scalar.activation(out=out, in_=in_, func=ACT.Identity, scale=scale, bias=shift)
+                nc.scalar.activation(
+                    out=out, in_=in_, func=ACT.Identity, scale=inv_std, bias=column(st, "neg_mean_over_std", i)
+                )
             elif engine == "vector":
-                nc.vector.tensor_scalar(out=out, in0=in_, scalar1=scale, scalar2=shift, op0=ALU.mult, op1=ALU.add)
+                nc.vector.tensor_scalar(out=out, in0=in_, scalar1=neg_mean, scalar2=inv_std, op0=ALU.add, op1=ALU.mult)
             else:
-                nc.gpsimd.tensor_scalar(out=out, in0=in_, scalar1=scale, scalar2=shift, op0=ALU.mult, op1=ALU.add)
+                nc.gpsimd.tensor_scalar(out=out, in0=in_, scalar1=neg_mean, scalar2=inv_std, op0=ALU.add, op1=ALU.mult)
+
+        def scalar_shift(st, i):
+            nc.scalar.activation(
+                out=column(st, "neg_mean_over_std", i), in_=column(st, "neg_mean", i), func=ACT.Identity,
+                scale=column(st, "inv_std", i),
+            )
 
         def gate_columns(j, bt, first_tile):
             return pre[j][bt][:, first_tile * P : first_tile * P + HIDDEN]
 
         groups = [(j, first) for j in range(2) for first in range(0, BATCH_TILES, PAIR)]
-        statistics = {group: new_statistics("pre%d_%d" % group, PAIR, CHUNKS, GATES) for group in groups}
+        statistics = {group: new_statistics("pre%d_%d" % group, PAIR, CHUNKS, len(SQUARE_PIECES), GATES) for group in groups}
 
-        def normalise_group(engines, group, first_tile):
+        def normalise_group(engines, group, first_tile, pieces=1):
             j, first = group
-            for i, engine in enumerate(engines):
-                piece = gate_columns(j, first + i, first_tile)
-                normalise(engine, piece, piece, statistics[group], i)
+            width = HIDDEN // pieces
+            for part in range(pieces):
+                for i, engine in enumerate(engines):
+                    piece = gate_columns(j, first + i, first_tile)[:, part * width : (part + 1) * width]
+                    normalise(engine, piece, piece, statistics[group], i)
 
         with tc.tile_pool(name="weights", bufs=1) as weights:
             planes = []
@@ -221,7 +230,7 @@ def tile_layernormlstmcell_kernel(
             x_tiles = {}
 
             def load_activation(j, bt):
-                x_sb = stage.tile([P, K], BF16, tag="x_sb", bufs=4)
+                x_sb = weights.tile([P, K], BF16, tag="x_sb", bufs=4)
                 nc.sync.dma_start(out=x_sb[:], in_=acts[j][bt * P : (bt + 1) * P, :])
                 x_tiles[(j, bt)] = x_sb
 
@@ -282,7 +291,7 @@ def tile_layernormlstmcell_kernel(
                             x_words[:, 256 * g + u : 256 * (g + 1) : 2],
                             identity[:],
                         )
-                grouped = stage.tile([P, PASSES * P * 4], BF16, tag="grouped", align_bytes=64)
+                grouped = weights.tile([P, PASSES * P * 4], BF16, tag="grouped", bufs=2, align_bytes=64)
                 nc.scalar.copy(
                     out=grouped[:].bitcast(F32).rearrange("p (g b u) -> p g b u", g=PASSES, u=2),
                     in_=flipped[:].rearrange("p (g u) b -> p g b u", u=2),
@@ -321,8 +330,11 @@ def tile_layernormlstmcell_kernel(
                     accum_out=statistics[(j, bt - bt % PAIR)]["sums"][:, bt % PAIR, c : c + 1],
                 )
 
-            def chunk_squares(j, bt, c):
-                squares_about_pivot(statistics[(j, bt - bt % PAIR)], bt % PAIR, c, pre[j][bt][:, chunk_columns(c)])
+            def piece_squares(j, bt, piece):
+                first_chunk, end_chunk = SQUARE_PIECES[piece]
+                squares_about_pivot(
+                    statistics[(j, bt - bt % PAIR)], bt % PAIR, piece, pre[j][bt][:, first_chunk * BANK : end_chunk * BANK]
+                )
 
             def feature_vectors():
                 vector_cols = psum.tile([P, P], BF16, tag="flip", bufs=2)
@@ -347,20 +359,19 @@ def tile_layernormlstmcell_kernel(
                 for c in range(CHUNKS):
                     for i in range(PAIR):
                         chunk_product(j, first + i, c)
-                        if c > 0:
-                            chunk_squares(j, first + i, c)
-                    if c == 0:
-                        for i in range(PAIR):
+                        if c == 0:
                             pivot(st, i)
-                            chunk_squares(j, first + i, 0)
+                        for piece, (first_chunk, end_chunk) in enumerate(SQUARE_PIECES):
+                            if end_chunk == c + 1:
+                                piece_squares(j, first + i, piece)
                     if number == 0 and c == 0:
                         late_loads()
                     if number == 0 and c == PREPARE_AT + PAIR:
                         last_loads()
                     if number + 1 < len(groups) and PREPARE_AT <= c < PREPARE_AT + PAIR:
                         regroup_activation(groups[number + 1][0], groups[number + 1][1] + c - PREPARE_AT)
-                    if number + 1 < len(groups) and PREPARE_AT + 1 <= c < PREPARE_AT + 1 + PAIR:
-                        quantise_activation(groups[number + 1][0], groups[number + 1][1] + c - PREPARE_AT - 1)
+                    if number + 1 < len(groups) and PREPARE_AT + QUANTISE_AFTER <= c < PREPARE_AT + QUANTISE_AFTER + PAIR:
+                        quantise_activation(groups[number + 1][0], groups[number + 1][1] + c - PREPARE_AT - QUANTISE_AFTER)
                     if number == 1 and c == CHUNKS - 1:
                         feature_vectors()
                     if c == CHUNKS - 1:
@@ -450,7 +461,7 @@ def tile_layernormlstmcell_kernel(
             cell = [pre[0][bt][:, 0:HIDDEN] for bt in batch_tiles]
             cell_normal = [pre[0][bt][:, HIDDEN : 2 * HIDDEN] for bt in batch_tiles]
             hidden = [pre[1][bt][:, 0:HIDDEN] for bt in batch_tiles]
-            cell_st = new_statistics("cell", BATCH_TILES, HIDDEN_BANKS, HIDDEN)
+            cell_st = new_statistics("cell", BATCH_TILES, HIDDEN_BANKS, HIDDEN_BANKS, HIDDEN)
             rows_bank = {}
 
             def bank_columns(bank):
@@ -469,16 +480,10 @@ def tile_layernormlstmcell_kernel(
 
             def cell_out(bt, bank):
                 cols = bank_columns(bank)
-                if bt % 2 == 0:
-                    nc.vector.tensor_scalar(
-                        out=cell[bt][:, cols], in0=rows_bank[(bt, bank)][:], scalar1=1.0, scalar2=0.0,
-                        op0=ALU.mult, op1=ALU.add, accum_out=cell_st["sums"][:, bt, bank : bank + 1],
-                    )
-                else:
-                    nc.scalar.activation(
-                        out=cell[bt][:, cols], in_=rows_bank[(bt, bank)][:], func=ACT.Identity,
-                        accum_out=cell_st["sums"][:, bt, bank : bank + 1],
-                    )
+                nc.vector.tensor_scalar(
+                    out=cell[bt][:, cols], in0=rows_bank[(bt, bank)][:], scalar1=1.0, scalar2=0.0,
+                    op0=ALU.mult, op1=ALU.add, accum_out=cell_st["sums"][:, bt, bank : bank + 1],
+                )
                 nc.sync.dma_start(out=out_1[bt * P : (bt + 1) * P, cols], in_=cell[bt][:, cols])
 
             def cell_squares(bt, bank):
@@ -496,7 +501,8 @@ def tile_layernormlstmcell_kernel(
                     first_product_part(t - 1, on_vector=(t % 2 == 1))
             first_product_part(LEAD - 1, on_vector=False)
             deviation_of(statistics[last])
-            normalise_group(("gpsimd", "scalar"), last, IN_GATE)
+            scalar_shift(statistics[last], 1)
+            normalise_group(("gpsimd", "scalar"), last, IN_GATE, pieces=2)
             normalise_group(("gpsimd",) * PAIR, last, IN_TRANSFORM)
             for group in groups[-2:]:
                 normalise_group(("gpsimd",) * PAIR, group, FORGET_GATE)
@@ -546,6 +552,8 @@ def tile_layernormlstmcell_kernel(
             for bank in range(HIDDEN_BANKS):
                 cols = bank_columns(bank)
                 for bt, engine in zip(batch_tiles, ("vector", "vector", "vector", "scalar")):
+                    if engine == "scalar" and bank == 0:
+                        scalar_shift(cell_st, bt)
                     normalise(engine, cell_normal[bt][:, cols], cell[bt][:, cols], cell_st, bt)
 
             def squash(h):

@@ -40,10 +40,10 @@ GATE_ORDER = (IN_GATE, IN_TRANSFORM, FORGET_GATE, OUT_GATE)
 FORGET_GATE_BIAS = -1.0
 EPS = 1e-5
 PAIR = 2
-LEAD = 12
-HELD_BACK = 3
+LEAD = 8
+HELD_BACK = 2
 PAUSE = 3
-VECTOR_EVERY = 3
+VECTOR_EVERY = 2
 PREPARE_AT = 2
 QUANTISE_AFTER = 3
 SQUARE_PIECES = ((0, 2), (2, 4), (4, 6), (6, 7), (7, 8))
@@ -93,8 +93,14 @@ def tile_layernormlstmcell_kernel(
         nc.gpsimd.memset(half[:], 0.5)
         minus_one = keep.tile([P, BATCH_TILES], F32, name="minus_one")
         nc.gpsimd.memset(minus_one[:], -1.0)
+        unread_sigmoid = keep.tile([P, BATCH_TILES], F32, name="unread_sigmoid")
+        nc.scalar.activation(out=unread_sigmoid[:], in_=half[:], func=ACT.Sigmoid)
 
-        pre = [[keep.tile([P, GATES], F32, name="pre%d_%d" % (j, bt)) for bt in batch_tiles] for j in range(2)]
+        first_product = keep.tile([P, BATCH_TILES, GATES], F32, name="first_product")
+        pre = [
+            [first_product[:, bt, :] for bt in batch_tiles],
+            [keep.tile([P, GATES], F32, name="pre1_%d" % bt)[:] for bt in batch_tiles],
+        ]
         cx_sb = [keep.tile([P, HIDDEN], BF16, name="cx_sb%d" % bt) for bt in batch_tiles]
         vector_rows = keep.tile([P, P], BF16, name="vector_rows")
         out_rows = keep.tile([P, P], BF16, name="out_rows")
@@ -163,6 +169,21 @@ def tile_layernormlstmcell_kernel(
                 out=column(st, "centred", i), in_=column(st, "neg_centred", i), func=ACT.Relu,
                 scale=-1.0 * st["length"] / st["pieces"],
             )
+
+        def mean_and_centred_on_vector(st):
+            width = st["width"]
+            total = columns("total", width)
+            nc.vector.reduce_sum(out=total[:], in_=st["sums"][:], axis=AXIS.X)
+            nc.vector.tensor_scalar_mul(out=st["neg_mean"][:], in0=total[:], scalar1=-1.0 / st["length"])
+            offset = columns("offset", width)
+            nc.vector.tensor_sub(out=offset[:], in0=st["neg_pivot"][:], in1=st["neg_mean"][:])
+            nc.vector.scalar_tensor_tensor(
+                out=st["offset_term"][:], in0=offset[:], scalar=-1.0 * st["length"], in1=offset[:], op0=ALU.mult, op1=ALU.mult
+            )
+            about_pivot = columns("about_pivot", width)
+            nc.vector.reduce_sum(out=about_pivot[:], in_=st["square_sums"][:], axis=AXIS.X)
+            nc.vector.tensor_add(out=st["neg_centred"][:], in0=about_pivot[:], in1=st["offset_term"][:])
+            nc.vector.tensor_scalar_max(out=st["centred"][:], in0=st["neg_centred"][:], scalar1=0.0)
 
         def deviation_of(st):
             width = st["width"]
@@ -410,15 +431,15 @@ def tile_layernormlstmcell_kernel(
 
             def first_product_part(t, on_vector):
                 f = sequence[t][0] + sequence[t][1]
-                part = gate_pool.tile([P, BATCH_TILES, P], F32, tag="first_part", bufs=LEAD + 1)
+                part = first_product[:, :, f * P : (f + 1) * P]
                 if on_vector:
                     nc.vector.tensor_scalar(
-                        out=part[:], in0=flipped[0][t][:], scalar1=gain_col[0][:, f : f + 1],
+                        out=part, in0=flipped[0][t][:], scalar1=gain_col[0][:, f : f + 1],
                         scalar2=shift_col[:, f : f + 1], op0=ALU.mult, op1=ALU.add,
                     )
                 else:
                     nc.scalar.activation(
-                        out=part[:], in_=flipped[0][t][:], func=ACT.Identity,
+                        out=part, in_=flipped[0][t][:], func=ACT.Identity,
                         scale=gain_col[0][:, f : f + 1], bias=shift_col[:, f : f + 1],
                     )
                 first_part[t] = part
@@ -433,10 +454,10 @@ def tile_layernormlstmcell_kernel(
                 elif first_tile == OUT_GATE:
                     result[t] = out_gate[h]
                 else:
-                    squashed = gate_pool.tile([P, BATCH_TILES, P], F32, tag="squashed", bufs=4)
+                    squashed = gate_pool.tile([P, BATCH_TILES, P], F32, tag="squashed", bufs=8)
                     result[t] = squashed
                 nc.vector.scalar_tensor_tensor(
-                    out=result[t][:], in0=flipped[1][t][:], scalar=gain_col[1][:, f : f + 1], in1=first_part[t][:],
+                    out=result[t][:], in0=flipped[1][t][:], scalar=gain_col[1][:, f : f + 1], in1=first_part[t],
                     op0=ALU.mult, op1=ALU.add,
                 )
 
@@ -490,16 +511,13 @@ def tile_layernormlstmcell_kernel(
                 if bank == 0:
                     pivot(cell_st, bt)
                 squares_about_pivot(cell_st, bt, bank, cell[bt][:, bank_columns(bank)])
-                if bank == HIDDEN_BANKS - 1:
-                    mean_of(cell_st, bt)
-                    centred_of(cell_st, bt)
 
             last = groups[-1]
             for t in range(LEAD):
                 to_features(0, t)
                 if t >= 1:
-                    first_product_part(t - 1, on_vector=(t % 2 == 1))
-            first_product_part(LEAD - 1, on_vector=False)
+                    first_product_part(t - 1, on_vector=(t % 4 != 0))
+            first_product_part(LEAD - 1, on_vector=True)
             deviation_of(statistics[last])
             scalar_shift(statistics[last], 1)
             normalise_group(("gpsimd", "scalar"), last, IN_GATE, pieces=2)
@@ -526,6 +544,7 @@ def tile_layernormlstmcell_kernel(
                     at(start + bt + 1, cell_out, bt, bank)
                     at(start + bt + 2, cell_squares, bt, bank)
             last_cell_step = start + BATCH_TILES + 1
+            at(last_cell_step, mean_and_centred_on_vector, cell_st)
             at(last_cell_step, deviation_of, cell_st)
 
             def tile_at(step):
@@ -543,7 +562,7 @@ def tile_layernormlstmcell_kernel(
                         made += 1
                     argument(tile_at(step))
                     if waiting is not None:
-                        first_product_part(waiting, on_vector=(waiting % VECTOR_EVERY == 0))
+                        first_product_part(waiting, on_vector=(waiting % VECTOR_EVERY == 0 and sequence[waiting][0] != OUT_GATE))
                 if tile_at(step - 1) is not None:
                     function(tile_at(step - 1))
                 for job, args in jobs.get(step, ()):
@@ -551,16 +570,14 @@ def tile_layernormlstmcell_kernel(
 
             for bank in range(HIDDEN_BANKS):
                 cols = bank_columns(bank)
-                for bt, engine in zip(batch_tiles, ("vector", "vector", "vector", "scalar")):
-                    if engine == "scalar" and bank == 0:
-                        scalar_shift(cell_st, bt)
-                    normalise(engine, cell_normal[bt][:, cols], cell[bt][:, cols], cell_st, bt)
+                for bt in batch_tiles:
+                    normalise("vector", cell_normal[bt][:, cols], cell[bt][:, cols], cell_st, bt)
 
             def squash(h):
                 bank = psum.tile([P, BATCH_TILES, P], F32, tag="acc")
                 for bt in batch_tiles:
                     nc.tensor.transpose(bank[:, bt, :], cell_normal[bt][:, h * P : (h + 1) * P], identity[:])
-                squashed = gate_pool.tile([P, BATCH_TILES, P], F32, tag="squashed", bufs=4)
+                squashed = gate_pool.tile([P, BATCH_TILES, P], F32, tag="squashed", bufs=8)
                 nc.scalar.activation(
                     out=squashed[:], in_=bank[:], func=ACT.Tanh,
                     scale=out_feature[:, 0, h : h + 1], bias=out_feature[:, 1, h : h + 1],
@@ -574,10 +591,7 @@ def tile_layernormlstmcell_kernel(
                         back[:, q * P : (q + 1) * P], out_gate[bank * BLOCKS_PER_BANK + q][:, bt, :], identity[:]
                     )
                 cols = bank_columns(bank)
-                if bt % 2 == 0:
-                    nc.vector.tensor_copy(out=hidden[bt][:, cols], in_=back[:])
-                else:
-                    nc.scalar.copy(out=hidden[bt][:, cols], in_=back[:])
+                nc.scalar.copy(out=hidden[bt][:, cols], in_=back[:])
                 nc.sync.dma_start(out=out_0[bt * P : (bt + 1) * P, cols], in_=hidden[bt][:, cols])
 
             for h in range(HIDDEN_TILES + 2):

@@ -226,6 +226,8 @@ def tile_layernormlstmcell_kernel(
                     normalise(engine, piece, piece, statistics[group], i)
 
         with tc.tile_pool(name="weights", bufs=1) as weights:
+            bias_chunks = weights.tile([P, BANK], BF16, name="bias_chunks")
+            nc.vector.memset(bias_chunks[:], 0.0)
             planes = []
             for j in range(2):
                 plane = weights.tile([P, PASSES, GATES], U8, name="plane%d" % j, align_bytes=64)
@@ -255,19 +257,38 @@ def tile_layernormlstmcell_kernel(
                 nc.sync.dma_start(out=x_sb[:], in_=acts[j][bt * P : (bt + 1) * P, :])
                 x_tiles[(j, bt)] = x_sb
 
-            def load_scales(j):
-                scale_rows = w_scales[j].bitcast(I32).rearrange("g (q r) n -> r q g n", r=4)
+            def load_scales(j, start, width):
                 for r in range(4):
-                    nc.sync.dma_start(out=planes[j][r:P:32, :, :].bitcast(I32), in_=scale_rows[r])
+                    nc.sync.dma_start(
+                        out=planes[j][r:P:32, :, start : start + width].bitcast(I32),
+                        in_=w_scales[j][:, :, start : start + width].bitcast(I32).rearrange("g (q r) n -> r q g n", r=4)[r],
+                    )
 
-            def load_quarter(j, c):
+            def load_words(j, c, start, width):
+                first = c * QUARTER + start
                 nc.sync.dma_start(
-                    out=words[j][c][:].bitcast(I32),
-                    in_=w_words[j][:, :, 2 * c * QUARTER : 2 * (c + 1) * QUARTER].bitcast(I32).rearrange("g p n -> p g n"),
+                    out=words[j][c][:, :, 2 * start : 2 * (start + width)].bitcast(I32),
+                    in_=w_words[j][:, :, 2 * first : 2 * (first + width)].bitcast(I32).rearrange("g p n -> p g n"),
                 )
+
+            def load_repeated_bias(j, c):
                 nc.sync.dma_start(
                     out=bias_rep[j][c][:], in_=biases[j][c * QUARTER : (c + 1) * QUARTER].partition_broadcast(P)
                 )
+
+
+            def repeat_bias(c, on_vector):
+                repeated = psum.tile([P, BANK], F32, tag="acc")
+                nc.tensor.matmul(
+                    out=repeated[:], lhsT=identity_bf16[:, c : c + 1].to_broadcast([P, P]), rhs=bias_chunks[:],
+                    start=True, stop=True,
+                )
+                part = c % CHUNKS_PER_QUARTER
+                target = bias_rep[0][c // CHUNKS_PER_QUARTER][:, part * BANK : (part + 1) * BANK]
+                if on_vector:
+                    nc.vector.tensor_copy(out=target, in_=repeated[:])
+                else:
+                    nc.scalar.copy(out=target, in_=repeated[:])
 
             def load_rows(rows, vectors, count):
                 for i, vector in enumerate(vectors):
@@ -276,27 +297,33 @@ def tile_layernormlstmcell_kernel(
                     )
 
             load_activation(0, 0)
+            nc.sync.dma_start(out=bias_chunks[0:CHUNKS, :], in_=biases[0].rearrange("(c n) -> c n", n=BANK))
             load_activation(0, 1)
-            load_scales(0)
-            load_quarter(0, 0)
-            load_quarter(0, 1)
+            load_scales(0, 0, QUARTER)
+            load_words(0, 0, 0, BANK)
+            load_words(0, 0, BANK, BANK)
+            load_scales(0, QUARTER, GATES - QUARTER)
+            load_words(0, 1, 0, QUARTER)
             load_activation(0, 2)
             load_activation(0, 3)
-            load_quarter(0, 2)
-            load_quarter(0, 3)
+            load_words(0, 2, 0, QUARTER)
+            load_words(0, 3, 0, QUARTER)
 
             def late_loads():
                 for bt in range(PAIR):
                     load_activation(1, bt)
                 load_rows(vector_rows, (ln_i2h_w, ln_h2h_w, ln_i2h_b, ln_h2h_b), FEATURE_TILES)
                 load_rows(out_rows, (ln_h2o_w, ln_h2o_b), HIDDEN_TILES)
-                load_scales(1)
-                for c in range(QUARTERS):
-                    load_quarter(1, c)
+                load_scales(1, 0, GATES)
+                load_words(1, 0, 0, QUARTER)
+                load_repeated_bias(1, 0)
 
             def last_loads():
                 for bt in range(PAIR, BATCH_TILES):
                     load_activation(1, bt)
+                for c in range(1, QUARTERS):
+                    load_words(1, c, 0, QUARTER)
+                    load_repeated_bias(1, c)
                 for bt in batch_tiles:
                     nc.sync.dma_start(out=cx_sb[bt][:], in_=cx[bt * P : (bt + 1) * P, :])
 
@@ -371,9 +398,14 @@ def tile_layernormlstmcell_kernel(
                 nc.tensor.transpose(out_cols[:], out_rows[:], identity_bf16[:])
                 nc.scalar.copy(out=out_feature[:].rearrange("p i f -> p (i f)"), in_=out_cols[:, 0 : 2 * HIDDEN_TILES])
 
-            for i in range(PAIR):
-                regroup_activation(0, i)
-                quantise_activation(0, i)
+            regroup_activation(0, 0)
+            repeat_bias(0, on_vector=True)
+            quantise_activation(0, 0)
+            regroup_activation(0, 1)
+            repeat_bias(1, on_vector=True)
+            quantise_activation(0, 1)
+            repeat_bias(2, on_vector=False)
+            repeat_bias(3, on_vector=False)
             for number, group in enumerate(groups):
                 j, first = group
                 st = statistics[group]
@@ -385,6 +417,8 @@ def tile_layernormlstmcell_kernel(
                         for piece, (first_chunk, end_chunk) in enumerate(SQUARE_PIECES):
                             if end_chunk == c + 1:
                                 piece_squares(j, first + i, piece)
+                    if number == 0 and c + 4 < CHUNKS:
+                        repeat_bias(c + 4, on_vector=False)
                     if number == 0 and c == 0:
                         late_loads()
                     if number == 0 and c == PREPARE_AT + PAIR:

@@ -307,7 +307,9 @@ def tile_layernormlstmcell_kernel(
             load_activation(0, 2)
             load_activation(0, 3)
             load_words(0, 2, 0, QUARTER)
+            load_repeated_bias(0, 2)
             load_words(0, 3, 0, QUARTER)
+            load_repeated_bias(0, 3)
 
             def late_loads():
                 for bt in range(PAIR):
@@ -417,8 +419,6 @@ def tile_layernormlstmcell_kernel(
                         for piece, (first_chunk, end_chunk) in enumerate(SQUARE_PIECES):
                             if end_chunk == c + 1:
                                 piece_squares(j, first + i, piece)
-                    if number == 0 and c + 4 < CHUNKS:
-                        repeat_bias(c + 4, on_vector=False)
                     if number == 0 and c == 0:
                         late_loads()
                     if number == 0 and c == PREPARE_AT + PAIR:
@@ -625,7 +625,10 @@ def tile_layernormlstmcell_kernel(
                         back[:, q * P : (q + 1) * P], out_gate[bank * BLOCKS_PER_BANK + q][:, bt, :], identity[:]
                     )
                 cols = bank_columns(bank)
-                nc.scalar.copy(out=hidden[bt][:, cols], in_=back[:])
+                if bank == HIDDEN_BANKS - 1 and bt % 2 == 0:
+                    nc.vector.tensor_copy(out=hidden[bt][:, cols], in_=back[:])
+                else:
+                    nc.scalar.copy(out=hidden[bt][:, cols], in_=back[:])
                 nc.sync.dma_start(out=out_0[bt * P : (bt + 1) * P, cols], in_=hidden[bt][:, cols])
 
             for h in range(HIDDEN_TILES + 2):

@@ -85,12 +85,12 @@ def tile_layernormlstmcell_kernel(
         stage = ctx.enter_context(tc.tile_pool(name="stage", bufs=2))
         psum = ctx.enter_context(tc.psum_pool(name="psum", bufs=6))
 
+        half = keep.tile([P, BATCH_TILES], F32, name="half")
+        nc.gpsimd.memset(half[:], 0.5)
         identity = keep.tile([P, P], F32, name="identity")
         make_identity(nc, identity[:])
         identity_bf16 = keep.tile([P, P], BF16, name="identity_bf16")
         make_identity(nc, identity_bf16[:])
-        half = keep.tile([P, BATCH_TILES], F32, name="half")
-        nc.gpsimd.memset(half[:], 0.5)
         minus_one = keep.tile([P, BATCH_TILES], F32, name="minus_one")
         nc.gpsimd.memset(minus_one[:], -1.0)
         unread_sigmoid = keep.tile([P, BATCH_TILES], F32, name="unread_sigmoid")
@@ -193,6 +193,16 @@ def tile_layernormlstmcell_kernel(
                 op0=ALU.mult, op1=ALU.add,
             )
             nc.gpsimd.tensor_tensor(out=st["inv_std"][:], in0=st["std_eps"][:], in1=minus_one[:, 0:width], op=ALU.pow)
+
+        def root_of(st):
+            nc.gpsimd.tensor_tensor(out=st["root"][:], in0=st["centred"][:], in1=half[:, 0 : st["width"]], op=ALU.pow)
+
+        def deviation_from_root(st):
+            nc.vector.tensor_scalar(
+                out=st["std_eps"][:], in0=st["root"][:], scalar1=1.0 / math.sqrt(st["length"] - 1), scalar2=EPS,
+                op0=ALU.mult, op1=ALU.add,
+            )
+            nc.vector.reciprocal(out=st["inv_std"][:], in_=st["std_eps"][:])
 
         def normalise(engine, out, in_, st, i):
             neg_mean, inv_std = column(st, "neg_mean", i), column(st, "inv_std", i)
@@ -579,7 +589,7 @@ def tile_layernormlstmcell_kernel(
                     at(start + bt + 2, cell_squares, bt, bank)
             last_cell_step = start + BATCH_TILES + 1
             at(last_cell_step, mean_and_centred_on_vector, cell_st)
-            at(last_cell_step, deviation_of, cell_st)
+            at(last_cell_step, root_of, cell_st)
 
             def tile_at(step):
                 return steps[step] if 0 <= step < len(steps) else None
@@ -602,6 +612,7 @@ def tile_layernormlstmcell_kernel(
                 for job, args in jobs.get(step, ()):
                     job(*args)
 
+            deviation_from_root(cell_st)
             for bank in range(HIDDEN_BANKS):
                 cols = bank_columns(bank)
                 for bt in batch_tiles:

@@ -41,7 +41,7 @@ FORGET_GATE_BIAS = -1.0
 EPS = 1e-5
 PAIR = 2
 LEAD = 8
-HELD_BACK = 2
+HELD_BACK = 4
 PAUSE = 3
 VECTOR_EVERY = 2
 PREPARE_AT = 2
@@ -563,6 +563,9 @@ def tile_layernormlstmcell_kernel(
                     first_product_part(t - 1, on_vector=(t % 4 != 0))
             first_product_part(LEAD - 1, on_vector=True)
             deviation_of(statistics[last])
+            for i in range(PAIR):
+                scalar_shift(statistics[groups[-2]], i)
+            normalise_group(("scalar",) * PAIR, groups[-2], OUT_GATE)
             scalar_shift(statistics[last], 1)
             normalise_group(("gpsimd", "scalar"), last, IN_GATE, pieces=2)
             normalise_group(("gpsimd",) * PAIR, last, IN_TRANSFORM)
@@ -576,8 +579,7 @@ def tile_layernormlstmcell_kernel(
 
             steps = list(range(count - HELD_BACK)) + [None] * PAUSE + list(range(count - HELD_BACK, count))
             forget_step = sequence.index((FORGET_GATE, 0))
-            for group in groups[-2:]:
-                at(forget_step + 1, normalise_group, ("gpsimd",) * PAIR, group, OUT_GATE)
+            at(forget_step + 1, normalise_group, ("gpsimd",) * PAIR, last, OUT_GATE)
             for h in range(HIDDEN_TILES):
                 at(forget_step + h, flip_cx, h)
                 at(forget_step + h + 2, kept_part, h)

@@ -45,7 +45,7 @@ HELD_BACK = 4
 PAUSE = 3
 VECTOR_EVERY = 2
 PREPARE_AT = 2
-QUANTISE_AFTER = 3
+QUANTISE_AT = 6
 SQUARE_PIECES = ((0, 2), (2, 4), (4, 6), (6, 7), (7, 8))
 SQUARES_PIECE = 2 * BANK
 
@@ -251,14 +251,13 @@ def tile_layernormlstmcell_kernel(
                 [weights.tile([P, QUARTER], BF16, name="bias_rep%d_%d" % (j, c)) for c in range(QUARTERS)]
                 for j in range(2)
             ]
-            codes = [
-                [weights.tile([P, PASSES * P], U32, name="codes%d_%d" % (j, bt), align_bytes=64) for bt in batch_tiles]
-                for j in range(2)
-            ]
-            code_scales = [
-                [weights.tile([P, PASSES * P], U8, name="code_scales%d_%d" % (j, bt), align_bytes=64) for bt in batch_tiles]
-                for j in range(2)
-            ]
+            codes = {
+                group: weights.tile([P, PAIR * PASSES * P], U32, name="codes%d_%d" % group, align_bytes=64) for group in groups
+            }
+            code_scales = {
+                group: weights.tile([P, PAIR * PASSES * P], U8, name="code_scales%d_%d" % group, align_bytes=64)
+                for group in groups
+            }
 
             x_tiles = {}
 
@@ -351,20 +350,33 @@ def tile_layernormlstmcell_kernel(
                             x_words[:, 256 * g + u : 256 * (g + 1) : 2],
                             identity[:],
                         )
-                grouped = weights.tile([P, PASSES * P * 4], BF16, tag="grouped", bufs=2, align_bytes=64)
+                group = (j, bt - bt % PAIR)
+                if bt % PAIR == 0:
+                    grouped = weights.tile([P, PAIR * K], BF16, tag="grouped", bufs=1, align_bytes=64)
+                    grouped_tiles[group] = grouped
                 nc.scalar.copy(
-                    out=grouped[:].bitcast(F32).rearrange("p (g b u) -> p g b u", g=PASSES, u=2),
+                    out=grouped_tiles[group][:, (bt % PAIR) * K : (bt % PAIR + 1) * K]
+                    .bitcast(F32)
+                    .rearrange("p (g b u) -> p g b u", g=PASSES, u=2),
                     in_=flipped[:].rearrange("p (g u) b -> p g b u", u=2),
                 )
-                grouped_tiles[(j, bt)] = grouped
 
-            def quantise_activation(j, bt):
+            def quantise_activation(group, first_tile, tiles):
+                words = slice(first_tile * PASSES * P, (first_tile + tiles) * PASSES * P)
                 nc.vector.quantize_mx(
-                    out=codes[j][bt][:].bitcast(FP8X4), scales=code_scales[j][bt][:], in_=grouped_tiles[(j, bt)][:]
+                    out=codes[group][:, words].bitcast(FP8X4), scales=code_scales[group][:, words],
+                    in_=grouped_tiles[group][:, first_tile * K : (first_tile + tiles) * K],
                 )
+
+            def wait_for_quantise(group):
+                nc.gpsimd.memset(grouped_tiles[group][:, 0:16], 0.0)
 
             def chunk_columns(c):
                 return slice(c * BANK, (c + 1) * BANK)
+
+            def code_columns(bt, g):
+                start = ((bt % PAIR) * PASSES + g) * P
+                return slice(start, start + P)
 
             def chunk_product(j, bt, c):
                 quarter = c // CHUNKS_PER_QUARTER
@@ -373,8 +385,8 @@ def tile_layernormlstmcell_kernel(
                 for g in range(PASSES):
                     nc.tensor.matmul_mx(
                         out=acc[:],
-                        lhsT=codes[j][bt][:, g * P : (g + 1) * P].bitcast(FP8X4),
-                        lhsT_scale=code_scales[j][bt][:, g * P : (g + 1) * P],
+                        lhsT=codes[(j, bt - bt % PAIR)][:, code_columns(bt, g)].bitcast(FP8X4),
+                        lhsT_scale=code_scales[(j, bt - bt % PAIR)][:, code_columns(bt, g)],
                         rhs=words[j][quarter][:, g, 2 * BANK * part : 2 * BANK * (part + 1)].bitcast(FP4X4),
                         rhs_scale=planes[j][:, g, BANK * c : BANK * (c + 1)],
                         start=(g == 0),
@@ -412,10 +424,10 @@ def tile_layernormlstmcell_kernel(
 
             regroup_activation(0, 0)
             repeat_bias(0, on_vector=True)
-            quantise_activation(0, 0)
+            quantise_activation(groups[0], 0, 1)
             regroup_activation(0, 1)
             repeat_bias(1, on_vector=True)
-            quantise_activation(0, 1)
+            quantise_activation(groups[0], 1, 1)
             repeat_bias(2, on_vector=False)
             repeat_bias(3, on_vector=False)
             for number, group in enumerate(groups):
@@ -435,8 +447,12 @@ def tile_layernormlstmcell_kernel(
                         last_loads()
                     if number + 1 < len(groups) and PREPARE_AT <= c < PREPARE_AT + PAIR:
                         regroup_activation(groups[number + 1][0], groups[number + 1][1] + c - PREPARE_AT)
-                    if number + 1 < len(groups) and PREPARE_AT + QUANTISE_AFTER <= c < PREPARE_AT + QUANTISE_AFTER + PAIR:
-                        quantise_activation(groups[number + 1][0], groups[number + 1][1] + c - PREPARE_AT - QUANTISE_AFTER)
+                    if number + 1 < len(groups) and c == QUANTISE_AT:
+                        quantise_activation(groups[number + 1], 0, PAIR)
+                        if number >= 1:
+                            wait_for_quantise(groups[number + 1])
+                            for first_tile in GATE_ORDER[2:]:
+                                normalise_group(("gpsimd",) * PAIR, groups[number - 1], first_tile)
                     if number == 1 and c == CHUNKS - 1:
                         feature_vectors()
                     if c == CHUNKS - 1:
@@ -445,8 +461,7 @@ def tile_layernormlstmcell_kernel(
                             centred_of(st, i)
                         if number + 1 < len(groups):
                             deviation_of(st)
-                            wanted = GATE_ORDER if number + 2 < len(groups) else GATE_ORDER[:2]
-                            for first_tile in wanted:
+                            for first_tile in GATE_ORDER[:2]:
                                 normalise_group(("gpsimd",) * PAIR, group, first_tile)
 
 

@@ -44,6 +44,8 @@ LEAD = 8
 HELD_BACK = 4
 PAUSE = 3
 VECTOR_EVERY = 2
+VECTOR_UNTIL = 18
+PUT_OFF = (3, 6, 9, 12, 15)
 PREPARE_AT = 2
 QUANTISE_AT = 6
 SQUARE_PIECES = ((0, 2), (2, 4), (4, 6), (6, 7), (7, 8))
@@ -108,12 +110,14 @@ def tile_layernormlstmcell_kernel(
         per_feature = keep.tile([P, 4, FEATURE_TILES], F32, name="per_feature")
         shift_col = keep.tile([P, FEATURE_TILES], F32, name="shift_col")
         out_feature = keep.tile([P, 2, HIDDEN_TILES], F32, name="out_feature")
+        late_gain = [keep.tile([P, HELD_BACK * P], BF16, name="late_gain%d" % j) for j in range(2)]
 
         def columns(name, width):
             return keep.tile([P, width], F32, name=name)
 
         def new_statistics(name, width, chunks, pieces, length):
             return {
+                "name": name,
                 "width": width,
                 "chunks": chunks,
                 "pieces": pieces,
@@ -172,15 +176,15 @@ def tile_layernormlstmcell_kernel(
 
         def mean_and_centred_on_vector(st):
             width = st["width"]
-            total = columns("total", width)
+            total = columns(st["name"] + "_total", width)
             nc.vector.reduce_sum(out=total[:], in_=st["sums"][:], axis=AXIS.X)
             nc.vector.tensor_scalar_mul(out=st["neg_mean"][:], in0=total[:], scalar1=-1.0 / st["length"])
-            offset = columns("offset", width)
+            offset = columns(st["name"] + "_offset", width)
             nc.vector.tensor_sub(out=offset[:], in0=st["neg_pivot"][:], in1=st["neg_mean"][:])
             nc.vector.scalar_tensor_tensor(
                 out=st["offset_term"][:], in0=offset[:], scalar=-1.0 * st["length"], in1=offset[:], op0=ALU.mult, op1=ALU.mult
             )
-            about_pivot = columns("about_pivot", width)
+            about_pivot = columns(st["name"] + "_about_pivot", width)
             nc.vector.reduce_sum(out=about_pivot[:], in_=st["square_sums"][:], axis=AXIS.X)
             nc.vector.tensor_add(out=st["neg_centred"][:], in0=about_pivot[:], in1=st["offset_term"][:])
             nc.vector.tensor_scalar_max(out=st["centred"][:], in0=st["neg_centred"][:], scalar1=0.0)
@@ -234,6 +238,16 @@ def tile_layernormlstmcell_kernel(
                 for i, engine in enumerate(engines):
                     piece = gate_columns(j, first + i, first_tile)[:, part * width : (part + 1) * width]
                     normalise(engine, piece, piece, statistics[group], i)
+
+        def late_columns(j, bt):
+            return gate_columns(j, bt, OUT_GATE)[:, HIDDEN - HELD_BACK * P : HIDDEN]
+
+        def gain_group(group):
+            j, first = group
+            for i in range(PAIR):
+                nc.gpsimd.tensor_tensor(
+                    out=late_columns(j, first + i), in0=late_columns(j, first + i), in1=late_gain[j][:], op=ALU.mult
+                )
 
         with tc.tile_pool(name="weights", bufs=1) as weights:
             bias_chunks = weights.tile([P, BANK], BF16, name="bias_chunks")
@@ -335,6 +349,12 @@ def tile_layernormlstmcell_kernel(
                 for c in range(1, QUARTERS):
                     load_words(1, c, 0, QUARTER)
                     load_repeated_bias(1, c)
+                late_start = OUT_GATE * P + HIDDEN - HELD_BACK * P
+                for j, gains in enumerate((ln_i2h_w, ln_h2h_w)):
+                    nc.sync.dma_start(
+                        out=late_gain[j][:],
+                        in_=gains.rearrange("o n -> (o n)")[late_start : late_start + HELD_BACK * P].partition_broadcast(P),
+                    )
                 for bt in batch_tiles:
                     nc.sync.dma_start(out=cx_sb[bt][:], in_=cx[bt * P : (bt + 1) * P, :])
 
@@ -455,7 +475,7 @@ def tile_layernormlstmcell_kernel(
                                 normalise_group(("gpsimd",) * PAIR, groups[number - 1], first_tile)
                     if number == 1 and c == CHUNKS - 1:
                         feature_vectors()
-                    if c == CHUNKS - 1:
+                    if c == CHUNKS - 1 and number + 1 < len(groups):
                         for i in range(PAIR):
                             mean_of(st, i)
                             centred_of(st, i)
@@ -487,6 +507,17 @@ def tile_layernormlstmcell_kernel(
                 for bt in batch_tiles:
                     nc.tensor.transpose(bank[:, bt, :], pre[j][bt][:, f * P : (f + 1) * P], identity[:])
                 flipped[j][t] = bank
+
+            def to_features_sum(t):
+                f = sequence[t][0] + sequence[t][1]
+                bank = psum.tile([P, BATCH_TILES, P], F32, tag="acc")
+                for bt in batch_tiles:
+                    for j in range(2):
+                        nc.tensor.matmul(
+                            out=bank[:, bt, :], lhsT=pre[j][bt][:, f * P : (f + 1) * P], rhs=identity[:],
+                            is_transpose=True, start=(j == 0), stop=(j == 1),
+                        )
+                flipped[1][t] = bank
 
             def first_product_part(t, on_vector):
                 f = sequence[t][0] + sequence[t][1]
@@ -522,6 +553,12 @@ def tile_layernormlstmcell_kernel(
 
             def function(t):
                 first_tile, h = sequence[t]
+                if t >= count - HELD_BACK:
+                    f = first_tile + h
+                    nc.scalar.activation(
+                        out=out_gate[h][:], in_=flipped[1][t][:], func=ACT.Sigmoid, bias=shift_col[:, f : f + 1]
+                    )
+                    return
                 func = ACT.Tanh if first_tile == IN_TRANSFORM else ACT.Sigmoid
                 nc.scalar.activation(out=result[t][:], in_=result[t][:], func=func)
                 if first_tile == IN_TRANSFORM:
@@ -572,17 +609,20 @@ def tile_layernormlstmcell_kernel(
                 squares_about_pivot(cell_st, bt, bank, cell[bt][:, bank_columns(bank)])
 
             last = groups[-1]
-            for t in range(LEAD):
+            normalise_group(("vector",) * PAIR, groups[-2], OUT_GATE)
+            for t in range(3):
                 to_features(0, t)
-                if t >= 1:
-                    first_product_part(t - 1, on_vector=(t % 4 != 0))
-            first_product_part(LEAD - 1, on_vector=True)
-            deviation_of(statistics[last])
-            for i in range(PAIR):
-                scalar_shift(statistics[groups[-2]], i)
-            normalise_group(("scalar",) * PAIR, groups[-2], OUT_GATE)
+            mean_and_centred_on_vector(statistics[last])
+            root_of(statistics[last])
+            first_product_part(0, on_vector=True)
+            first_product_part(1, on_vector=False)
+            first_product_part(2, on_vector=False)
+            deviation_from_root(statistics[last])
             scalar_shift(statistics[last], 1)
             normalise_group(("gpsimd", "scalar"), last, IN_GATE, pieces=2)
+            for t in range(3, LEAD):
+                to_features(0, t)
+                first_product_part(t, on_vector=(t < 6))
             normalise_group(("gpsimd",) * PAIR, last, IN_TRANSFORM)
             for group in groups[-2:]:
                 normalise_group(("gpsimd",) * PAIR, group, FORGET_GATE)
@@ -595,6 +635,8 @@ def tile_layernormlstmcell_kernel(
             steps = list(range(count - HELD_BACK)) + [None] * PAUSE + list(range(count - HELD_BACK, count))
             forget_step = sequence.index((FORGET_GATE, 0))
             at(forget_step + 1, normalise_group, ("gpsimd",) * PAIR, last, OUT_GATE)
+            for group in groups:
+                at(forget_step + 1, gain_group, group)
             for h in range(HIDDEN_TILES):
                 at(forget_step + h, flip_cx, h)
                 at(forget_step + h + 2, kept_part, h)
@@ -615,15 +657,18 @@ def tile_layernormlstmcell_kernel(
             made = LEAD
             for step in range(max(len(steps), last_cell_step) + 1):
                 if tile_at(step + 1) is not None:
-                    to_features(1, tile_at(step + 1))
-                if tile_at(step) is not None:
+                    if tile_at(step + 1) < count - HELD_BACK:
+                        to_features(1, tile_at(step + 1))
+                    else:
+                        to_features_sum(tile_at(step + 1))
+                if tile_at(step) is not None and tile_at(step) < count - HELD_BACK:
                     waiting = made - 1 if made - 1 not in first_part else None
-                    if made < count:
+                    if made < count - HELD_BACK and step not in PUT_OFF:
                         to_features(0, made)
                         made += 1
                     argument(tile_at(step))
                     if waiting is not None:
-                        first_product_part(waiting, on_vector=(waiting % VECTOR_EVERY == 0 and sequence[waiting][0] != OUT_GATE))
+                        first_product_part(waiting, on_vector=(waiting % VECTOR_EVERY == 0 and waiting < VECTOR_UNTIL))
                 if tile_at(step - 1) is not None:
                     function(tile_at(step - 1))
                 for job, args in jobs.get(step, ()):

@@ -337,18 +337,19 @@ def tile_layernormlstmcell_kernel(
             def late_loads():
                 for bt in range(PAIR):
                     load_activation(1, bt)
-                load_rows(vector_rows, (ln_i2h_w, ln_h2h_w, ln_i2h_b, ln_h2h_b), FEATURE_TILES)
-                load_rows(out_rows, (ln_h2o_w, ln_h2o_b), HIDDEN_TILES)
                 load_scales(1, 0, GATES)
                 load_words(1, 0, 0, QUARTER)
                 load_repeated_bias(1, 0)
 
             def last_loads():
-                for bt in range(PAIR, BATCH_TILES):
-                    load_activation(1, bt)
                 for c in range(1, QUARTERS):
                     load_words(1, c, 0, QUARTER)
                     load_repeated_bias(1, c)
+                    if c == 1:
+                        for bt in range(PAIR, BATCH_TILES):
+                            load_activation(1, bt)
+                load_rows(vector_rows, (ln_i2h_w, ln_h2h_w, ln_i2h_b, ln_h2h_b), FEATURE_TILES)
+                load_rows(out_rows, (ln_h2o_w, ln_h2o_b), HIDDEN_TILES)
                 late_start = OUT_GATE * P + HIDDEN - HELD_BACK * P
                 for j, gains in enumerate((ln_i2h_w, ln_h2h_w)):
                     nc.sync.dma_start(
@@ -465,15 +466,16 @@ def tile_layernormlstmcell_kernel(
                         late_loads()
                     if number == 0 and c == PREPARE_AT + PAIR:
                         last_loads()
-                    if number + 1 < len(groups) and PREPARE_AT <= c < PREPARE_AT + PAIR:
-                        regroup_activation(groups[number + 1][0], groups[number + 1][1] + c - PREPARE_AT)
+                    prepare_at = PREPARE_AT + (1 if number + 2 == len(groups) else 0)
+                    if number + 1 < len(groups) and prepare_at <= c < prepare_at + PAIR:
+                        regroup_activation(groups[number + 1][0], groups[number + 1][1] + c - prepare_at)
                     if number + 1 < len(groups) and c == QUANTISE_AT:
                         quantise_activation(groups[number + 1], 0, PAIR)
                         if number >= 1:
                             wait_for_quantise(groups[number + 1])
                             for first_tile in GATE_ORDER[2:]:
                                 normalise_group(("gpsimd",) * PAIR, groups[number - 1], first_tile)
-                    if number == 1 and c == CHUNKS - 1:
+                    if number + 1 == len(groups) and c == CHUNKS // 2:
                         feature_vectors()
                     if c == CHUNKS - 1 and number + 1 < len(groups):
                         for i in range(PAIR):

@@ -47,6 +47,7 @@ VECTOR_EVERY = 2
 VECTOR_UNTIL = 18
 PUT_OFF = (3, 6, 9, 12, 15)
 PREPARE_AT = 2
+LAST_PIECE = 2
 QUANTISE_AT = 6
 SQUARE_PIECES = ((0, 2), (2, 4), (4, 6), (6, 7), (7, 8))
 SQUARES_PIECE = 2 * BANK
@@ -587,7 +588,7 @@ def tile_layernormlstmcell_kernel(
                 return slice(bank * BANK, (bank + 1) * BANK)
 
             def cell_to_rows(bt, bank):
-                back = psum.tile([P, BANK], F32, tag="flip", bufs=2)
+                back = psum.tile([P, BANK], F32, tag="acc")
                 for q in range(BLOCKS_PER_BANK):
                     h = bank * BLOCKS_PER_BANK + q
                     for i, tiles in enumerate((forget, fresh)):
@@ -693,23 +694,23 @@ def tile_layernormlstmcell_kernel(
                 )
                 nc.vector.tensor_mul(out=out_gate[h][:], in0=out_gate[h][:], in1=squashed[:])
 
-            def hidden_out(bt, bank):
-                back = psum.tile([P, BANK], F32, tag="flip", bufs=2)
-                for q in range(BLOCKS_PER_BANK):
-                    nc.tensor.transpose(
-                        back[:, q * P : (q + 1) * P], out_gate[bank * BLOCKS_PER_BANK + q][:, bt, :], identity[:]
-                    )
-                cols = bank_columns(bank)
-                if bank == HIDDEN_BANKS - 1 and bt % 2 == 0:
-                    nc.vector.tensor_copy(out=hidden[bt][:, cols], in_=back[:])
+            def hidden_out(bt, first, tiles, on_vector):
+                back = psum.tile([P, BANK], F32, tag="acc")
+                for q in range(tiles):
+                    nc.tensor.transpose(back[:, q * P : (q + 1) * P], out_gate[first + q][:, bt, :], identity[:])
+                cols = slice(first * P, (first + tiles) * P)
+                if on_vector:
+                    nc.vector.tensor_copy(out=hidden[bt][:, cols], in_=back[:, 0 : tiles * P])
                 else:
-                    nc.scalar.copy(out=hidden[bt][:, cols], in_=back[:])
+                    nc.scalar.copy(out=hidden[bt][:, cols], in_=back[:, 0 : tiles * P])
                 nc.sync.dma_start(out=out_0[bt * P : (bt + 1) * P, cols], in_=hidden[bt][:, cols])
 
-            for h in range(HIDDEN_TILES + 2):
-                if h < HIDDEN_TILES:
-                    squash(h)
-                if h >= BLOCKS_PER_BANK + 1 and h - BLOCKS_PER_BANK - 1 < BATCH_TILES:
-                    hidden_out(h - BLOCKS_PER_BANK - 1, 0)
+            for h in range(HIDDEN_TILES):
+                squash(h)
+                if h >= BLOCKS_PER_BANK + 1:
+                    hidden_out(h - BLOCKS_PER_BANK - 1, 0, BLOCKS_PER_BANK, on_vector=False)
+            hidden_out(BATCH_TILES - 1, 0, BLOCKS_PER_BANK, on_vector=False)
             for bt in batch_tiles:
-                hidden_out(bt, 1)
+                hidden_out(bt, BLOCKS_PER_BANK, LAST_PIECE, on_vector=False)
+            for bt in batch_tiles:
+                hidden_out(bt, BLOCKS_PER_BANK + LAST_PIECE, LAST_PIECE, on_vector=(bt + 1 < BATCH_TILES))

@@ -42,6 +42,7 @@ EPS = 1e-5
 PAIR = 2
 LEAD = 8
 HELD_BACK = 4
+LATE_TILES = 2
 PAUSE = 3
 VECTOR_EVERY = 2
 VECTOR_UNTIL = 18
@@ -109,9 +110,9 @@ def tile_layernormlstmcell_kernel(
         out_rows = keep.tile([P, P], BF16, name="out_rows")
         nc.gpsimd.memset(out_rows[:], 0.0)
         per_feature = keep.tile([P, 4, FEATURE_TILES], F32, name="per_feature")
-        shift_col = keep.tile([P, FEATURE_TILES], F32, name="shift_col")
+        late_shift = keep.tile([P, LATE_TILES], F32, name="late_shift")
         out_feature = keep.tile([P, 2, HIDDEN_TILES], F32, name="out_feature")
-        late_gain = [keep.tile([P, HELD_BACK * P], BF16, name="late_gain%d" % j) for j in range(2)]
+        late_gain = [keep.tile([P, LATE_TILES * P], BF16, name="late_gain%d" % j) for j in range(2)]
 
         def columns(name, width):
             return keep.tile([P, width], F32, name=name)
@@ -125,7 +126,6 @@ def tile_layernormlstmcell_kernel(
                 "length": length,
                 "sums": keep.tile([P, width, chunks], F32, name=name + "_sums"),
                 "square_sums": keep.tile([P, width, pieces], F32, name=name + "_square_sums"),
-                "neg_pivot": columns(name + "_neg_pivot", width),
                 "neg_mean": columns(name + "_neg_mean", width),
                 "offset_term": columns(name + "_offset_term", width),
                 "neg_centred": columns(name + "_neg_centred", width),
@@ -139,16 +139,14 @@ def tile_layernormlstmcell_kernel(
         def column(st, key, i):
             return st[key][:, i : i + 1]
 
-        def pivot(st, i):
-            chunk_length = st["length"] // st["chunks"]
-            nc.scalar.activation(
-                out=column(st, "neg_pivot", i), in_=st["sums"][:, i, 0:1], func=ACT.Identity, scale=-1.0 / chunk_length
-            )
+        def chunk_length(st):
+            return st["length"] // st["chunks"]
 
         def squares_about_pivot(st, i, c, values):
             unread = stage.tile([P, SQUARES_PIECE], BF16, tag="unread_squares")
             nc.scalar.activation(
-                out=unread[:, 0 : values.shape[1]], in_=values, func=ACT.Square, bias=column(st, "neg_pivot", i),
+                out=unread[:, 0 : values.shape[1]], in_=values, func=ACT.Square,
+                scale=-1.0 * chunk_length(st), bias=st["sums"][:, i, 0:1],
                 accum_out=st["square_sums"][:, i, c : c + 1],
             )
 
@@ -159,15 +157,15 @@ def tile_layernormlstmcell_kernel(
                 accum_out=column(st, "neg_mean", i),
             )
             nc.scalar.activation(
-                out=column(st, "offset_term", i), in_=column(st, "neg_mean", i), func=ACT.Square,
-                scale=-1.0, bias=column(st, "neg_pivot", i),
+                out=column(st, "offset_term", i), in_=st["sums"][:, i, 0:1], func=ACT.Square,
+                scale=1.0 / chunk_length(st), bias=column(st, "neg_mean", i),
             )
 
         def centred_of(st, i):
             unread = stage.tile([P, CHUNKS], F32, tag="unread_columns")
             nc.scalar.activation(
                 out=unread[:, 0 : st["pieces"]], in_=st["square_sums"][:, i, :], func=ACT.Identity,
-                scale=-1.0 * st["pieces"] / st["length"],
+                scale=-1.0 * st["pieces"] / st["length"] / (chunk_length(st) * chunk_length(st)),
                 bias=column(st, "offset_term", i), accum_out=column(st, "neg_centred", i),
             )
             nc.scalar.activation(
@@ -181,13 +179,19 @@ def tile_layernormlstmcell_kernel(
             nc.vector.reduce_sum(out=total[:], in_=st["sums"][:], axis=AXIS.X)
             nc.vector.tensor_scalar_mul(out=st["neg_mean"][:], in0=total[:], scalar1=-1.0 / st["length"])
             offset = columns(st["name"] + "_offset", width)
-            nc.vector.tensor_sub(out=offset[:], in0=st["neg_pivot"][:], in1=st["neg_mean"][:])
+            nc.vector.scalar_tensor_tensor(
+                out=offset[:], in0=st["sums"][:, :, 0], scalar=-1.0 / chunk_length(st), in1=st["neg_mean"][:],
+                op0=ALU.mult, op1=ALU.subtract,
+            )
             nc.vector.scalar_tensor_tensor(
                 out=st["offset_term"][:], in0=offset[:], scalar=-1.0 * st["length"], in1=offset[:], op0=ALU.mult, op1=ALU.mult
             )
             about_pivot = columns(st["name"] + "_about_pivot", width)
             nc.vector.reduce_sum(out=about_pivot[:], in_=st["square_sums"][:], axis=AXIS.X)
-            nc.vector.tensor_add(out=st["neg_centred"][:], in0=about_pivot[:], in1=st["offset_term"][:])
+            nc.vector.scalar_tensor_tensor(
+                out=st["neg_centred"][:], in0=about_pivot[:], scalar=1.0 / (chunk_length(st) * chunk_length(st)),
+                in1=st["offset_term"][:], op0=ALU.mult, op1=ALU.add,
+            )
             nc.vector.tensor_scalar_max(out=st["centred"][:], in0=st["neg_centred"][:], scalar1=0.0)
 
         def deviation_of(st):
@@ -241,7 +245,7 @@ def tile_layernormlstmcell_kernel(
                     normalise(engine, piece, piece, statistics[group], i)
 
         def late_columns(j, bt):
-            return gate_columns(j, bt, OUT_GATE)[:, HIDDEN - HELD_BACK * P : HIDDEN]
+            return gate_columns(j, bt, OUT_GATE)[:, HIDDEN - LATE_TILES * P : HIDDEN]
 
         def gain_group(group):
             j, first = group
@@ -253,11 +257,10 @@ def tile_layernormlstmcell_kernel(
         with tc.tile_pool(name="weights", bufs=1) as weights:
             bias_chunks = weights.tile([P, BANK], BF16, name="bias_chunks")
             nc.vector.memset(bias_chunks[:], 0.0)
-            planes = []
-            for j in range(2):
-                plane = weights.tile([P, PASSES, GATES], U8, name="plane%d" % j, align_bytes=64)
-                nc.vector.memset(plane[:].bitcast(I32), 0)
-                planes.append(plane)
+            planes = [weights.tile([P, PASSES, GATES], U8, name="plane%d" % j, align_bytes=64) for j in range(2)]
+            nc.vector.memset(planes[0][:, :, 0:QUARTER].bitcast(I32), 0)
+            nc.vector.memset(planes[0][:, :, QUARTER:GATES].bitcast(I32), 0)
+            nc.vector.memset(planes[1][:].bitcast(I32), 0)
             words = [
                 [weights.tile([P, PASSES, 2 * QUARTER], U8, name="words%d_%d" % (j, c), align_bytes=64) for c in range(QUARTERS)]
                 for j in range(2)
@@ -351,11 +354,11 @@ def tile_layernormlstmcell_kernel(
                             load_activation(1, bt)
                 load_rows(vector_rows, (ln_i2h_w, ln_h2h_w, ln_i2h_b, ln_h2h_b), FEATURE_TILES)
                 load_rows(out_rows, (ln_h2o_w, ln_h2o_b), HIDDEN_TILES)
-                late_start = OUT_GATE * P + HIDDEN - HELD_BACK * P
+                late_start = OUT_GATE * P + HIDDEN - LATE_TILES * P
                 for j, gains in enumerate((ln_i2h_w, ln_h2h_w)):
                     nc.sync.dma_start(
                         out=late_gain[j][:],
-                        in_=gains.rearrange("o n -> (o n)")[late_start : late_start + HELD_BACK * P].partition_broadcast(P),
+                        in_=gains.rearrange("o n -> (o n)")[late_start : late_start + LATE_TILES * P].partition_broadcast(P),
                     )
                 for bt in batch_tiles:
                     nc.sync.dma_start(out=cx_sb[bt][:], in_=cx[bt * P : (bt + 1) * P, :])
@@ -434,12 +437,17 @@ def tile_layernormlstmcell_kernel(
                 vector_cols = psum.tile([P, P], BF16, tag="flip", bufs=2)
                 nc.tensor.transpose(vector_cols[:], vector_rows[:], identity_bf16[:])
                 nc.scalar.copy(out=per_feature[:].rearrange("p i f -> p (i f)"), in_=vector_cols[:])
-                nc.gpsimd.tensor_tensor(out=shift_col[:], in0=per_feature[:, 2, :], in1=per_feature[:, 3, :], op=ALU.add)
                 forget_tiles = slice(FORGET_GATE, FORGET_GATE + HIDDEN_TILES)
-                nc.gpsimd.tensor_scalar(
-                    out=shift_col[:, forget_tiles], in0=shift_col[:, forget_tiles], scalar1=1.0, scalar2=FORGET_GATE_BIAS,
-                    op0=ALU.mult, op1=ALU.add,
+                nc.scalar.activation(
+                    out=per_feature[:, 3, forget_tiles], in_=per_feature[:, 3, forget_tiles], func=ACT.Identity,
+                    bias=minus_one[:, 0:1],
                 )
+                for q in range(LATE_TILES):
+                    f = OUT_GATE + HIDDEN_TILES - LATE_TILES + q
+                    nc.scalar.activation(
+                        out=late_shift[:, q : q + 1], in_=per_feature[:, 2, f : f + 1], func=ACT.Identity,
+                        bias=per_feature[:, 3, f : f + 1],
+                    )
                 out_cols = psum.tile([P, P], BF16, tag="flip", bufs=2)
                 nc.tensor.transpose(out_cols[:], out_rows[:], identity_bf16[:])
                 nc.scalar.copy(out=out_feature[:].rearrange("p i f -> p (i f)"), in_=out_cols[:, 0 : 2 * HIDDEN_TILES])
@@ -458,8 +466,6 @@ def tile_layernormlstmcell_kernel(
                 for c in range(CHUNKS):
                     for i in range(PAIR):
                         chunk_product(j, first + i, c)
-                        if c == 0:
-                            pivot(st, i)
                         for piece, (first_chunk, end_chunk) in enumerate(SQUARE_PIECES):
                             if end_chunk == c + 1:
                                 piece_squares(j, first + i, piece)
@@ -484,7 +490,7 @@ def tile_layernormlstmcell_kernel(
                             centred_of(st, i)
                         if number + 1 < len(groups):
                             deviation_of(st)
-                            for first_tile in GATE_ORDER[:2]:
+                            for first_tile in GATE_ORDER[: (2 if number + 2 < len(groups) else 1)]:
                                 normalise_group(("gpsimd",) * PAIR, group, first_tile)
 
 
@@ -528,12 +534,12 @@ def tile_layernormlstmcell_kernel(
                 if on_vector:
                     nc.vector.tensor_scalar(
                         out=part, in0=flipped[0][t][:], scalar1=gain_col[0][:, f : f + 1],
-                        scalar2=shift_col[:, f : f + 1], op0=ALU.mult, op1=ALU.add,
+                        scalar2=per_feature[:, 2, f : f + 1], op0=ALU.mult, op1=ALU.add,
                     )
                 else:
                     nc.scalar.activation(
                         out=part, in_=flipped[0][t][:], func=ACT.Identity,
-                        scale=gain_col[0][:, f : f + 1], bias=shift_col[:, f : f + 1],
+                        scale=gain_col[0][:, f : f + 1], bias=per_feature[:, 2, f : f + 1],
                     )
                 first_part[t] = part
 
@@ -556,14 +562,15 @@ def tile_layernormlstmcell_kernel(
 
             def function(t):
                 first_tile, h = sequence[t]
-                if t >= count - HELD_BACK:
-                    f = first_tile + h
+                if t >= count - LATE_TILES:
+                    q = t - (count - LATE_TILES)
                     nc.scalar.activation(
-                        out=out_gate[h][:], in_=flipped[1][t][:], func=ACT.Sigmoid, bias=shift_col[:, f : f + 1]
+                        out=out_gate[h][:], in_=flipped[1][t][:], func=ACT.Sigmoid, bias=late_shift[:, q : q + 1]
                     )
                     return
+                f = first_tile + h
                 func = ACT.Tanh if first_tile == IN_TRANSFORM else ACT.Sigmoid
-                nc.scalar.activation(out=result[t][:], in_=result[t][:], func=func)
+                nc.scalar.activation(out=result[t][:], in_=result[t][:], func=func, bias=per_feature[:, 3, f : f + 1])
                 if first_tile == IN_TRANSFORM:
                     nc.gpsimd.tensor_tensor(out=fresh[h][:], in0=fresh[h][:], in1=result[t][:], op=ALU.mult)
 
@@ -607,8 +614,6 @@ def tile_layernormlstmcell_kernel(
                 nc.sync.dma_start(out=out_1[bt * P : (bt + 1) * P, cols], in_=cell[bt][:, cols])
 
             def cell_squares(bt, bank):
-                if bank == 0:
-                    pivot(cell_st, bt)
                 squares_about_pivot(cell_st, bt, bank, cell[bt][:, bank_columns(bank)])
 
             last = groups[-1]
@@ -626,9 +631,11 @@ def tile_layernormlstmcell_kernel(
             for t in range(3, LEAD):
                 to_features(0, t)
                 first_product_part(t, on_vector=(t < 6))
-            normalise_group(("gpsimd",) * PAIR, last, IN_TRANSFORM)
+            for group in groups[-2:]:
+                normalise_group(("gpsimd",) * PAIR, group, IN_TRANSFORM)
             for group in groups[-2:]:
                 normalise_group(("gpsimd",) * PAIR, group, FORGET_GATE)
+            normalise_group(("gpsimd",) * PAIR, last, OUT_GATE)
 
             jobs = {}
 
@@ -637,7 +644,6 @@ def tile_layernormlstmcell_kernel(
 
             steps = list(range(count - HELD_BACK)) + [None] * PAUSE + list(range(count - HELD_BACK, count))
             forget_step = sequence.index((FORGET_GATE, 0))
-            at(forget_step + 1, normalise_group, ("gpsimd",) * PAIR, last, OUT_GATE)
             for group in groups:
                 at(forget_step + 1, gain_group, group)
             for h in range(HIDDEN_TILES):
@@ -660,13 +666,13 @@ def tile_layernormlstmcell_kernel(
             made = LEAD
             for step in range(max(len(steps), last_cell_step) + 1):
                 if tile_at(step + 1) is not None:
-                    if tile_at(step + 1) < count - HELD_BACK:
+                    if tile_at(step + 1) < count - LATE_TILES:
                         to_features(1, tile_at(step + 1))
                     else:
                         to_features_sum(tile_at(step + 1))
-                if tile_at(step) is not None and tile_at(step) < count - HELD_BACK:
+                if tile_at(step) is not None and tile_at(step) < count - LATE_TILES:
                     waiting = made - 1 if made - 1 not in first_part else None
-                    if made < count - HELD_BACK and step not in PUT_OFF:
+                    if made < count - LATE_TILES and step not in PUT_OFF:
                         to_features(0, made)
                         made += 1
                     argument(tile_at(step))

from contextlib import ExitStack
import math

import concourse.mybir as mybir
from concourse.masks import make_identity

F32 = mybir.dt.float32
BF16 = mybir.dt.bfloat16
I32 = mybir.dt.int32
U32 = mybir.dt.uint32
U8 = mybir.dt.uint8
FP8X4 = mybir.dt.float8_e4m3fn_x4
FP4X4 = mybir.dt.float4_e2m1fn_x4
ALU = mybir.AluOpType
ACT = mybir.ActivationFunctionType
AXIS = mybir.AxisListType

P = 128
BATCH = 512
K = 1024
HIDDEN = 1024
GATES = 4 * HIDDEN
K_PASS = 4 * P
PASSES = K // K_PASS
BATCH_TILES = BATCH // P
BANK = 512
CHUNKS = GATES // BANK
QUARTERS = 4
QUARTER = GATES // QUARTERS
CHUNKS_PER_QUARTER = CHUNKS // QUARTERS
FEATURE_TILES = GATES // P
HIDDEN_TILES = HIDDEN // P
HIDDEN_BANKS = HIDDEN // BANK
BLOCKS_PER_BANK = BANK // P
IN_GATE = 0 * HIDDEN_TILES
FORGET_GATE = 1 * HIDDEN_TILES
OUT_GATE = 2 * HIDDEN_TILES
IN_TRANSFORM = 3 * HIDDEN_TILES
GATE_ORDER = (IN_GATE, IN_TRANSFORM, FORGET_GATE, OUT_GATE)
FORGET_GATE_BIAS = -1.0
EPS = 1e-5
PAIR = 2
LEAD = 8
HELD_BACK = 4
LATE_TILES = 2
PAUSE = 3
VECTOR_EVERY = 2
VECTOR_UNTIL = 18
PUT_OFF = (3, 6, 9, 12, 15)
PREPARE_AT = 2
LAST_PIECE = 2
QUANTISE_AT = 6
SQUARE_PIECES = ((0, 2), (2, 4), (4, 6), (6, 7), (7, 8))
SQUARES_PIECE = 2 * BANK

FLOPS = 2 * 2 * BATCH * K * GATES


def tile_layernormlstmcell_kernel(
    tc,
    inputs,
    hx,
    cx,
    w_i2h_words,
    w_i2h_scales,
    b_i2h,
    w_h2h_words,
    w_h2h_scales,
    b_h2h,
    ln_i2h_w,
    ln_i2h_b,
    ln_h2h_w,
    ln_h2h_b,
    ln_h2o_w,
    ln_h2o_b,
    out_0,
    out_1,
):
    nc = tc.nc
    acts = (inputs, hx)
    w_words = (w_i2h_words, w_h2h_words)
    w_scales = (w_i2h_scales, w_h2h_scales)
    biases = (b_i2h, b_h2h)
    batch_tiles = range(BATCH_TILES)

    with ExitStack() as ctx:
        ctx.enter_context(tc.manual_schedule())
        keep = ctx.enter_context(tc.tile_pool(name="keep", bufs=1))
        stage = ctx.enter_context(tc.tile_pool(name="stage", bufs=2))
        psum = ctx.enter_context(tc.psum_pool(name="psum", bufs=6))

        half = keep.tile([P, BATCH_TILES], F32, name="half")
        nc.gpsimd.memset(half[:], 0.5)
        identity = keep.tile([P, P], F32, name="identity")
        make_identity(nc, identity[:])
        identity_bf16 = keep.tile([P, P], BF16, name="identity_bf16")
        make_identity(nc, identity_bf16[:])
        minus_one = keep.tile([P, BATCH_TILES], F32, name="minus_one")
        nc.gpsimd.memset(minus_one[:], -1.0)
        unread_sigmoid = keep.tile([P, BATCH_TILES], F32, name="unread_sigmoid")
        nc.scalar.activation(out=unread_sigmoid[:], in_=half[:], func=ACT.Sigmoid)

        first_product = keep.tile([P, BATCH_TILES, GATES], F32, name="first_product")
        pre = [
            [first_product[:, bt, :] for bt in batch_tiles],
            [keep.tile([P, GATES], F32, name="pre1_%d" % bt)[:] for bt in batch_tiles],
        ]
        cx_sb = [keep.tile([P, HIDDEN], BF16, name="cx_sb%d" % bt) for bt in batch_tiles]
        vector_rows = keep.tile([P, P], BF16, name="vector_rows")
        out_rows = keep.tile([P, P], BF16, name="out_rows")
        nc.gpsimd.memset(out_rows[:], 0.0)
        per_feature = keep.tile([P, 4, FEATURE_TILES], F32, name="per_feature")
        late_shift = keep.tile([P, LATE_TILES], F32, name="late_shift")
        out_feature = keep.tile([P, 2, HIDDEN_TILES], F32, name="out_feature")
        late_gain = [keep.tile([P, LATE_TILES * P], BF16, name="late_gain%d" % j) for j in range(2)]

        def columns(name, width):
            return keep.tile([P, width], F32, name=name)

        def new_statistics(name, width, chunks, pieces, length):
            return {
                "name": name,
                "width": width,
                "chunks": chunks,
                "pieces": pieces,
                "length": length,
                "sums": keep.tile([P, width, chunks], F32, name=name + "_sums"),
                "square_sums": keep.tile([P, width, pieces], F32, name=name + "_square_sums"),
                "neg_mean": columns(name + "_neg_mean", width),
                "offset_term": columns(name + "_offset_term", width),
                "neg_centred": columns(name + "_neg_centred", width),
                "centred": columns(name + "_centred", width),
                "root": columns(name + "_root", width),
                "std_eps": columns(name + "_std_eps", width),
                "inv_std": columns(name + "_inv_std", width),
                "neg_mean_over_std": columns(name + "_neg_mean_over_std", width),
            }

        def column(st, key, i):
            return st[key][:, i : i + 1]

        def chunk_length(st):
            return st["length"] // st["chunks"]

        def squares_about_pivot(st, i, c, values):
            unread = stage.tile([P, SQUARES_PIECE], BF16, tag="unread_squares")
            nc.scalar.activation(
                out=unread[:, 0 : values.shape[1]], in_=values, func=ACT.Square,
                scale=-1.0 * chunk_length(st), bias=st["sums"][:, i, 0:1],
                accum_out=st["square_sums"][:, i, c : c + 1],
            )

        def mean_of(st, i):
            unread = stage.tile([P, CHUNKS], F32, tag="unread_columns")
            nc.scalar.activation(
                out=unread[:, 0 : st["chunks"]], in_=st["sums"][:, i, :], func=ACT.Identity, scale=-1.0 / st["length"],
                accum_out=column(st, "neg_mean", i),
            )
            nc.scalar.activation(
                out=column(st, "offset_term", i), in_=st["sums"][:, i, 0:1], func=ACT.Square,
                scale=1.0 / chunk_length(st), bias=column(st, "neg_mean", i),
            )

        def centred_of(st, i):
            unread = stage.tile([P, CHUNKS], F32, tag="unread_columns")
            nc.scalar.activation(
                out=unread[:, 0 : st["pieces"]], in_=st["square_sums"][:, i, :], func=ACT.Identity,
                scale=-1.0 * st["pieces"] / st["length"] / (chunk_length(st) * chunk_length(st)),
                bias=column(st, "offset_term", i), accum_out=column(st, "neg_centred", i),
            )
            nc.scalar.activation(
                out=column(st, "centred", i), in_=column(st, "neg_centred", i), func=ACT.Relu,
                scale=-1.0 * st["length"] / st["pieces"],
            )

        def mean_and_centred_on_vector(st):
            width = st["width"]
            total = columns(st["name"] + "_total", width)
            nc.vector.reduce_sum(out=total[:], in_=st["sums"][:], axis=AXIS.X)
            nc.vector.tensor_scalar_mul(out=st["neg_mean"][:], in0=total[:], scalar1=-1.0 / st["length"])
            offset = columns(st["name"] + "_offset", width)
            nc.vector.scalar_tensor_tensor(
                out=offset[:], in0=st["sums"][:, :, 0], scalar=-1.0 / chunk_length(st), in1=st["neg_mean"][:],
                op0=ALU.mult, op1=ALU.subtract,
            )
            nc.vector.scalar_tensor_tensor(
                out=st["offset_term"][:], in0=offset[:], scalar=-1.0 * st["length"], in1=offset[:], op0=ALU.mult, op1=ALU.mult
            )
            about_pivot = columns(st["name"] + "_about_pivot", width)
            nc.vector.reduce_sum(out=about_pivot[:], in_=st["square_sums"][:], axis=AXIS.X)
            nc.vector.scalar_tensor_tensor(
                out=st["neg_centred"][:], in0=about_pivot[:], scalar=1.0 / (chunk_length(st) * chunk_length(st)),
                in1=st["offset_term"][:], op0=ALU.mult, op1=ALU.add,
            )
            nc.vector.tensor_scalar_max(out=st["centred"][:], in0=st["neg_centred"][:], scalar1=0.0)

        def deviation_of(st):
            width = st["width"]
            nc.gpsimd.tensor_tensor(out=st["root"][:], in0=st["centred"][:], in1=half[:, 0:width], op=ALU.pow)
            nc.gpsimd.tensor_scalar(
                out=st["std_eps"][:], in0=st["root"][:], scalar1=1.0 / math.sqrt(st["length"] - 1), scalar2=EPS,
                op0=ALU.mult, op1=ALU.add,
            )
            nc.gpsimd.tensor_tensor(out=st["inv_std"][:], in0=st["std_eps"][:], in1=minus_one[:, 0:width], op=ALU.pow)

        def root_of(st):
            nc.gpsimd.tensor_tensor(out=st["root"][:], in0=st["centred"][:], in1=half[:, 0 : st["width"]], op=ALU.pow)

        def deviation_from_root(st):
            nc.vector.tensor_scalar(
                out=st["std_eps"][:], in0=st["root"][:], scalar1=1.0 / math.sqrt(st["length"] - 1), scalar2=EPS,
                op0=ALU.mult, op1=ALU.add,
            )
            nc.vector.reciprocal(out=st["inv_std"][:], in_=st["std_eps"][:])

        def normalise(engine, out, in_, st, i):
            neg_mean, inv_std = column(st, "neg_mean", i), column(st, "inv_std", i)
            if engine == "scalar":
                nc.scalar.activation(
                    out=out, in_=in_, func=ACT.Identity, scale=inv_std, bias=column(st, "neg_mean_over_std", i)
                )
            elif engine == "vector":
                nc.vector.tensor_scalar(out=out, in0=in_, scalar1=neg_mean, scalar2=inv_std, op0=ALU.add, op1=ALU.mult)
            else:
                nc.gpsimd.tensor_scalar(out=out, in0=in_, scalar1=neg_mean, scalar2=inv_std, op0=ALU.add, op1=ALU.mult)

        def scalar_shift(st, i):
            nc.scalar.activation(
                out=column(st, "neg_mean_over_std", i), in_=column(st, "neg_mean", i), func=ACT.Identity,
                scale=column(st, "inv_std", i),
            )

        def gate_columns(j, bt, first_tile):
            return pre[j][bt][:, first_tile * P : first_tile * P + HIDDEN]

        groups = [(j, first) for j in range(2) for first in range(0, BATCH_TILES, PAIR)]
        statistics = {group: new_statistics("pre%d_%d" % group, PAIR, CHUNKS, len(SQUARE_PIECES), GATES) for group in groups}

        def normalise_group(engines, group, first_tile, pieces=1):
            j, first = group
            width = HIDDEN // pieces
            for part in range(pieces):
                for i, engine in enumerate(engines):
                    piece = gate_columns(j, first + i, first_tile)[:, part * width : (part + 1) * width]
                    normalise(engine, piece, piece, statistics[group], i)

        def late_columns(j, bt):
            return gate_columns(j, bt, OUT_GATE)[:, HIDDEN - LATE_TILES * P : HIDDEN]

        def gain_group(group):
            j, first = group
            for i in range(PAIR):
                nc.gpsimd.tensor_tensor(
                    out=late_columns(j, first + i), in0=late_columns(j, first + i), in1=late_gain[j][:], op=ALU.mult
                )

        with tc.tile_pool(name="weights", bufs=1) as weights:
            bias_chunks = weights.tile([P, BANK], BF16, name="bias_chunks")
            nc.vector.memset(bias_chunks[:], 0.0)
            planes = [weights.tile([P, PASSES, GATES], U8, name="plane%d" % j, align_bytes=64) for j in range(2)]
            nc.vector.memset(planes[0][:, :, 0:QUARTER].bitcast(I32), 0)
            nc.vector.memset(planes[0][:, :, QUARTER:GATES].bitcast(I32), 0)
            nc.vector.memset(planes[1][:].bitcast(I32), 0)
            words = [
                [weights.tile([P, PASSES, 2 * QUARTER], U8, name="words%d_%d" % (j, c), align_bytes=64) for c in range(QUARTERS)]
                for j in range(2)
            ]
            bias_rep = [
                [weights.tile([P, QUARTER], BF16, name="bias_rep%d_%d" % (j, c)) for c in range(QUARTERS)]
                for j in range(2)
            ]
            codes = {
                group: weights.tile([P, PAIR * PASSES * P], U32, name="codes%d_%d" % group, align_bytes=64) for group in groups
            }
            code_scales = {
                group: weights.tile([P, PAIR * PASSES * P], U8, name="code_scales%d_%d" % group, align_bytes=64)
                for group in groups
            }

            x_tiles = {}

            def load_activation(j, bt):
                x_sb = weights.tile([P, K], BF16, tag="x_sb", bufs=4)
                nc.sync.dma_start(out=x_sb[:], in_=acts[j][bt * P : (bt + 1) * P, :])
                x_tiles[(j, bt)] = x_sb

            def load_scales(j, start, width):
                for r in range(4):
                    nc.sync.dma_start(
                        out=planes[j][r:P:32, :, start : start + width].bitcast(I32),
                        in_=w_scales[j][:, :, start : start + width].bitcast(I32).rearrange("g (q r) n -> r q g n", r=4)[r],
                    )

            def load_words(j, c, start, width):
                first = c * QUARTER + start
                nc.sync.dma_start(
                    out=words[j][c][:, :, 2 * start : 2 * (start + width)].bitcast(I32),
                    in_=w_words[j][:, :, 2 * first : 2 * (first + width)].bitcast(I32).rearrange("g p n -> p g n"),
                )

            def load_repeated_bias(j, c):
                nc.sync.dma_start(
                    out=bias_rep[j][c][:], in_=biases[j][c * QUARTER : (c + 1) * QUARTER].partition_broadcast(P)
                )


            def repeat_bias(c, on_vector):
                repeated = psum.tile([P, BANK], F32, tag="acc")
                nc.tensor.matmul(
                    out=repeated[:], lhsT=identity_bf16[:, c : c + 1].to_broadcast([P, P]), rhs=bias_chunks[:],
                    start=True, stop=True,
                )
                part = c % CHUNKS_PER_QUARTER
                target = bias_rep[0][c // CHUNKS_PER_QUARTER][:, part * BANK : (part + 1) * BANK]
                if on_vector:
                    nc.vector.tensor_copy(out=target, in_=repeated[:])
                else:
                    nc.scalar.copy(out=target, in_=repeated[:])

            def load_rows(rows, vectors, count):
                for i, vector in enumerate(vectors):
                    nc.sync.dma_start(
                        out=rows[i * count : (i + 1) * count, :], in_=vector.rearrange("o (f p) -> (o f) p", p=P)
                    )

            load_activation(0, 0)
            nc.sync.dma_start(out=bias_chunks[0:CHUNKS, :], in_=biases[0].rearrange("(c n) -> c n", n=BANK))
            load_activation(0, 1)
            load_scales(0, 0, QUARTER)
            load_words(0, 0, 0, BANK)
            load_words(0, 0, BANK, BANK)
            load_scales(0, QUARTER, GATES - QUARTER)
            load_words(0, 1, 0, QUARTER)
            load_activation(0, 2)
            load_activation(0, 3)
            load_words(0, 2, 0, QUARTER)
            load_repeated_bias(0, 2)
            load_words(0, 3, 0, QUARTER)
            load_repeated_bias(0, 3)

            def late_loads():
                for bt in range(PAIR):
                    load_activation(1, bt)
                load_scales(1, 0, GATES)
                load_words(1, 0, 0, QUARTER)
                load_repeated_bias(1, 0)

            def last_loads():
                for c in range(1, QUARTERS):
                    load_words(1, c, 0, QUARTER)
                    load_repeated_bias(1, c)
                    if c == 1:
                        for bt in range(PAIR, BATCH_TILES):
                            load_activation(1, bt)
                load_rows(vector_rows, (ln_i2h_w, ln_h2h_w, ln_i2h_b, ln_h2h_b), FEATURE_TILES)
                load_rows(out_rows, (ln_h2o_w, ln_h2o_b), HIDDEN_TILES)
                late_start = OUT_GATE * P + HIDDEN - LATE_TILES * P
                for j, gains in enumerate((ln_i2h_w, ln_h2h_w)):
                    nc.sync.dma_start(
                        out=late_gain[j][:],
                        in_=gains.rearrange("o n -> (o n)")[late_start : late_start + LATE_TILES * P].partition_broadcast(P),
                    )
                for bt in batch_tiles:
                    nc.sync.dma_start(out=cx_sb[bt][:], in_=cx[bt * P : (bt + 1) * P, :])

            grouped_tiles = {}

            def regroup_activation(j, bt):
                x_words = x_tiles[(j, bt)][:].bitcast(F32)
                flipped = psum.tile([P, PASSES * 2, P], F32, tag="flip", bufs=2)
                for g in range(PASSES):
                    for u in range(2):
                        nc.tensor.transpose(
                            flipped[:, 2 * g + u, :],
                            x_words[:, 256 * g + u : 256 * (g + 1) : 2],
                            identity[:],
                        )
                group = (j, bt - bt % PAIR)
                if bt % PAIR == 0:
                    grouped = weights.tile([P, PAIR * K], BF16, tag="grouped", bufs=1, align_bytes=64)
                    grouped_tiles[group] = grouped
                nc.scalar.copy(
                    out=grouped_tiles[group][:, (bt % PAIR) * K : (bt % PAIR + 1) * K]
                    .bitcast(F32)
                    .rearrange("p (g b u) -> p g b u", g=PASSES, u=2),
                    in_=flipped[:].rearrange("p (g u) b -> p g b u", u=2),
                )

            def quantise_activation(group, first_tile, tiles):
                words = slice(first_tile * PASSES * P, (first_tile + tiles) * PASSES * P)
                nc.vector.quantize_mx(
                    out=codes[group][:, words].bitcast(FP8X4), scales=code_scales[group][:, words],
                    in_=grouped_tiles[group][:, first_tile * K : (first_tile + tiles) * K],
                )

            def wait_for_quantise(group):
                nc.gpsimd.memset(grouped_tiles[group][:, 0:16], 0.0)

            def chunk_columns(c):
                return slice(c * BANK, (c + 1) * BANK)

            def code_columns(bt, g):
                start = ((bt % PAIR) * PASSES + g) * P
                return slice(start, start + P)

            def chunk_product(j, bt, c):
                quarter = c // CHUNKS_PER_QUARTER
                part = c % CHUNKS_PER_QUARTER
                acc = psum.tile([P, BANK], F32, tag="acc")
                for g in range(PASSES):
                    nc.tensor.matmul_mx(
                        out=acc[:],
                        lhsT=codes[(j, bt - bt % PAIR)][:, code_columns(bt, g)].bitcast(FP8X4),
                        lhsT_scale=code_scales[(j, bt - bt % PAIR)][:, code_columns(bt, g)],
                        rhs=words[j][quarter][:, g, 2 * BANK * part : 2 * BANK * (part + 1)].bitcast(FP4X4),
                        rhs_scale=planes[j][:, g, BANK * c : BANK * (c + 1)],
                        start=(g == 0),
                        stop=(g == PASSES - 1),
                    )
                nc.vector.scalar_tensor_tensor(
                    out=pre[j][bt][:, chunk_columns(c)],
                    in0=acc[:],
                    scalar=1.0,
                    in1=bias_rep[j][quarter][:, part * BANK : (part + 1) * BANK],
                    op0=ALU.mult,
                    op1=ALU.add,
                    accum_out=statistics[(j, bt - bt % PAIR)]["sums"][:, bt % PAIR, c : c + 1],
                )

            def piece_squares(j, bt, piece):
                first_chunk, end_chunk = SQUARE_PIECES[piece]
                squares_about_pivot(
                    statistics[(j, bt - bt % PAIR)], bt % PAIR, piece, pre[j][bt][:, first_chunk * BANK : end_chunk * BANK]
                )

            def feature_vectors():
                vector_cols = psum.tile([P, P], BF16, tag="flip", bufs=2)
                nc.tensor.transpose(vector_cols[:], vector_rows[:], identity_bf16[:])
                nc.scalar.copy(out=per_feature[:].rearrange("p i f -> p (i f)"), in_=vector_cols[:])
                forget_tiles = slice(FORGET_GATE, FORGET_GATE + HIDDEN_TILES)
                nc.scalar.activation(
                    out=per_feature[:, 3, forget_tiles], in_=per_feature[:, 3, forget_tiles], func=ACT.Identity,
                    bias=minus_one[:, 0:1],
                )
                for q in range(LATE_TILES):
                    f = OUT_GATE + HIDDEN_TILES - LATE_TILES + q
                    nc.scalar.activation(
                        out=late_shift[:, q : q + 1], in_=per_feature[:, 2, f : f + 1], func=ACT.Identity,
                        bias=per_feature[:, 3, f : f + 1],
                    )
                out_cols = psum.tile([P, P], BF16, tag="flip", bufs=2)
                nc.tensor.transpose(out_cols[:], out_rows[:], identity_bf16[:])
                nc.scalar.copy(out=out_feature[:].rearrange("p i f -> p (i f)"), in_=out_cols[:, 0 : 2 * HIDDEN_TILES])

            regroup_activation(0, 0)
            repeat_bias(0, on_vector=True)
            quantise_activation(groups[0], 0, 1)
            regroup_activation(0, 1)
            repeat_bias(1, on_vector=True)
            quantise_activation(groups[0], 1, 1)
            repeat_bias(2, on_vector=False)
            repeat_bias(3, on_vector=False)
            for number, group in enumerate(groups):
                j, first = group
                st = statistics[group]
                for c in range(CHUNKS):
                    for i in range(PAIR):
                        chunk_product(j, first + i, c)
                        for piece, (first_chunk, end_chunk) in enumerate(SQUARE_PIECES):
                            if end_chunk == c + 1:
                                piece_squares(j, first + i, piece)
                    if number == 0 and c == 0:
                        late_loads()
                    if number == 0 and c == PREPARE_AT + PAIR:
                        last_loads()
                    prepare_at = PREPARE_AT + (1 if number + 2 == len(groups) else 0)
                    if number + 1 < len(groups) and prepare_at <= c < prepare_at + PAIR:
                        regroup_activation(groups[number + 1][0], groups[number + 1][1] + c - prepare_at)
                    if number + 1 < len(groups) and c == QUANTISE_AT:
                        quantise_activation(groups[number + 1], 0, PAIR)
                        if number >= 1:
                            wait_for_quantise(groups[number + 1])
                            for first_tile in GATE_ORDER[2:]:
                                normalise_group(("gpsimd",) * PAIR, groups[number - 1], first_tile)
                    if number + 1 == len(groups) and c == CHUNKS // 2:
                        feature_vectors()
                    if c == CHUNKS - 1 and number + 1 < len(groups):
                        for i in range(PAIR):
                            mean_of(st, i)
                            centred_of(st, i)
                        if number + 1 < len(groups):
                            deviation_of(st)
                            for first_tile in GATE_ORDER[: (2 if number + 2 < len(groups) else 1)]:
                                normalise_group(("gpsimd",) * PAIR, group, first_tile)


        with tc.tile_pool(name="gates", bufs=1) as gate_pool:
            gain_col = (per_feature[:, 0, :], per_feature[:, 1, :])

            def gate_tiles(name):
                return [gate_pool.tile([P, BATCH_TILES, P], F32, name="%s%d" % (name, h)) for h in range(HIDDEN_TILES)]

            forget = gate_tiles("forget")
            fresh = gate_tiles("fresh")
            out_gate = gate_tiles("out_gate")

            sequence = [(first_tile, h) for first_tile in GATE_ORDER for h in range(HIDDEN_TILES)]
            count = len(sequence)
            flipped = ({}, {})
            first_part = {}
            result = {}

            def to_features(j, t):
                f = sequence[t][0] + sequence[t][1]
                bank = psum.tile([P, BATCH_TILES, P], F32, tag="acc")
                for bt in batch_tiles:
                    nc.tensor.transpose(bank[:, bt, :], pre[j][bt][:, f * P : (f + 1) * P], identity[:])
                flipped[j][t] = bank

            def to_features_sum(t):
                f = sequence[t][0] + sequence[t][1]
                bank = psum.tile([P, BATCH_TILES, P], F32, tag="acc")
                for bt in batch_tiles:
                    for j in range(2):
                        nc.tensor.matmul(
                            out=bank[:, bt, :], lhsT=pre[j][bt][:, f * P : (f + 1) * P], rhs=identity[:],
                            is_transpose=True, start=(j == 0), stop=(j == 1),
                        )
                flipped[1][t] = bank

            def first_product_part(t, on_vector):
                f = sequence[t][0] + sequence[t][1]
                part = first_product[:, :, f * P : (f + 1) * P]
                if on_vector:
                    nc.vector.tensor_scalar(
                        out=part, in0=flipped[0][t][:], scalar1=gain_col[0][:, f : f + 1],
                        scalar2=per_feature[:, 2, f : f + 1], op0=ALU.mult, op1=ALU.add,
                    )
                else:
                    nc.scalar.activation(
                        out=part, in_=flipped[0][t][:], func=ACT.Identity,
                        scale=gain_col[0][:, f : f + 1], bias=per_feature[:, 2, f : f + 1],
                    )
                first_part[t] = part

            def argument(t):
                first_tile, h = sequence[t]
                f = first_tile + h
                if first_tile == IN_GATE:
                    result[t] = fresh[h]
                elif first_tile == FORGET_GATE:
                    result[t] = forget[h]
                elif first_tile == OUT_GATE:
                    result[t] = out_gate[h]
                else:
                    squashed = gate_pool.tile([P, BATCH_TILES, P], F32, tag="squashed", bufs=8)
                    result[t] = squashed
                nc.vector.scalar_tensor_tensor(
                    out=result[t][:], in0=flipped[1][t][:], scalar=gain_col[1][:, f : f + 1], in1=first_part[t],
                    op0=ALU.mult, op1=ALU.add,
                )

            def function(t):
                first_tile, h = sequence[t]
                if t >= count - LATE_TILES:
                    q = t - (count - LATE_TILES)
                    nc.scalar.activation(
                        out=out_gate[h][:], in_=flipped[1][t][:], func=ACT.Sigmoid, bias=late_shift[:, q : q + 1]
                    )
                    return
                f = first_tile + h
                func = ACT.Tanh if first_tile == IN_TRANSFORM else ACT.Sigmoid
                nc.scalar.activation(out=result[t][:], in_=result[t][:], func=func, bias=per_feature[:, 3, f : f + 1])
                if first_tile == IN_TRANSFORM:
                    nc.gpsimd.tensor_tensor(out=fresh[h][:], in0=fresh[h][:], in1=result[t][:], op=ALU.mult)

            cx_features = {}

            def flip_cx(h):
                bank = psum.tile([P, BATCH_TILES, P], BF16, tag="flip", bufs=2)
                for bt in batch_tiles:
                    nc.tensor.transpose(bank[:, bt, :], cx_sb[bt][:, h * P : (h + 1) * P], identity_bf16[:])
                cx_features[h] = bank

            def kept_part(h):
                nc.vector.tensor_mul(out=forget[h][:], in0=forget[h][:], in1=cx_features[h][:])

            cell = [pre[0][bt][:, 0:HIDDEN] for bt in batch_tiles]
            cell_normal = [pre[0][bt][:, HIDDEN : 2 * HIDDEN] for bt in batch_tiles]
            hidden = [pre[1][bt][:, 0:HIDDEN] for bt in batch_tiles]
            cell_st = new_statistics("cell", BATCH_TILES, HIDDEN_BANKS, HIDDEN_BANKS, HIDDEN)
            rows_bank = {}

            def bank_columns(bank):
                return slice(bank * BANK, (bank + 1) * BANK)

            def cell_to_rows(bt, bank):
                back = psum.tile([P, BANK], F32, tag="acc")
                for q in range(BLOCKS_PER_BANK):
                    h = bank * BLOCKS_PER_BANK + q
                    for i, tiles in enumerate((forget, fresh)):
                        nc.tensor.matmul(
                            out=back[:, q * P : (q + 1) * P], lhsT=tiles[h][:, bt, :], rhs=identity[:],
                            is_transpose=True, start=(i == 0), stop=(i == 1),
                        )
                rows_bank[(bt, bank)] = back

            def cell_out(bt, bank):
                cols = bank_columns(bank)
                nc.vector.tensor_scalar(
                    out=cell[bt][:, cols], in0=rows_bank[(bt, bank)][:], scalar1=1.0, scalar2=0.0,
                    op0=ALU.mult, op1=ALU.add, accum_out=cell_st["sums"][:, bt, bank : bank + 1],
                )
                nc.sync.dma_start(out=out_1[bt * P : (bt + 1) * P, cols], in_=cell[bt][:, cols])

            def cell_squares(bt, bank):
                squares_about_pivot(cell_st, bt, bank, cell[bt][:, bank_columns(bank)])

            last = groups[-1]
            normalise_group(("vector",) * PAIR, groups[-2], OUT_GATE)
            for t in range(3):
                to_features(0, t)
            mean_and_centred_on_vector(statistics[last])
            root_of(statistics[last])
            first_product_part(0, on_vector=True)
            first_product_part(1, on_vector=False)
            first_product_part(2, on_vector=False)
            deviation_from_root(statistics[last])
            scalar_shift(statistics[last], 1)
            normalise_group(("gpsimd", "scalar"), last, IN_GATE, pieces=2)
            for t in range(3, LEAD):
                to_features(0, t)
                first_product_part(t, on_vector=(t < 6))
            for group in groups[-2:]:
                normalise_group(("gpsimd",) * PAIR, group, IN_TRANSFORM)
            for group in groups[-2:]:
                normalise_group(("gpsimd",) * PAIR, group, FORGET_GATE)
            normalise_group(("gpsimd",) * PAIR, last, OUT_GATE)

            jobs = {}

            def at(step, job, *args):
                jobs.setdefault(step, []).append((job, args))

            steps = list(range(count - HELD_BACK)) + [None] * PAUSE + list(range(count - HELD_BACK, count))
            forget_step = sequence.index((FORGET_GATE, 0))
            for group in groups:
                at(forget_step + 1, gain_group, group)
            for h in range(HIDDEN_TILES):
                at(forget_step + h, flip_cx, h)
                at(forget_step + h + 2, kept_part, h)
            for bank in range(HIDDEN_BANKS):
                start = forget_step + (bank + 1) * BLOCKS_PER_BANK + 2
                for bt in batch_tiles:
                    at(start + bt, cell_to_rows, bt, bank)
                    at(start + bt + 1, cell_out, bt, bank)
                    at(start + bt + 2, cell_squares, bt, bank)
            last_cell_step = start + BATCH_TILES + 1
            at(last_cell_step, mean_and_centred_on_vector, cell_st)
            at(last_cell_step, root_of, cell_st)

            def tile_at(step):
                return steps[step] if 0 <= step < len(steps) else None

            to_features(1, 0)
            made = LEAD
            for step in range(max(len(steps), last_cell_step) + 1):
                if tile_at(step + 1) is not None:
                    if tile_at(step + 1) < count - LATE_TILES:
                        to_features(1, tile_at(step + 1))
                    else:
                        to_features_sum(tile_at(step + 1))
                if tile_at(step) is not None and tile_at(step) < count - LATE_TILES:
                    waiting = made - 1 if made - 1 not in first_part else None
                    if made < count - LATE_TILES and step not in PUT_OFF:
                        to_features(0, made)
                        made += 1
                    argument(tile_at(step))
                    if waiting is not None:
                        first_product_part(waiting, on_vector=(waiting % VECTOR_EVERY == 0 and waiting < VECTOR_UNTIL))
                if tile_at(step - 1) is not None:
                    function(tile_at(step - 1))
                for job, args in jobs.get(step, ()):
                    job(*args)

            deviation_from_root(cell_st)
            for bank in range(HIDDEN_BANKS):
                cols = bank_columns(bank)
                for bt in batch_tiles:
                    normalise("vector", cell_normal[bt][:, cols], cell[bt][:, cols], cell_st, bt)

            def squash(h):
                bank = psum.tile([P, BATCH_TILES, P], F32, tag="acc")
                for bt in batch_tiles:
                    nc.tensor.transpose(bank[:, bt, :], cell_normal[bt][:, h * P : (h + 1) * P], identity[:])
                squashed = gate_pool.tile([P, BATCH_TILES, P], F32, tag="squashed", bufs=8)
                nc.scalar.activation(
                    out=squashed[:], in_=bank[:], func=ACT.Tanh,
                    scale=out_feature[:, 0, h : h + 1], bias=out_feature[:, 1, h : h + 1],
                )
                nc.vector.tensor_mul(out=out_gate[h][:], in0=out_gate[h][:], in1=squashed[:])

            def hidden_out(bt, first, tiles, on_vector):
                back = psum.tile([P, BANK], F32, tag="acc")
                for q in range(tiles):
                    nc.tensor.transpose(back[:, q * P : (q + 1) * P], out_gate[first + q][:, bt, :], identity[:])
                cols = slice(first * P, (first + tiles) * P)
                if on_vector:
                    nc.vector.tensor_copy(out=hidden[bt][:, cols], in_=back[:, 0 : tiles * P])
                else:
                    nc.scalar.copy(out=hidden[bt][:, cols], in_=back[:, 0 : tiles * P])
                nc.sync.dma_start(out=out_0[bt * P : (bt + 1) * P, cols], in_=hidden[bt][:, cols])

            for h in range(HIDDEN_TILES):
                squash(h)
                if h >= BLOCKS_PER_BANK + 1:
                    hidden_out(h - BLOCKS_PER_BANK - 1, 0, BLOCKS_PER_BANK, on_vector=False)
            hidden_out(BATCH_TILES - 1, 0, BLOCKS_PER_BANK, on_vector=False)
            for bt in batch_tiles:
                hidden_out(bt, BLOCKS_PER_BANK, LAST_PIECE, on_vector=False)
            for bt in batch_tiles:
                hidden_out(bt, BLOCKS_PER_BANK + LAST_PIECE, LAST_PIECE, on_vector=(bt + 1 < BATCH_TILES))
